import numpy as np
import ml_dtypes


def mxq(x, axis, fmt="e4m3"):
    dtype, down = {"e4m3": (ml_dtypes.float8_e4m3fn, 7), "e5m2": (ml_dtypes.float8_e5m2, 14)}[fmt]
    v = np.moveaxis(np.asarray(x, np.float32).astype(ml_dtypes.bfloat16).astype(np.float64), axis, -1)
    blocks = v.reshape(v.shape[:-1] + (-1, 32))
    amax = np.abs(blocks).max(-1, keepdims=True)
    byte = np.maximum(np.where(amax > 0, np.frexp(amax)[1] - 1 + 127, 0) - down, 1)
    scale = np.exp2(byte - 127.0)
    codes = (blocks / scale).astype(np.float32).astype(dtype).astype(np.float64)
    return np.moveaxis((codes * scale).reshape(v.shape), -1, axis)


WIDE = False


def mx_kscale(k):
    if not WIDE:
        return np.ones(k)
    levels = np.array([20, -20, 10, -10, 0])
    a = np.random.permutation(np.resize(levels, k // 512 * 4)).reshape(k // 512, 4)
    idx = np.arange(k)
    return np.exp2(a[idx // 512, idx % 128 // 32])


BF16 = ml_dtypes.bfloat16


def bf(x):
    return np.asarray(x, np.float32).astype(BF16)


def f64(x):
    return np.asarray(x).astype(np.float64)


B, NH, NW, C, K, P = 8, 8, 8, 256, 512, 4
T = P * P
N = B * NH * NW
HAD = np.array([[1.0, 1.0, 1.0, 1.0],
                [1.0, -1.0, 1.0, -1.0],
                [1.0, 1.0, -1.0, -1.0],
                [1.0, -1.0, -1.0, 1.0]])


def setup_inputs():
    s = mx_kscale(N).reshape(B, NH, NW)
    trans = np.random.standard_normal((T, B, NH, NW, C)) * s[None, :, :, :, None]
    weight = np.random.standard_normal((T, C, K)) * 0.5 * P / np.sqrt(C)
    bias = np.random.standard_normal((1, 1, 1, K)) * 0.2
    g = np.random.standard_normal((B, P * NH, P * NW, K))
    e = np.exp2(np.random.randint(-12, 1, (B, NH, NW))) / s
    e = np.repeat(np.repeat(e, P, axis=1), P, axis=2)[:, :, :, None]
    return {"trans": bf(trans), "weight": bf(weight), "bias": bf(bias), "grad_out": bf(g * e)}


def reference(trans, weight, bias, grad_out):
    x = f64(trans).reshape(T, N, C)
    g = f64(grad_out).reshape(B, NH, P, NW, P, K).transpose(2, 4, 0, 1, 3, 5)
    r = np.stack([sum(HAD[p, u] * g[p] for p in range(P)) for u in range(P)])
    gy = np.stack([sum(HAD[q, v] * r[:, q] for q in range(P)) for v in range(P)], axis=1) / T
    gy = gy.reshape(T, N, K)
    return mxq(x, 1, "e4m3").transpose(0, 2, 1) @ mxq(gy, 1, "e5m2")

@@ -1,0 +1,121 @@
+import concourse.mybir as mybir
+
+F32 = mybir.dt.float32
+BF16 = mybir.dt.bfloat16
+U32 = mybir.dt.uint32
+U8 = mybir.dt.uint8
+E4M3_X4 = mybir.dt.float8_e4m3fn_x4
+E5M2_X4 = mybir.dt.float8_e5m2_x4
+COPY = mybir.ActivationFunctionType.Copy
+SIGN_OP = (mybir.AluOpType.add, mybir.AluOpType.subtract)
+
+PARTS = 128
+PACK = 4
+SIDE = 4
+T = SIDE * SIDE
+N = 512
+C = 256
+K = 512
+ROW = PACK * SIDE * K
+G_CHUNKS = 8
+CHUNK = ROW // G_CHUNKS
+C_HALVES = C // PARTS
+
+FLOPS = 2 * T * N * C * K
+BYTES = 2 * T * N * C + 2 * T * N * K + 4 * T * C * K
+
+
+def tile_iwht3layer_pa_kernel(tc, trans, weight, bias, grad_out, out):
+    nc = tc.nc
+
+    g_dram = grad_out.rearrange("b (i p) (jh x) k -> jh (b i) p (x k)", p=SIDE, jh=2)
+    x_dram = trans.rearrange("t b i (jh r) c -> t (b i jh) (r c)", r=PACK)
+    out_dram = out.rearrange("t (h m) k -> t m h k", h=C_HALVES)
+
+    with tc.tile_pool(name="tree", bufs=1) as tree, tc.tile_pool(name="flow", bufs=2) as flow, tc.tile_pool(
+        name="xin", bufs=4
+    ) as xin, tc.psum_pool(name="psum", bufs=4) as psum:
+        g_chunks = []
+        for c in range(G_CHUNKS):
+            g_tile = tree.tile([PARTS, SIDE, CHUNK], BF16, name="g%d" % c)
+            for jh in range(2):
+                nc.sync.dma_start(
+                    out=g_tile[jh:PARTS:2, :, :], in_=g_dram[jh, :, :, c * CHUNK : (c + 1) * CHUNK]
+                )
+            g_chunks.append(g_tile)
+
+        level1 = tree.tile([PARTS, 2, ROW], F32, name="level1")
+        level2 = tree.tile([PARTS, PACK, 2, 2 * K], F32, name="level2")
+        level3 = tree.tile([PARTS, PACK, 2, K], F32, name="level3")
+
+        for u0 in range(2):
+            for c in range(G_CHUNKS):
+                pairs = g_chunks[c][:].rearrange("n (p1 p0) w -> n p1 p0 w", p0=2)
+                nc.vector.tensor_tensor(
+                    out=level1[:, :, c * CHUNK : (c + 1) * CHUNK],
+                    in0=pairs[:, :, 0, :],
+                    in1=pairs[:, :, 1, :],
+                    op=SIGN_OP[u0],
+                )
+            for u1 in range(2):
+                nc.vector.tensor_tensor(
+                    out=level2[:].rearrange("n r q w -> n (r q w)"),
+                    in0=level1[:, 0, :],
+                    in1=level1[:, 1, :],
+                    op=SIGN_OP[u1],
+                )
+                for v1 in range(2):
+                    nc.vector.tensor_tensor(
+                        out=level3[:].rearrange("n r q k -> n r (q k)"),
+                        in0=level2[:, :, 0, :],
+                        in1=level2[:, :, 1, :],
+                        op=SIGN_OP[v1],
+                    )
+                    for v0 in range(2):
+                        t = SIDE * (2 * u1 + u0) + 2 * v1 + v0
+
+                        sums = flow.tile([PARTS, PACK, K], BF16, name="sums")
+                        nc.vector.tensor_tensor(
+                            out=sums[:], in0=level3[:, :, 0, :], in1=level3[:, :, 1, :], op=SIGN_OP[v0]
+                        )
+                        gy = flow.tile([PARTS, K, PACK], BF16, name="gy", align_bytes=64)
+                        nc.scalar.activation(
+                            out=gy[:], in_=sums[:].rearrange("n r k -> n k r"), func=COPY, scale=1.0 / T
+                        )
+                        gy_codes = flow.tile([PARTS, K], U32, name="gy_codes", align_bytes=64)
+                        gy_scales = flow.tile([PARTS, K], U8, name="gy_scales", align_bytes=64)
+                        nc.vector.quantize_mx(
+                            out=gy_codes[:].bitcast(E5M2_X4),
+                            scales=gy_scales[:],
+                            in_=gy[:].rearrange("n k r -> n (k r)"),
+                        )
+
+                        x_raw = xin.tile([PARTS, PACK, C], BF16, name="x_raw")
+                        nc.sync.dma_start(
+                            out=x_raw[:].rearrange("n r c -> n (r c)"), in_=x_dram[t]
+                        )
+                        x = flow.tile([PARTS, C, PACK], BF16, name="x", align_bytes=64)
+                        nc.scalar.copy(out=x[:], in_=x_raw[:].rearrange("n r c -> n c r"))
+                        x_codes = flow.tile([PARTS, C], U32, name="x_codes", align_bytes=64)
+                        x_scales = flow.tile([PARTS, C], U8, name="x_scales", align_bytes=64)
+                        nc.vector.quantize_mx(
+                            out=x_codes[:].bitcast(E4M3_X4),
+                            scales=x_scales[:],
+                            in_=x[:].rearrange("n c r -> n (c r)"),
+                        )
+
+                        result = flow.tile([PARTS, C_HALVES, K], F32, name="result")
+                        for h in range(C_HALVES):
+                            cols = slice(h * PARTS, (h + 1) * PARTS)
+                            acc = psum.tile([PARTS, K], F32, name="acc")
+                            nc.tensor.matmul_mx(
+                                out=acc[:],
+                                lhsT=x_codes[:, cols].bitcast(E4M3_X4),
+                                lhsT_scale=x_scales[:, cols],
+                                rhs=gy_codes[:].bitcast(E5M2_X4),
+                                rhs_scale=gy_scales[:],
+                                start=True,
+                                stop=True,
+                            )
+                            nc.scalar.copy(out=result[:, h, :], in_=acc[:])
+                        nc.scalar.dma_start(out=out_dram[t], in_=result[:])

@@ -1,4 +1,5 @@
 import concourse.mybir as mybir
+from concourse.masks import make_identity
 
 F32 = mybir.dt.float32
 BF16 = mybir.dt.bfloat16
@@ -16,71 +17,135 @@ T = SIDE * SIDE
 N = 512
 C = 256
 K = 512
-ROW = PACK * SIDE * K
-G_CHUNKS = 8
-CHUNK = ROW // G_CHUNKS
 C_HALVES = C // PARTS
+
+OCTET = PARTS // T
+GROUP = 4
+GROUPS_PER_R = 3
+OCTETS = GROUP * GROUPS_PER_R
+K_TENSOR = OCTETS * OCTET
+K_VECTOR = K - K_TENSOR
 
 FLOPS = 2 * T * N * C * K
 BYTES = 2 * T * N * C + 2 * T * N * K + 4 * T * C * K
 
 
+def transform_matrix(nc, pool, ident):
+    current = pool.tile([PARTS, PARTS], BF16, name="matrix0")
+    nc.vector.tensor_scalar_mul(out=current[:], in0=ident[:], scalar1=1.0 / T)
+    for level in range(4):
+        step = PARTS // 2 ** (level + 1)
+        following = pool.tile([PARTS, PARTS], BF16, name="matrix%d" % (level + 1))
+        halves = current[:].rearrange("n (a two b) -> n a two b", two=2, b=step)
+        signed = following[:].rearrange("n (a two b) -> n a two b", two=2, b=step)
+        for bit in range(2):
+            nc.vector.tensor_tensor(
+                out=signed[:, :, bit, :], in0=halves[:, :, 0, :], in1=halves[:, :, 1, :], op=SIGN_OP[bit]
+            )
+        current = following
+    return current
+
+
 def tile_iwht3layer_pa_kernel(tc, trans, weight, bias, grad_out, out):
     nc = tc.nc
 
-    g_dram = grad_out.rearrange("b (i p) (jh x) k -> jh (b i) p (x k)", p=SIDE, jh=2)
+    g_dram = grad_out.rearrange("b (i p) (jh r q) k -> jh (b i) p r q k", p=SIDE, jh=2, r=PACK)
     x_dram = trans.rearrange("t b i (jh r) c -> t (b i jh) (r c)", r=PACK)
     out_dram = out.rearrange("t (h m) k -> t m h k", h=C_HALVES)
 
-    with tc.tile_pool(name="tree", bufs=1) as tree, tc.tile_pool(name="flow", bufs=2) as flow, tc.tile_pool(
-        name="xin", bufs=4
-    ) as xin, tc.psum_pool(name="psum", bufs=4) as psum:
-        g_chunks = []
-        for c in range(G_CHUNKS):
-            g_tile = tree.tile([PARTS, SIDE, CHUNK], BF16, name="g%d" % c)
-            for jh in range(2):
-                nc.sync.dma_start(
-                    out=g_tile[jh:PARTS:2, :, :], in_=g_dram[jh, :, :, c * CHUNK : (c + 1) * CHUNK]
-                )
-            g_chunks.append(g_tile)
+    with tc.tile_pool(name="keep", bufs=1) as keep, tc.tile_pool(name="flow", bufs=2) as flow, tc.tile_pool(
+        name="leaf", bufs=3
+    ) as leaf, tc.tile_pool(name="xin", bufs=4) as xin, tc.psum_pool(name="turn", bufs=1) as turn, tc.psum_pool(
+        name="psum", bufs=4
+    ) as psum:
+        ident = keep.tile([PARTS, PARTS], BF16, name="ident")
+        make_identity(nc, ident[:])
+        matrix = transform_matrix(nc, keep, ident)
 
-        level1 = tree.tile([PARTS, 2, ROW], F32, name="level1")
-        level2 = tree.tile([PARTS, PACK, 2, 2 * K], F32, name="level2")
-        level3 = tree.tile([PARTS, PACK, 2, K], F32, name="level3")
+        g_tiles = []
+        for r in range(PACK):
+            g_tile = keep.tile([PARTS, SIDE, SIDE, K], BF16, name="g%d" % r)
+            for q in range(0, SIDE, 2):
+                for jh in range(2):
+                    nc.sync.dma_start(
+                        out=g_tile[jh:PARTS:2, :, q : q + 2, :], in_=g_dram[jh, :, :, r, q : q + 2, :]
+                    )
+            g_tiles.append(g_tile)
+
+        gy_tensor = keep.tile([PARTS, PACK, OCTETS, PARTS], BF16, name="gy_tensor")
+        for r in range(PACK):
+            picked = flow.tile([PARTS, OCTETS, T, OCTET], BF16, name="picked")
+            nc.scalar.copy(
+                out=picked[:],
+                in_=g_tiles[r][:, :, :, 0:K_TENSOR].rearrange("n p q (o e) -> n o (p q) e", e=OCTET),
+            )
+            for first in range(0, OCTETS, GROUP):
+                pixels_psum = turn.tile([PARTS, GROUP, PARTS], BF16, name="pixels_psum")
+                for j in range(GROUP):
+                    nc.tensor.transpose(
+                        out=pixels_psum[:, j, :],
+                        in_=picked[:, first + j, :, :].rearrange("n a e -> n (a e)"),
+                        identity=ident[:],
+                    )
+                pixels = flow.tile([PARTS, GROUP, PARTS], BF16, name="pixels")
+                nc.scalar.copy(out=pixels[:], in_=pixels_psum[:])
+                coeffs_psum = turn.tile([PARTS, GROUP, PARTS], F32, name="coeffs_psum")
+                nc.tensor.matmul(
+                    out=coeffs_psum[:].rearrange("n j m -> n (j m)"),
+                    lhsT=matrix[:],
+                    rhs=pixels[:].rearrange("n j m -> n (j m)"),
+                    start=True,
+                    stop=True,
+                )
+                coeffs = flow.tile([PARTS, GROUP, PARTS], BF16, name="coeffs")
+                nc.scalar.copy(out=coeffs[:], in_=coeffs_psum[:])
+                back_psum = turn.tile([PARTS, GROUP, PARTS], BF16, name="back_psum")
+                for j in range(GROUP):
+                    nc.tensor.transpose(out=back_psum[:, j, :], in_=coeffs[:, j, :], identity=ident[:])
+                nc.scalar.copy(out=gy_tensor[:, r, first : first + GROUP, :], in_=back_psum[:])
+        gy_tensor_by_t = gy_tensor[:].rearrange("n r o (t e) -> n t o e r", e=OCTET)
+
+        level1 = keep.tile([PARTS, 2, PACK, SIDE, K_VECTOR], F32, name="level1")
+        level2 = keep.tile([PARTS, PACK, SIDE, K_VECTOR], F32, name="level2")
+        level3 = keep.tile([PARTS, PACK, 2, K_VECTOR], F32, name="level3")
+        level2_halves = level2[:].rearrange("n r (q1 q0) k -> n r q1 q0 k", q0=2)
 
         for u0 in range(2):
-            for c in range(G_CHUNKS):
-                pairs = g_chunks[c][:].rearrange("n (p1 p0) w -> n p1 p0 w", p0=2)
-                nc.vector.tensor_tensor(
-                    out=level1[:, :, c * CHUNK : (c + 1) * CHUNK],
-                    in0=pairs[:, :, 0, :],
-                    in1=pairs[:, :, 1, :],
-                    op=SIGN_OP[u0],
-                )
+            for r in range(PACK):
+                pairs = g_tiles[r][:].rearrange("n (p1 p0) q k -> n p1 p0 q k", p0=2)
+                for q in range(0, SIDE, 2):
+                    nc.vector.tensor_tensor(
+                        out=level1[:, :, r, q : q + 2, :],
+                        in0=pairs[:, :, 0, q : q + 2, K_TENSOR:K],
+                        in1=pairs[:, :, 1, q : q + 2, K_TENSOR:K],
+                        op=SIGN_OP[u0],
+                    )
             for u1 in range(2):
-                nc.vector.tensor_tensor(
-                    out=level2[:].rearrange("n r q w -> n (r q w)"),
-                    in0=level1[:, 0, :],
-                    in1=level1[:, 1, :],
-                    op=SIGN_OP[u1],
-                )
+                for r in range(PACK):
+                    nc.vector.tensor_tensor(
+                        out=level2[:, r], in0=level1[:, 0, r], in1=level1[:, 1, r], op=SIGN_OP[u1]
+                    )
                 for v1 in range(2):
                     nc.vector.tensor_tensor(
-                        out=level3[:].rearrange("n r q k -> n r (q k)"),
-                        in0=level2[:, :, 0, :],
-                        in1=level2[:, :, 1, :],
-                        op=SIGN_OP[v1],
+                        out=level3[:], in0=level2_halves[:, :, 0], in1=level2_halves[:, :, 1], op=SIGN_OP[v1]
                     )
                     for v0 in range(2):
                         t = SIDE * (2 * u1 + u0) + 2 * v1 + v0
 
-                        sums = flow.tile([PARTS, PACK, K], BF16, name="sums")
+                        sums = leaf.tile([PARTS, PACK, K_VECTOR], BF16, name="sums")
                         nc.vector.tensor_tensor(
                             out=sums[:], in0=level3[:, :, 0, :], in1=level3[:, :, 1, :], op=SIGN_OP[v0]
                         )
                         gy = flow.tile([PARTS, K, PACK], BF16, name="gy", align_bytes=64)
+                        nc.scalar.copy(
+                            out=gy[:, 0:K_TENSOR, :].rearrange("n (o e) r -> n o e r", e=OCTET),
+                            in_=gy_tensor_by_t[:, t],
+                        )
                         nc.scalar.activation(
-                            out=gy[:], in_=sums[:].rearrange("n r k -> n k r"), func=COPY, scale=1.0 / T
+                            out=gy[:, K_TENSOR:K, :],
+                            in_=sums[:].rearrange("n r k -> n k r"),
+                            func=COPY,
+                            scale=1.0 / T,
                         )
                         gy_codes = flow.tile([PARTS, K], U32, name="gy_codes", align_bytes=64)
                         gy_scales = flow.tile([PARTS, K], U8, name="gy_scales", align_bytes=64)
@@ -91,9 +156,7 @@ def tile_iwht3layer_pa_kernel(tc, trans, weight, bias, grad_out, out):
                         )
 
                         x_raw = xin.tile([PARTS, PACK, C], BF16, name="x_raw")
-                        nc.sync.dma_start(
-                            out=x_raw[:].rearrange("n r c -> n (r c)"), in_=x_dram[t]
-                        )
+                        nc.sync.dma_start(out=x_raw[:].rearrange("n r c -> n (r c)"), in_=x_dram[t])
                         x = flow.tile([PARTS, C, PACK], BF16, name="x", align_bytes=64)
                         nc.scalar.copy(out=x[:], in_=x_raw[:].rearrange("n r c -> n c r"))
                         x_codes = flow.tile([PARTS, C], U32, name="x_codes", align_bytes=64)

@@ -50,14 +50,14 @@ def tile_iwht3layer_pa_kernel(tc, trans, weight, bias, grad_out, out):
     nc = tc.nc
 
     g_dram = grad_out.rearrange("b (i p) (jh r q) k -> jh (b i) p r q k", p=SIDE, jh=2, r=PACK)
-    x_dram = trans.rearrange("t b i (jh r) c -> t (b i jh) (r c)", r=PACK)
+    x_dram = trans.rearrange("(u v) b i (jh r) c -> u (b i jh) v (r c)", v=SIDE, r=PACK)
     out_dram = out.rearrange("t (h m) k -> t m h k", h=C_HALVES)
+
+    u_order = [2 * u1 + u0 for u0 in range(2) for u1 in range(2)]
 
     with tc.tile_pool(name="keep", bufs=1) as keep, tc.tile_pool(name="flow", bufs=2) as flow, tc.tile_pool(
         name="leaf", bufs=3
-    ) as leaf, tc.tile_pool(name="xin", bufs=4) as xin, tc.psum_pool(name="turn", bufs=1) as turn, tc.psum_pool(
-        name="psum", bufs=4
-    ) as psum:
+    ) as leaf, tc.manual_schedule():
         ident = keep.tile([PARTS, PARTS], BF16, name="ident")
         make_identity(nc, ident[:])
         matrix = transform_matrix(nc, keep, ident)
@@ -71,114 +71,183 @@ def tile_iwht3layer_pa_kernel(tc, trans, weight, bias, grad_out, out):
                         out=g_tile[jh:PARTS:2, :, q : q + 2, :], in_=g_dram[jh, :, :, r, q : q + 2, :]
                     )
             g_tiles.append(g_tile)
-
-        gy_tensor = keep.tile([PARTS, PACK, OCTETS, PARTS], BF16, name="gy_tensor")
-        for r in range(PACK):
-            picked = flow.tile([PARTS, OCTETS, T, OCTET], BF16, name="picked")
-            nc.scalar.copy(
-                out=picked[:],
-                in_=g_tiles[r][:, :, :, 0:K_TENSOR].rearrange("n p q (o e) -> n o (p q) e", e=OCTET),
-            )
-            for first in range(0, OCTETS, GROUP):
-                pixels_psum = turn.tile([PARTS, GROUP, PARTS], BF16, name="pixels_psum")
-                for j in range(GROUP):
-                    nc.tensor.transpose(
-                        out=pixels_psum[:, j, :],
-                        in_=picked[:, first + j, :, :].rearrange("n a e -> n (a e)"),
-                        identity=ident[:],
-                    )
-                pixels = flow.tile([PARTS, GROUP, PARTS], BF16, name="pixels")
-                nc.scalar.copy(out=pixels[:], in_=pixels_psum[:])
-                coeffs_psum = turn.tile([PARTS, GROUP, PARTS], F32, name="coeffs_psum")
-                nc.tensor.matmul(
-                    out=coeffs_psum[:].rearrange("n j m -> n (j m)"),
-                    lhsT=matrix[:],
-                    rhs=pixels[:].rearrange("n j m -> n (j m)"),
-                    start=True,
-                    stop=True,
-                )
-                coeffs = flow.tile([PARTS, GROUP, PARTS], BF16, name="coeffs")
-                nc.scalar.copy(out=coeffs[:], in_=coeffs_psum[:])
-                back_psum = turn.tile([PARTS, GROUP, PARTS], BF16, name="back_psum")
-                for j in range(GROUP):
-                    nc.tensor.transpose(out=back_psum[:, j, :], in_=coeffs[:, j, :], identity=ident[:])
-                nc.scalar.copy(out=gy_tensor[:, r, first : first + GROUP, :], in_=back_psum[:])
-        gy_tensor_by_t = gy_tensor[:].rearrange("n r o (t e) -> n t o e r", e=OCTET)
+        x_raw_of = {}
+        for u in u_order:
+            x_raw = keep.tile([PARTS, SIDE, PACK, C], BF16, name="x_raw")
+            nc.sync.dma_start(out=x_raw[:].rearrange("n v r c -> n v (r c)"), in_=x_dram[u])
+            x_raw_of[u] = x_raw
 
         level1 = keep.tile([PARTS, 2, PACK, SIDE, K_VECTOR], F32, name="level1")
         level2 = keep.tile([PARTS, PACK, SIDE, K_VECTOR], F32, name="level2")
         level3 = keep.tile([PARTS, PACK, 2, K_VECTOR], F32, name="level3")
-        level2_halves = level2[:].rearrange("n r (q1 q0) k -> n r q1 q0 k", q0=2)
 
-        for u0 in range(2):
-            for r in range(PACK):
-                pairs = g_tiles[r][:].rearrange("n (p1 p0) q k -> n p1 p0 q k", p0=2)
-                for q in range(0, SIDE, 2):
-                    nc.vector.tensor_tensor(
-                        out=level1[:, :, r, q : q + 2, :],
-                        in0=pairs[:, :, 0, q : q + 2, K_TENSOR:K],
-                        in1=pairs[:, :, 1, q : q + 2, K_TENSOR:K],
-                        op=SIGN_OP[u0],
+        gy_tensor = keep.tile([PARTS, PACK, OCTETS, PARTS], BF16, name="gy_tensor")
+        gy_tensor_by_t = gy_tensor[:].rearrange("n r o (t e) -> n t o e r", e=OCTET)
+        with tc.tile_pool(name="turn_sbuf", bufs=2) as turn_sbuf, tc.psum_pool(name="turn_psum", bufs=2) as turn_psum:
+            picked_of = {}
+            pixels_of = {}
+            coeffs_of = {}
+
+            def pixels_to_partitions(group):
+                r, first = group // GROUPS_PER_R, (group % GROUPS_PER_R) * GROUP
+                if first == 0:
+                    picked = turn_sbuf.tile([PARTS, OCTETS, T, OCTET], BF16, name="picked")
+                    nc.scalar.copy(
+                        out=picked[:],
+                        in_=g_tiles[r][:, :, :, 0:K_TENSOR].rearrange("n p q (o e) -> n o (p q) e", e=OCTET),
                     )
-            for u1 in range(2):
-                for r in range(PACK):
-                    nc.vector.tensor_tensor(
-                        out=level2[:, r], in0=level1[:, 0, r], in1=level1[:, 1, r], op=SIGN_OP[u1]
+                    picked_of[r] = picked
+                pixels_psum = turn_psum.tile([PARTS, GROUP, PARTS], BF16, name="pixels_psum")
+                for j in range(GROUP):
+                    nc.tensor.transpose(
+                        out=pixels_psum[:, j, :],
+                        in_=picked_of[r][:, first + j, :, :].rearrange("n a e -> n (a e)"),
+                        identity=ident[:],
                     )
-                for v1 in range(2):
-                    nc.vector.tensor_tensor(
-                        out=level3[:], in0=level2_halves[:, :, 0], in1=level2_halves[:, :, 1], op=SIGN_OP[v1]
+                pixels = turn_sbuf.tile([PARTS, GROUP, PARTS], BF16, name="pixels")
+                nc.scalar.copy(out=pixels[:], in_=pixels_psum[:])
+                pixels_of[group] = pixels
+
+            def transform(group):
+                coeffs_psum = turn_psum.tile([PARTS, GROUP, PARTS], F32, name="coeffs_psum")
+                nc.tensor.matmul(
+                    out=coeffs_psum[:].rearrange("n j m -> n (j m)"),
+                    lhsT=matrix[:],
+                    rhs=pixels_of[group][:].rearrange("n j m -> n (j m)"),
+                    start=True,
+                    stop=True,
+                )
+                coeffs = turn_sbuf.tile([PARTS, GROUP, PARTS], BF16, name="coeffs")
+                nc.scalar.copy(out=coeffs[:], in_=coeffs_psum[:])
+                coeffs_of[group] = coeffs
+
+            def coefficients_back(group):
+                r, first = group // GROUPS_PER_R, (group % GROUPS_PER_R) * GROUP
+                back_psum = turn_psum.tile([PARTS, GROUP, PARTS], BF16, name="back_psum")
+                for j in range(GROUP):
+                    nc.tensor.transpose(
+                        out=back_psum[:, j, :], in_=coeffs_of[group][:, j, :], identity=ident[:]
                     )
-                    for v0 in range(2):
-                        t = SIDE * (2 * u1 + u0) + 2 * v1 + v0
+                nc.scalar.copy(out=gy_tensor[:, r, first : first + GROUP, :], in_=back_psum[:])
 
-                        sums = leaf.tile([PARTS, PACK, K_VECTOR], BF16, name="sums")
-                        nc.vector.tensor_tensor(
-                            out=sums[:], in0=level3[:, :, 0, :], in1=level3[:, :, 1, :], op=SIGN_OP[v0]
-                        )
-                        gy = flow.tile([PARTS, K, PACK], BF16, name="gy", align_bytes=64)
-                        nc.scalar.copy(
-                            out=gy[:, 0:K_TENSOR, :].rearrange("n (o e) r -> n o e r", e=OCTET),
-                            in_=gy_tensor_by_t[:, t],
-                        )
-                        nc.scalar.activation(
-                            out=gy[:, K_TENSOR:K, :],
-                            in_=sums[:].rearrange("n r k -> n k r"),
-                            func=COPY,
-                            scale=1.0 / T,
-                        )
-                        gy_codes = flow.tile([PARTS, K], U32, name="gy_codes", align_bytes=64)
-                        gy_scales = flow.tile([PARTS, K], U8, name="gy_scales", align_bytes=64)
-                        nc.vector.quantize_mx(
-                            out=gy_codes[:].bitcast(E5M2_X4),
-                            scales=gy_scales[:],
-                            in_=gy[:].rearrange("n k r -> n (k r)"),
-                        )
+            groups = PACK * GROUPS_PER_R
+            for step in range(groups + 2):
+                if step < groups:
+                    pixels_to_partitions(step)
+                if 1 <= step <= groups:
+                    transform(step - 1)
+                if step >= 2:
+                    coefficients_back(step - 2)
 
-                        x_raw = xin.tile([PARTS, PACK, C], BF16, name="x_raw")
-                        nc.sync.dma_start(out=x_raw[:].rearrange("n r c -> n (r c)"), in_=x_dram[t])
-                        x = flow.tile([PARTS, C, PACK], BF16, name="x", align_bytes=64)
-                        nc.scalar.copy(out=x[:], in_=x_raw[:].rearrange("n r c -> n c r"))
-                        x_codes = flow.tile([PARTS, C], U32, name="x_codes", align_bytes=64)
-                        x_scales = flow.tile([PARTS, C], U8, name="x_scales", align_bytes=64)
-                        nc.vector.quantize_mx(
-                            out=x_codes[:].bitcast(E4M3_X4),
-                            scales=x_scales[:],
-                            in_=x[:].rearrange("n c r -> n (c r)"),
-                        )
+        with tc.tile_pool(name="x_pool", bufs=1) as x_pool, tc.psum_pool(name="psum", bufs=4) as psum:
+            level2_halves = level2[:].rearrange("n r (q1 q0) k -> n r q1 q0 k", q0=2)
+            x_of = {}
+            x_codes_of = {}
+            prepared = {}
+            products = {}
 
-                        result = flow.tile([PARTS, C_HALVES, K], F32, name="result")
-                        for h in range(C_HALVES):
-                            cols = slice(h * PARTS, (h + 1) * PARTS)
-                            acc = psum.tile([PARTS, K], F32, name="acc")
-                            nc.tensor.matmul_mx(
-                                out=acc[:],
-                                lhsT=x_codes[:, cols].bitcast(E4M3_X4),
-                                lhsT_scale=x_scales[:, cols],
-                                rhs=gy_codes[:].bitcast(E5M2_X4),
-                                rhs_scale=gy_scales[:],
-                                start=True,
-                                stop=True,
+            def prepare(number, t, sums):
+                gy = leaf.tile([PARTS, K, PACK], BF16, name="gy", align_bytes=64)
+                nc.scalar.copy(
+                    out=gy[:, 0:K_TENSOR, :].rearrange("n (o e) r -> n o e r", e=OCTET), in_=gy_tensor_by_t[:, t]
+                )
+                nc.scalar.activation(
+                    out=gy[:, K_TENSOR:K, :], in_=sums[:].rearrange("n r k -> n k r"), func=COPY, scale=1.0 / T
+                )
+                prepared[number] = (t, gy)
+
+            def multiply(number):
+                if number < 0:
+                    return
+                t, gy = prepared[number]
+                u, v = t // SIDE, t % SIDE
+                if u not in x_codes_of:
+                    x_codes = flow.tile([PARTS, SIDE * C], U32, name="x_codes", align_bytes=64)
+                    x_scales = flow.tile([PARTS, SIDE * C], U8, name="x_scales", align_bytes=64)
+                    nc.vector.quantize_mx(
+                        out=x_codes[:].bitcast(E4M3_X4),
+                        scales=x_scales[:],
+                        in_=x_of[u][:].rearrange("n v c r -> n (v c r)"),
+                    )
+                    x_codes_of[u] = (x_codes, x_scales)
+                x_codes, x_scales = x_codes_of[u]
+                gy_codes = flow.tile([PARTS, K], U32, name="gy_codes", align_bytes=64)
+                gy_scales = flow.tile([PARTS, K], U8, name="gy_scales", align_bytes=64)
+                nc.vector.quantize_mx(
+                    out=gy_codes[:].bitcast(E5M2_X4), scales=gy_scales[:], in_=gy[:].rearrange("n k r -> n (k r)")
+                )
+                banks = []
+                for h in range(C_HALVES):
+                    column = v * C + h * PARTS
+                    acc = psum.tile([PARTS, K], F32, name="acc")
+                    nc.tensor.matmul_mx(
+                        out=acc[:],
+                        lhsT=x_codes[:, column : column + PARTS].bitcast(E4M3_X4),
+                        lhsT_scale=x_scales[:, column : column + PARTS],
+                        rhs=gy_codes[:].bitcast(E5M2_X4),
+                        rhs_scale=gy_scales[:],
+                        start=True,
+                        stop=True,
+                    )
+                    banks.append(acc)
+                products[number] = (t, banks)
+
+            def store(number, vector_is_idle):
+                if number < 0:
+                    return
+                t, banks = products[number]
+                result = flow.tile([PARTS, C_HALVES, K], F32, name="result")
+                for h in range(C_HALVES):
+                    if vector_is_idle:
+                        nc.vector.tensor_copy(out=result[:, h, :], in_=banks[h][:])
+                    else:
+                        nc.scalar.copy(out=result[:, h, :], in_=banks[h][:])
+                store_queue = nc.sync if vector_is_idle else nc.scalar
+                store_queue.dma_start(out=out_dram[t], in_=result[:])
+
+            number = 0
+            for u0 in range(2):
+                for u1 in range(2):
+                    u = 2 * u1 + u0
+                    x = x_pool.tile([PARTS, SIDE, C, PACK], BF16, name="x", align_bytes=64)
+                    nc.scalar.copy(out=x[:], in_=x_raw_of[u][:].rearrange("n v r c -> n v c r"))
+                    x_of[u] = x
+                    for r in range(PACK + 1):
+                        if u1 == 0 and r < PACK:
+                            pairs = g_tiles[r][:].rearrange("n (p1 p0) q k -> n p1 p0 q k", p0=2)
+                            for q in range(0, SIDE, 2):
+                                nc.vector.tensor_tensor(
+                                    out=level1[:, :, r, q : q + 2, :],
+                                    in0=pairs[:, :, 0, q : q + 2, K_TENSOR:K],
+                                    in1=pairs[:, :, 1, q : q + 2, K_TENSOR:K],
+                                    op=SIGN_OP[u0],
+                                )
+                        if r >= 1:
+                            nc.vector.tensor_tensor(
+                                out=level2[:, r - 1],
+                                in0=level1[:, 0, r - 1],
+                                in1=level1[:, 1, r - 1],
+                                op=SIGN_OP[u1],
                             )
-                            nc.scalar.copy(out=result[:, h, :], in_=acc[:])
-                        nc.scalar.dma_start(out=out_dram[t], in_=result[:])
+                    for v1 in range(2):
+                        nc.vector.tensor_tensor(
+                            out=level3[:],
+                            in0=level2_halves[:, :, 0],
+                            in1=level2_halves[:, :, 1],
+                            op=SIGN_OP[v1],
+                        )
+                        multiply(number - 2)
+                        for v0 in range(2):
+                            sums = leaf.tile([PARTS, PACK, K_VECTOR], BF16, name="sums")
+                            nc.vector.tensor_tensor(
+                                out=sums[:], in0=level3[:, :, 0, :], in1=level3[:, :, 1, :], op=SIGN_OP[v0]
+                            )
+                            prepare(number + v0, SIDE * u + 2 * v1 + v0, sums)
+                        multiply(number - 1)
+                        store(number - 2, False)
+                        store(number - 1, False)
+                        number += 2
+            multiply(number - 2)
+            multiply(number - 1)
+            store(number - 2, True)
+            store(number - 1, True)

@@ -32,7 +32,7 @@ BYTES = 2 * T * N * C + 2 * T * N * K + 4 * T * C * K
 
 def transform_matrix(nc, pool, ident):
     current = pool.tile([PARTS, PARTS], BF16, name="matrix0")
-    nc.vector.tensor_scalar_mul(out=current[:], in0=ident[:], scalar1=1.0 / T)
+    nc.scalar.activation(out=current[:], in_=ident[:], func=COPY, scale=1.0 / T)
     for level in range(4):
         step = PARTS // 2 ** (level + 1)
         following = pool.tile([PARTS, PARTS], BF16, name="matrix%d" % (level + 1))
@@ -86,7 +86,6 @@ def tile_iwht3layer_pa_kernel(tc, trans, weight, bias, grad_out, out):
         with tc.tile_pool(name="turn_sbuf", bufs=2) as turn_sbuf, tc.psum_pool(name="turn_psum", bufs=2) as turn_psum:
             picked_of = {}
             pixels_of = {}
-            coeffs_of = {}
 
             def pixels_to_partitions(group):
                 r, first = group // GROUPS_PER_R, (group % GROUPS_PER_R) * GROUP
@@ -109,35 +108,20 @@ def tile_iwht3layer_pa_kernel(tc, trans, weight, bias, grad_out, out):
                 pixels_of[group] = pixels
 
             def transform(group):
-                coeffs_psum = turn_psum.tile([PARTS, GROUP, PARTS], F32, name="coeffs_psum")
-                nc.tensor.matmul(
-                    out=coeffs_psum[:].rearrange("n j m -> n (j m)"),
-                    lhsT=matrix[:],
-                    rhs=pixels_of[group][:].rearrange("n j m -> n (j m)"),
-                    start=True,
-                    stop=True,
-                )
-                coeffs = turn_sbuf.tile([PARTS, GROUP, PARTS], BF16, name="coeffs")
-                nc.scalar.copy(out=coeffs[:], in_=coeffs_psum[:])
-                coeffs_of[group] = coeffs
-
-            def coefficients_back(group):
                 r, first = group // GROUPS_PER_R, (group % GROUPS_PER_R) * GROUP
-                back_psum = turn_psum.tile([PARTS, GROUP, PARTS], BF16, name="back_psum")
+                coeffs_psum = turn_psum.tile([PARTS, GROUP, PARTS], F32, name="coeffs_psum")
                 for j in range(GROUP):
-                    nc.tensor.transpose(
-                        out=back_psum[:, j, :], in_=coeffs_of[group][:, j, :], identity=ident[:]
+                    nc.tensor.matmul(
+                        out=coeffs_psum[:, j, :], lhsT=pixels_of[group][:, j, :], rhs=matrix[:], start=True, stop=True
                     )
-                nc.scalar.copy(out=gy_tensor[:, r, first : first + GROUP, :], in_=back_psum[:])
+                nc.scalar.copy(out=gy_tensor[:, r, first : first + GROUP, :], in_=coeffs_psum[:])
 
             groups = PACK * GROUPS_PER_R
-            for step in range(groups + 2):
+            for step in range(groups + 1):
                 if step < groups:
                     pixels_to_partitions(step)
-                if 1 <= step <= groups:
+                if step >= 1:
                     transform(step - 1)
-                if step >= 2:
-                    coefficients_back(step - 2)
 
         with tc.tile_pool(name="x_pool", bufs=1) as x_pool, tc.psum_pool(name="psum", bufs=4) as psum:
             level2_halves = level2[:].rearrange("n r (q1 q0) k -> n r q1 q0 k", q0=2)

@@ -14,6 +14,7 @@ PARTS = 128
 PACK = 4
 SIDE = 4
 T = SIDE * SIDE
+LEVELS = 4
 N = 512
 C = 256
 K = 512
@@ -33,11 +34,11 @@ BYTES = 2 * T * N * C + 2 * T * N * K + 4 * T * C * K
 def transform_matrix(nc, pool, ident):
     current = pool.tile([PARTS, PARTS], BF16, name="matrix0")
     nc.scalar.activation(out=current[:], in_=ident[:], func=COPY, scale=1.0 / T)
-    for level in range(4):
-        step = PARTS // 2 ** (level + 1)
+    for level in range(LEVELS):
+        distance = PARTS // 2 ** (level + 1)
         following = pool.tile([PARTS, PARTS], BF16, name="matrix%d" % (level + 1))
-        halves = current[:].rearrange("n (a two b) -> n a two b", two=2, b=step)
-        signed = following[:].rearrange("n (a two b) -> n a two b", two=2, b=step)
+        halves = current[:].rearrange("n (a two b) -> n a two b", two=2, b=distance)
+        signed = following[:].rearrange("n (a two b) -> n a two b", two=2, b=distance)
         for bit in range(2):
             nc.vector.tensor_tensor(
                 out=signed[:, :, bit, :], in0=halves[:, :, 0, :], in1=halves[:, :, 1, :], op=SIGN_OP[bit]
@@ -49,7 +50,7 @@ def transform_matrix(nc, pool, ident):
 def tile_iwht3layer_pa_kernel(tc, trans, weight, bias, grad_out, out):
     nc = tc.nc
 
-    g_dram = grad_out.rearrange("b (i p) (jh r q) k -> jh (b i) p r q k", p=SIDE, jh=2, r=PACK)
+    g_dram = grad_out.rearrange("b (i p) (jh r q) k -> jh (b i) p r (q k)", p=SIDE, jh=2, r=PACK)
     x_dram = trans.rearrange("(u v) b i (jh r) c -> u (b i jh) v (r c)", v=SIDE, r=PACK)
     out_dram = out.rearrange("t (h m) k -> t m h k", h=C_HALVES)
 
@@ -65,10 +66,11 @@ def tile_iwht3layer_pa_kernel(tc, trans, weight, bias, grad_out, out):
         g_tiles = []
         for r in range(PACK):
             g_tile = keep.tile([PARTS, SIDE, SIDE, K], BF16, name="g%d" % r)
-            for q in range(0, SIDE, 2):
+            for p in range(0, SIDE, 2):
                 for jh in range(2):
                     nc.sync.dma_start(
-                        out=g_tile[jh:PARTS:2, :, q : q + 2, :], in_=g_dram[jh, :, :, r, q : q + 2, :]
+                        out=g_tile[jh:PARTS:2, p : p + 2, :, :].rearrange("n p q k -> n p (q k)"),
+                        in_=g_dram[jh, :, p : p + 2, r, :],
                     )
             g_tiles.append(g_tile)
         x_raw_of = {}
@@ -127,24 +129,23 @@ def tile_iwht3layer_pa_kernel(tc, trans, weight, bias, grad_out, out):
             level2_halves = level2[:].rearrange("n r (q1 q0) k -> n r q1 q0 k", q0=2)
             x_of = {}
             x_codes_of = {}
-            prepared = {}
-            products = {}
+            t_of = {}
+            gy_of = {}
+            banks_of = {}
 
-            def prepare(number, t, sums):
+            def open_leaf(number, t):
                 gy = leaf.tile([PARTS, K, PACK], BF16, name="gy", align_bytes=64)
                 nc.scalar.copy(
                     out=gy[:, 0:K_TENSOR, :].rearrange("n (o e) r -> n o e r", e=OCTET), in_=gy_tensor_by_t[:, t]
                 )
-                nc.scalar.activation(
-                    out=gy[:, K_TENSOR:K, :], in_=sums[:].rearrange("n r k -> n k r"), func=COPY, scale=1.0 / T
-                )
-                prepared[number] = (t, gy)
+                t_of[number] = t
+                gy_of[number] = gy
 
             def multiply(number):
                 if number < 0:
                     return
-                t, gy = prepared[number]
-                u, v = t // SIDE, t % SIDE
+                gy = gy_of[number]
+                u, v = t_of[number] // SIDE, t_of[number] % SIDE
                 if u not in x_codes_of:
                     x_codes = flow.tile([PARTS, SIDE * C], U32, name="x_codes", align_bytes=64)
                     x_scales = flow.tile([PARTS, SIDE * C], U8, name="x_scales", align_bytes=64)
@@ -174,20 +175,19 @@ def tile_iwht3layer_pa_kernel(tc, trans, weight, bias, grad_out, out):
                         stop=True,
                     )
                     banks.append(acc)
-                products[number] = (t, banks)
+                banks_of[number] = banks
 
             def store(number, vector_is_idle):
                 if number < 0:
                     return
-                t, banks = products[number]
                 result = flow.tile([PARTS, C_HALVES, K], F32, name="result")
                 for h in range(C_HALVES):
                     if vector_is_idle:
-                        nc.vector.tensor_copy(out=result[:, h, :], in_=banks[h][:])
+                        nc.vector.tensor_copy(out=result[:, h, :], in_=banks_of[number][h][:])
                     else:
-                        nc.scalar.copy(out=result[:, h, :], in_=banks[h][:])
+                        nc.scalar.copy(out=result[:, h, :], in_=banks_of[number][h][:])
                 store_queue = nc.sync if vector_is_idle else nc.scalar
-                store_queue.dma_start(out=out_dram[t], in_=result[:])
+                store_queue.dma_start(out=out_dram[t_of[number]], in_=result[:])
 
             number = 0
             for u0 in range(2):
@@ -198,12 +198,11 @@ def tile_iwht3layer_pa_kernel(tc, trans, weight, bias, grad_out, out):
                     x_of[u] = x
                     for r in range(PACK + 1):
                         if u1 == 0 and r < PACK:
-                            pairs = g_tiles[r][:].rearrange("n (p1 p0) q k -> n p1 p0 q k", p0=2)
-                            for q in range(0, SIDE, 2):
+                            for p1 in range(2):
                                 nc.vector.tensor_tensor(
-                                    out=level1[:, :, r, q : q + 2, :],
-                                    in0=pairs[:, :, 0, q : q + 2, K_TENSOR:K],
-                                    in1=pairs[:, :, 1, q : q + 2, K_TENSOR:K],
+                                    out=level1[:, p1, r],
+                                    in0=g_tiles[r][:, 2 * p1, :, K_TENSOR:K],
+                                    in1=g_tiles[r][:, 2 * p1 + 1, :, K_TENSOR:K],
                                     op=SIGN_OP[u0],
                                 )
                         if r >= 1:
@@ -222,11 +221,18 @@ def tile_iwht3layer_pa_kernel(tc, trans, weight, bias, grad_out, out):
                         )
                         multiply(number - 2)
                         for v0 in range(2):
+                            open_leaf(number + v0, SIDE * u + 2 * v1 + v0)
+                        for v0 in range(2):
                             sums = leaf.tile([PARTS, PACK, K_VECTOR], BF16, name="sums")
                             nc.vector.tensor_tensor(
                                 out=sums[:], in0=level3[:, :, 0, :], in1=level3[:, :, 1, :], op=SIGN_OP[v0]
                             )
-                            prepare(number + v0, SIDE * u + 2 * v1 + v0, sums)
+                            nc.scalar.activation(
+                                out=gy_of[number + v0][:, K_TENSOR:K, :],
+                                in_=sums[:].rearrange("n r k -> n k r"),
+                                func=COPY,
+                                scale=1.0 / T,
+                            )
                         multiply(number - 1)
                         store(number - 2, False)
                         store(number - 1, False)

@@ -21,19 +21,23 @@ K = 512
 C_HALVES = C // PARTS
 
 OCTET = PARTS // T
-GROUP = 4
-GROUPS_PER_R = 3
-OCTETS = GROUP * GROUPS_PER_R
+OCTETS = 12
 K_TENSOR = OCTETS * OCTET
-K_VECTOR = K - K_TENSOR
+K_POOL = 96
+K_SIDE = K_TENSOR + K_POOL
+K_VECTOR = K - K_SIDE
+UNIT = K_VECTOR * PACK
+UNIT_G = K_POOL * PACK
+BLOCK = 128
+BLOCKS = 4
+CHUNK = BLOCK * BLOCKS
 
 FLOPS = 2 * T * N * C * K
 BYTES = 2 * T * N * C + 2 * T * N * K + 4 * T * C * K
 
 
 def transform_matrix(nc, pool, ident):
-    current = pool.tile([PARTS, PARTS], BF16, name="matrix0")
-    nc.scalar.activation(out=current[:], in_=ident[:], func=COPY, scale=1.0 / T)
+    current = ident
     for level in range(LEVELS):
         distance = PARTS // 2 ** (level + 1)
         following = pool.tile([PARTS, PARTS], BF16, name="matrix%d" % (level + 1))
@@ -50,194 +54,329 @@ def transform_matrix(nc, pool, ident):
 def tile_iwht3layer_pa_kernel(tc, trans, weight, bias, grad_out, out):
     nc = tc.nc
 
-    g_dram = grad_out.rearrange("b (i p) (jh r q) k -> jh (b i) p r (q k)", p=SIDE, jh=2, r=PACK)
+    g_dram = grad_out.rearrange("b (i p) (jh r q) k -> jh p q (b i) r k", p=SIDE, jh=2, r=PACK)
     x_dram = trans.rearrange("(u v) b i (jh r) c -> u (b i jh) v (r c)", v=SIDE, r=PACK)
     out_dram = out.rearrange("t (h m) k -> t m h k", h=C_HALVES)
 
     u_order = [2 * u1 + u0 for u0 in range(2) for u1 in range(2)]
 
-    with tc.tile_pool(name="keep", bufs=1) as keep, tc.tile_pool(name="flow", bufs=2) as flow, tc.tile_pool(
-        name="leaf", bufs=3
-    ) as leaf, tc.manual_schedule():
+    with tc.tile_pool(name="keep", bufs=1) as keep, tc.tile_pool(name="turned", bufs=3) as turned, tc.tile_pool(
+        name="pixel_pool", bufs=2
+    ) as pixel_pool, tc.psum_pool(name="psum_t", bufs=2) as psum_t, tc.psum_pool(
+        name="psum_a", bufs=2
+    ) as psum_a, tc.manual_schedule():
         ident = keep.tile([PARTS, PARTS], BF16, name="ident")
         make_identity(nc, ident[:])
+        ident_f = keep.tile([PARTS, PARTS], F32, name="ident_f")
+        make_identity(nc, ident_f[:])
+        warm = keep.tile([PARTS, 1], BF16, name="warm")
+        nc.scalar.copy(out=warm[:], in_=ident[:, 0:1])
         matrix = transform_matrix(nc, keep, ident)
 
-        g_tiles = []
-        for r in range(PACK):
-            g_tile = keep.tile([PARTS, SIDE, SIDE, K], BF16, name="g%d" % r)
-            for p in range(0, SIDE, 2):
-                for jh in range(2):
-                    nc.sync.dma_start(
-                        out=g_tile[jh:PARTS:2, p : p + 2, :, :].rearrange("n p q k -> n p (q k)"),
-                        in_=g_dram[jh, :, p : p + 2, r, :],
+        work = keep.tile([PARTS, T * UNIT], F32, name="work")
+        pool_a = keep.tile([PARTS, T * UNIT_G], F32, name="pool_a")
+        picked = keep.tile([PARTS, PACK, OCTETS, T, OCTET], BF16, name="picked")
+        side = keep.tile([PARTS, 2, T, UNIT_G], BF16, name="side")
+
+        jobs = []
+        st_of = {}
+        pa_of = {}
+
+        def turn(s):
+            pt = psum_t.tile([PARTS, BLOCKS, BLOCK], F32, name="pt")
+            for j in range(BLOCKS):
+                nc.tensor.transpose(out=pt[:, j, :], in_=jobs[s][0][j], identity=ident_f[:])
+            st = turned.tile([PARTS, BLOCKS, BLOCK], F32, name="st")
+            nc.scalar.copy(out=st[:], in_=pt[:])
+            st_of[s] = st
+
+        def turn_back(s):
+            pa = psum_a.tile([PARTS, BLOCKS, BLOCK], F32, name="pa")
+            for j in range(BLOCKS):
+                nc.tensor.transpose(out=pa[:, j, :], in_=st_of[s][:, j, :], identity=ident_f[:])
+            pa_of[s] = pa
+
+        def in_place(a0, b0):
+            def consume(pa):
+                first = pa[:].rearrange("n j w -> n (j w)")
+                nc.vector.tensor_tensor(
+                    out=work[:, a0 : a0 + CHUNK], in0=first, in1=work[:, b0 : b0 + CHUNK], op=SIGN_OP[0]
+                )
+                nc.vector.tensor_tensor(
+                    out=work[:, b0 : b0 + CHUNK], in0=first, in1=work[:, b0 : b0 + CHUNK], op=SIGN_OP[1]
+                )
+
+            return consume
+
+        def chunk_job(a0, b0):
+            sources = [work[:, a0 + j * BLOCK : a0 + (j + 1) * BLOCK] for j in range(BLOCKS)]
+            jobs.append((sources, in_place(a0, b0)))
+
+        chores = {}
+
+        def add_chore(step, chore):
+            chores.setdefault(step, []).append(chore)
+
+        def run_steps(first, last):
+            for s in range(first, last):
+                if s < len(jobs):
+                    turn(s)
+                for chore in chores.get(s, []):
+                    chore()
+                if 0 <= s - 2 < len(jobs):
+                    turn_back(s - 2)
+                if 0 <= s - 3 < len(jobs):
+                    jobs[s - 3][1](pa_of[s - 3])
+
+        with tc.tile_pool(name="g_pool", bufs=1) as g_pool:
+            g = {}
+            for q in range(SIDE):
+                for p in range(SIDE):
+                    g[q, p] = g_pool.tile([PARTS, PACK, K], BF16, name="g%d%d" % (q, p))
+                    for jh in range(2):
+                        nc.sync.dma_start(out=g[q, p][jh:PARTS:2, :, :], in_=g_dram[jh, p, q])
+
+            for q in range(SIDE):
+                for p1 in range(2):
+                    for u0 in range(2):
+                        start = ((u0 * 2 + p1) * SIDE + q) * UNIT_G
+                        nc.gpsimd.tensor_tensor(
+                            out=pool_a[:, start : start + UNIT_G].rearrange("n (k r) -> n k r", r=PACK),
+                            in0=g[q, 2 * p1][:, :, K_TENSOR:K_SIDE].rearrange("n r k -> n k r"),
+                            in1=g[q, 2 * p1 + 1][:, :, K_TENSOR:K_SIDE].rearrange("n r k -> n k r"),
+                            op=SIGN_OP[u0],
+                        )
+
+            def level1(p1, q, source_from, k_from, k_to):
+                def consume(pa):
+                    first = pa[:].bitcast(BF16)[:, :, k_from - source_from : k_to - source_from].rearrange(
+                        "n r k -> n k r"
                     )
-            g_tiles.append(g_tile)
-        x_raw_of = {}
-        for u in u_order:
-            x_raw = keep.tile([PARTS, SIDE, PACK, C], BF16, name="x_raw")
-            nc.sync.dma_start(out=x_raw[:].rearrange("n v r c -> n v (r c)"), in_=x_dram[u])
-            x_raw_of[u] = x_raw
+                    second = g[q, 2 * p1 + 1][:, :, k_from:k_to].rearrange("n r k -> n k r")
+                    for u0 in range(2):
+                        start = ((q * 2 + p1) * 2 + u0) * UNIT + (k_from - K_SIDE) * PACK
+                        nc.vector.tensor_tensor(
+                            out=work[:, start : start + (k_to - k_from) * PACK].rearrange(
+                                "n (k r) -> n k r", r=PACK
+                            ),
+                            in0=first,
+                            in1=second,
+                            op=SIGN_OP[u0],
+                        )
 
-        level1 = keep.tile([PARTS, 2, PACK, SIDE, K_VECTOR], F32, name="level1")
-        level2 = keep.tile([PARTS, PACK, SIDE, K_VECTOR], F32, name="level2")
-        level3 = keep.tile([PARTS, PACK, 2, K_VECTOR], F32, name="level3")
+                return consume
 
-        gy_tensor = keep.tile([PARTS, PACK, OCTETS, PARTS], BF16, name="gy_tensor")
-        gy_tensor_by_t = gy_tensor[:].rearrange("n r o (t e) -> n t o e r", e=OCTET)
-        with tc.tile_pool(name="turn_sbuf", bufs=2) as turn_sbuf, tc.psum_pool(name="turn_psum", bufs=2) as turn_psum:
-            picked_of = {}
-            pixels_of = {}
-
-            def pixels_to_partitions(group):
-                r, first = group // GROUPS_PER_R, (group % GROUPS_PER_R) * GROUP
-                if first == 0:
-                    picked = turn_sbuf.tile([PARTS, OCTETS, T, OCTET], BF16, name="picked")
+            def pick(q, p):
+                def chore():
                     nc.scalar.copy(
-                        out=picked[:],
-                        in_=g_tiles[r][:, :, :, 0:K_TENSOR].rearrange("n p q (o e) -> n o (p q) e", e=OCTET),
+                        out=picked[:, :, :, SIDE * p + q, :],
+                        in_=g[q, p][:, :, 0:K_TENSOR].rearrange("n r (o e) -> n r o e", e=OCTET),
                     )
-                    picked_of[r] = picked
-                pixels_psum = turn_psum.tile([PARTS, GROUP, PARTS], BF16, name="pixels_psum")
-                for j in range(GROUP):
-                    nc.tensor.transpose(
-                        out=pixels_psum[:, j, :],
-                        in_=picked_of[r][:, first + j, :, :].rearrange("n a e -> n (a e)"),
-                        identity=ident[:],
-                    )
-                pixels = turn_sbuf.tile([PARTS, GROUP, PARTS], BF16, name="pixels")
-                nc.scalar.copy(out=pixels[:], in_=pixels_psum[:])
-                pixels_of[group] = pixels
 
-            def transform(group):
-                r, first = group // GROUPS_PER_R, (group % GROUPS_PER_R) * GROUP
-                coeffs_psum = turn_psum.tile([PARTS, GROUP, PARTS], F32, name="coeffs_psum")
-                for j in range(GROUP):
-                    nc.tensor.matmul(
-                        out=coeffs_psum[:, j, :], lhsT=pixels_of[group][:, j, :], rhs=matrix[:], start=True, stop=True
-                    )
-                nc.scalar.copy(out=gy_tensor[:, r, first : first + GROUP, :], in_=coeffs_psum[:])
+                return chore
 
-            groups = PACK * GROUPS_PER_R
-            for step in range(groups + 1):
-                if step < groups:
-                    pixels_to_partitions(step)
-                if step >= 1:
-                    transform(step - 1)
+            for q in range(SIDE):
+                for p1 in range(2):
+                    for source_from, k_from, k_to in ((K_SIDE, K_SIDE, K_SIDE + 256), (K - 256, K_SIDE + 256, K)):
+                        sources = [
+                            g[q, 2 * p1][:, r, source_from : source_from + 256].bitcast(F32) for r in range(PACK)
+                        ]
+                        jobs.append((sources, level1(p1, q, source_from, k_from, k_to)))
+                for p in range(SIDE):
+                    add_chore(len(jobs) - 1 + p, pick(q, p))
+            level1_jobs = len(jobs)
 
-        with tc.tile_pool(name="x_pool", bufs=1) as x_pool, tc.psum_pool(name="psum", bufs=4) as psum:
-            level2_halves = level2[:].rearrange("n r (q1 q0) k -> n r q1 q0 k", q0=2)
+            for q in range(SIDE):
+                for c in range(2 * UNIT // CHUNK):
+                    chunk_job(q * 4 * UNIT + c * CHUNK, (q * 4 + 2) * UNIT + c * CHUNK)
+            for c in range(8 * UNIT // CHUNK):
+                chunk_job(c * CHUNK, 8 * UNIT + c * CHUNK)
+
+            run_steps(0, level1_jobs + 3)
+
+        with tc.tile_pool(name="x_pool", bufs=2) as x_pool:
+            x_raw_of = {}
             x_of = {}
             x_codes_of = {}
-            t_of = {}
-            gy_of = {}
-            banks_of = {}
 
-            def open_leaf(number, t):
-                gy = leaf.tile([PARTS, K, PACK], BF16, name="gy", align_bytes=64)
-                nc.scalar.copy(
-                    out=gy[:, 0:K_TENSOR, :].rearrange("n (o e) r -> n o e r", e=OCTET), in_=gy_tensor_by_t[:, t]
-                )
-                t_of[number] = t
-                gy_of[number] = gy
+            def load_x(u):
+                x_raw = x_pool.tile([PARTS, SIDE, PACK, C], BF16, name="x_raw")
+                nc.sync.dma_start(out=x_raw[:].rearrange("n v r c -> n v (r c)"), in_=x_dram[u])
+                x_raw_of[u] = x_raw
 
-            def multiply(number):
-                if number < 0:
-                    return
-                gy = gy_of[number]
-                u, v = t_of[number] // SIDE, t_of[number] % SIDE
-                if u not in x_codes_of:
-                    x_codes = flow.tile([PARTS, SIDE * C], U32, name="x_codes", align_bytes=64)
-                    x_scales = flow.tile([PARTS, SIDE * C], U8, name="x_scales", align_bytes=64)
-                    nc.vector.quantize_mx(
-                        out=x_codes[:].bitcast(E4M3_X4),
-                        scales=x_scales[:],
-                        in_=x_of[u][:].rearrange("n v c r -> n (v c r)"),
-                    )
-                    x_codes_of[u] = (x_codes, x_scales)
-                x_codes, x_scales = x_codes_of[u]
-                gy_codes = flow.tile([PARTS, K], U32, name="gy_codes", align_bytes=64)
-                gy_scales = flow.tile([PARTS, K], U8, name="gy_scales", align_bytes=64)
-                nc.vector.quantize_mx(
-                    out=gy_codes[:].bitcast(E5M2_X4), scales=gy_scales[:], in_=gy[:].rearrange("n k r -> n (k r)")
-                )
-                banks = []
-                for h in range(C_HALVES):
-                    column = v * C + h * PARTS
-                    acc = psum.tile([PARTS, K], F32, name="acc")
-                    nc.tensor.matmul_mx(
-                        out=acc[:],
-                        lhsT=x_codes[:, column : column + PARTS].bitcast(E4M3_X4),
-                        lhsT_scale=x_scales[:, column : column + PARTS],
-                        rhs=gy_codes[:].bitcast(E5M2_X4),
-                        rhs_scale=gy_scales[:],
-                        start=True,
-                        stop=True,
-                    )
-                    banks.append(acc)
-                banks_of[number] = banks
+            def regroup_x(u, v):
+                def chore():
+                    if v == 0:
+                        x_of[u] = x_pool.tile([PARTS, SIDE, C, PACK], BF16, name="x", align_bytes=64)
+                    nc.scalar.copy(out=x_of[u][:, v], in_=x_raw_of[u][:, v].rearrange("n r c -> n c r"))
 
-            def store(number, vector_is_idle):
-                if number < 0:
-                    return
-                result = flow.tile([PARTS, C_HALVES, K], F32, name="result")
-                for h in range(C_HALVES):
-                    if vector_is_idle:
-                        nc.vector.tensor_copy(out=result[:, h, :], in_=banks_of[number][h][:])
-                    else:
-                        nc.scalar.copy(out=result[:, h, :], in_=banks_of[number][h][:])
-                store_queue = nc.sync if vector_is_idle else nc.scalar
-                store_queue.dma_start(out=out_dram[t_of[number]], in_=result[:])
+                return chore
 
-            number = 0
-            for u0 in range(2):
-                for u1 in range(2):
-                    u = 2 * u1 + u0
-                    x = x_pool.tile([PARTS, SIDE, C, PACK], BF16, name="x", align_bytes=64)
-                    nc.scalar.copy(out=x[:], in_=x_raw_of[u][:].rearrange("n v r c -> n v c r"))
-                    x_of[u] = x
-                    for r in range(PACK + 1):
-                        if u1 == 0 and r < PACK:
-                            for p1 in range(2):
-                                nc.vector.tensor_tensor(
-                                    out=level1[:, p1, r],
-                                    in0=g_tiles[r][:, 2 * p1, :, K_TENSOR:K],
-                                    in1=g_tiles[r][:, 2 * p1 + 1, :, K_TENSOR:K],
-                                    op=SIGN_OP[u0],
-                                )
-                        if r >= 1:
-                            nc.vector.tensor_tensor(
-                                out=level2[:, r - 1],
-                                in0=level1[:, 0, r - 1],
-                                in1=level1[:, 1, r - 1],
-                                op=SIGN_OP[u1],
-                            )
-                    for v1 in range(2):
-                        nc.vector.tensor_tensor(
-                            out=level3[:],
-                            in0=level2_halves[:, :, 0],
-                            in1=level2_halves[:, :, 1],
-                            op=SIGN_OP[v1],
+            load_x(u_order[0])
+            load_x(u_order[1])
+
+            with tc.tile_pool(name="pool_pool", bufs=1) as pool_pool, tc.psum_pool(name="psum_pe", bufs=2) as psum_pe:
+                pool_b = pool_pool.tile([PARTS, 8 * UNIT_G], F32, name="pool_b")
+                side_by_bits = side[:, 1].rearrange("n (u1 u0 v1 v0) x -> n u1 u0 v1 v0 x", u1=2, u0=2, v1=2)
+                for u0 in range(2):
+                    half = pool_a[:, u0 * 8 * UNIT_G : (u0 + 1) * 8 * UNIT_G]
+                    for u1 in range(2):
+                        nc.gpsimd.tensor_tensor(
+                            out=pool_b[:, u1 * 4 * UNIT_G : (u1 + 1) * 4 * UNIT_G],
+                            in0=half[:, 0 : 4 * UNIT_G],
+                            in1=half[:, 4 * UNIT_G : 8 * UNIT_G],
+                            op=SIGN_OP[u1],
                         )
-                        multiply(number - 2)
-                        for v0 in range(2):
-                            open_leaf(number + v0, SIDE * u + 2 * v1 + v0)
-                        for v0 in range(2):
-                            sums = leaf.tile([PARTS, PACK, K_VECTOR], BF16, name="sums")
-                            nc.vector.tensor_tensor(
-                                out=sums[:], in0=level3[:, :, 0, :], in1=level3[:, :, 1, :], op=SIGN_OP[v0]
+                    b_view = pool_b[:].rearrange("n (u q1 x) -> n u q1 x", u=2, q1=2)
+                    a_view = half.rearrange("n (u v x) -> n u v x", u=2, v=2)
+                    for v1 in range(2):
+                        nc.gpsimd.tensor_tensor(
+                            out=a_view[:, :, v1, :], in0=b_view[:, :, 0, :], in1=b_view[:, :, 1, :], op=SIGN_OP[v1]
+                        )
+                    a_pairs = half.rearrange("n (u v q0 x) -> n u v q0 x", u=2, v=2, q0=2)
+                    for v0 in range(2):
+                        nc.gpsimd.tensor_tensor(
+                            out=side_by_bits[:, :, u0, :, v0, :],
+                            in0=a_pairs[:, :, :, 0, :],
+                            in1=a_pairs[:, :, :, 1, :],
+                            op=SIGN_OP[v0],
+                        )
+
+                pixels_of = {}
+
+                def pixels_to_partitions(o):
+                    def chore():
+                        pix_ps = psum_pe.tile([PARTS, PACK, PARTS], BF16, name="pix_ps")
+                        for r in range(PACK):
+                            nc.tensor.transpose(
+                                out=pix_ps[:, r, :],
+                                in_=picked[:, r, o, :, :].rearrange("n a e -> n (a e)"),
+                                identity=ident[:],
                             )
-                            nc.scalar.activation(
-                                out=gy_of[number + v0][:, K_TENSOR:K, :],
-                                in_=sums[:].rearrange("n r k -> n k r"),
-                                func=COPY,
-                                scale=1.0 / T,
+                        pixels = pixel_pool.tile([PARTS, PACK, PARTS], BF16, name="pixels")
+                        nc.scalar.copy(out=pixels[:], in_=pix_ps[:])
+                        pixels_of[o] = pixels
+
+                    return chore
+
+                def transform(o):
+                    def chore():
+                        coef_ps = psum_pe.tile([PARTS, PACK, PARTS], F32, name="coef_ps")
+                        for r in range(PACK):
+                            nc.tensor.matmul(
+                                out=coef_ps[:, r, :], lhsT=pixels_of[o][:, r, :], rhs=matrix[:], start=True, stop=True
                             )
-                        multiply(number - 1)
-                        store(number - 2, False)
-                        store(number - 1, False)
-                        number += 2
-            multiply(number - 2)
-            multiply(number - 1)
-            store(number - 2, True)
-            store(number - 1, True)
+                        nc.scalar.copy(
+                            out=side[:, 0, :, o * OCTET * PACK : (o + 1) * OCTET * PACK].rearrange(
+                                "n t (e r) -> n t e r", r=PACK
+                            ),
+                            in_=coef_ps[:].rearrange("n r (t e) -> n t e r", e=OCTET),
+                        )
+
+                    return chore
+
+                step = level1_jobs + 3
+                for o in range(OCTETS + 1):
+                    if o < OCTETS:
+                        add_chore(step + 2 * o, pixels_to_partitions(o))
+                    if o >= 1:
+                        add_chore(step + 2 * o + 1, transform(o - 1))
+                for i in range(2):
+                    for v in range(SIDE):
+                        add_chore(step + 27 + 4 * i + v, regroup_x(u_order[i], v))
+
+                run_steps(level1_jobs + 3, len(jobs) + 3)
+
+            with tc.tile_pool(name="leaf", bufs=3) as leaf, tc.tile_pool(name="flow", bufs=2) as flow, tc.psum_pool(
+                name="acc_pool", bufs=4
+            ) as acc_pool:
+                pairs = [(u0, u1, v1) for u0 in range(2) for u1 in range(2) for v1 in range(2)]
+                gy_of = {}
+                banks_of = {}
+
+                def first_t(m):
+                    u0, u1, v1 = pairs[m]
+                    return SIDE * (2 * u1 + u0) + 2 * v1
+
+                def sums(m):
+                    u0, u1, v1 = pairs[m]
+                    gy = leaf.tile([PARTS, 2, K * PACK], BF16, name="gy", align_bytes=64)
+                    nc.scalar.copy(
+                        out=gy[:, :, 0 : K_SIDE * PACK].rearrange("n v (s x) -> n v s x", s=2),
+                        in_=side[:, :, first_t(m) : first_t(m) + 2, :].rearrange("n s v x -> n v s x"),
+                    )
+                    a0 = (((2 * v1) * 2 + u1) * 2 + u0) * UNIT
+                    b0 = (((2 * v1 + 1) * 2 + u1) * 2 + u0) * UNIT
+                    for v0 in range(2):
+                        nc.vector.tensor_tensor(
+                            out=gy[:, v0, K_SIDE * PACK : K * PACK],
+                            in0=work[:, a0 : a0 + UNIT],
+                            in1=work[:, b0 : b0 + UNIT],
+                            op=SIGN_OP[v0],
+                        )
+                    gy_of[m] = gy
+
+                def multiply(m):
+                    u = first_t(m) // SIDE
+                    if u not in x_codes_of:
+                        x_codes = flow.tile([PARTS, SIDE * C], U32, name="x_codes", align_bytes=64)
+                        x_scales = flow.tile([PARTS, SIDE * C], U8, name="x_scales", align_bytes=64)
+                        nc.vector.quantize_mx(
+                            out=x_codes[:].bitcast(E4M3_X4),
+                            scales=x_scales[:],
+                            in_=x_of[u][:].rearrange("n v c r -> n (v c r)"),
+                        )
+                        x_codes_of[u] = (x_codes, x_scales)
+                    x_codes, x_scales = x_codes_of[u]
+                    gy_codes = flow.tile([PARTS, 2 * K], U32, name="gy_codes", align_bytes=64)
+                    gy_scales = flow.tile([PARTS, 2 * K], U8, name="gy_scales", align_bytes=64)
+                    nc.vector.quantize_mx(
+                        out=gy_codes[:].bitcast(E5M2_X4),
+                        scales=gy_scales[:],
+                        in_=gy_of[m][:].rearrange("n v x -> n (v x)"),
+                    )
+                    banks = []
+                    for v0 in range(2):
+                        v = (first_t(m) + v0) % SIDE
+                        for h in range(C_HALVES):
+                            column = v * C + h * PARTS
+                            acc = acc_pool.tile([PARTS, K], F32, name="acc")
+                            nc.tensor.matmul_mx(
+                                out=acc[:],
+                                lhsT=x_codes[:, column : column + PARTS].bitcast(E4M3_X4),
+                                lhsT_scale=x_scales[:, column : column + PARTS],
+                                rhs=gy_codes[:, v0 * K : (v0 + 1) * K].bitcast(E5M2_X4),
+                                rhs_scale=gy_scales[:, v0 * K : (v0 + 1) * K],
+                                start=True,
+                                stop=True,
+                            )
+                            banks.append(acc)
+                    banks_of[m] = banks
+
+                def store(m, vector_helps):
+                    for v0 in range(2):
+                        result = flow.tile([PARTS, C_HALVES, K], F32, name="result")
+                        for h in range(C_HALVES):
+                            bank = banks_of[m][v0 * C_HALVES + h]
+                            if vector_helps and h == 1:
+                                nc.vector.tensor_scalar(
+                                    out=result[:, h, :], in0=bank[:], scalar1=1.0 / T, scalar2=None,
+                                    op0=mybir.AluOpType.mult,
+                                )
+                            else:
+                                nc.scalar.activation(out=result[:, h, :], in_=bank[:], func=COPY, scale=1.0 / T)
+                        nc.scalar.dma_start(out=out_dram[first_t(m) + v0], in_=result[:])
+
+                count = len(pairs)
+                for m in range(count + 2):
+                    if m < count:
+                        sums(m)
+                    if 0 <= m - 2:
+                        store(m - 2, m - 2 >= count - 1)
+                    if 0 <= m - 1 < count:
+                        multiply(m - 1)
+                    if m in (1, 3):
+                        late = u_order[(m + 3) // 2]
+                        load_x(late)
+                        for v in range(SIDE):
+                            regroup_x(late, v)()

@@ -62,7 +62,9 @@ def tile_iwht3layer_pa_kernel(tc, trans, weight, bias, grad_out, out):
 
     with tc.tile_pool(name="keep", bufs=1) as keep, tc.tile_pool(name="turned", bufs=3) as turned, tc.tile_pool(
         name="pixel_pool", bufs=2
-    ) as pixel_pool, tc.psum_pool(name="psum_t", bufs=2) as psum_t, tc.psum_pool(
+    ) as pixel_pool, tc.tile_pool(name="x_pool", bufs=2) as x_pool, tc.tile_pool(
+        name="overlay", bufs=1
+    ) as overlay, tc.psum_pool(name="psum_t", bufs=2) as psum_t, tc.psum_pool(
         name="psum_a", bufs=2
     ) as psum_a, tc.manual_schedule():
         ident = keep.tile([PARTS, PARTS], BF16, name="ident")
@@ -74,9 +76,8 @@ def tile_iwht3layer_pa_kernel(tc, trans, weight, bias, grad_out, out):
         matrix = transform_matrix(nc, keep, ident)
 
         work = keep.tile([PARTS, T * UNIT], F32, name="work")
-        pool_a = keep.tile([PARTS, T * UNIT_G], F32, name="pool_a")
-        picked = keep.tile([PARTS, PACK, OCTETS, T, OCTET], BF16, name="picked")
-        side = keep.tile([PARTS, 2, T, UNIT_G], BF16, name="side")
+        pool_a = overlay.tile([PARTS, T * UNIT_G], F32, name="pool_a", offset=65536)
+        picked = overlay.tile([PARTS, PACK, OCTETS, T, OCTET], BF16, name="picked", offset=90112)
 
         jobs = []
         st_of = {}
@@ -128,255 +129,292 @@ def tile_iwht3layer_pa_kernel(tc, trans, weight, bias, grad_out, out):
                 if 0 <= s - 3 < len(jobs):
                     jobs[s - 3][1](pa_of[s - 3])
 
-        with tc.tile_pool(name="g_pool", bufs=1) as g_pool:
-            g = {}
-            for q in range(SIDE):
-                for p in range(SIDE):
-                    g[q, p] = g_pool.tile([PARTS, PACK, K], BF16, name="g%d%d" % (q, p))
-                    for jh in range(2):
-                        nc.sync.dma_start(out=g[q, p][jh:PARTS:2, :, :], in_=g_dram[jh, p, q])
+        g = {}
+        for q in range(SIDE):
+            for p in range(SIDE):
+                g[q, p] = overlay.tile([PARTS, PACK, K], BF16, name="g%d%d" % (q, p), offset=(SIDE * q + p) * 4096)
+                for jh in range(2):
+                    nc.sync.dma_start(out=g[q, p][jh:PARTS:2, :, :], in_=g_dram[jh, p, q])
 
-            for q in range(SIDE):
-                for p1 in range(2):
-                    for u0 in range(2):
-                        start = ((u0 * 2 + p1) * SIDE + q) * UNIT_G
-                        nc.gpsimd.tensor_tensor(
-                            out=pool_a[:, start : start + UNIT_G].rearrange("n (k r) -> n k r", r=PACK),
-                            in0=g[q, 2 * p1][:, :, K_TENSOR:K_SIDE].rearrange("n r k -> n k r"),
-                            in1=g[q, 2 * p1 + 1][:, :, K_TENSOR:K_SIDE].rearrange("n r k -> n k r"),
-                            op=SIGN_OP[u0],
-                        )
+        x_raw_of = {}
+        x_of = {}
+        x_codes_of = {}
 
-            def level1(p1, q, source_from, k_from, k_to):
-                def consume(pa):
-                    first = pa[:].bitcast(BF16)[:, :, k_from - source_from : k_to - source_from].rearrange(
-                        "n r k -> n k r"
-                    )
-                    second = g[q, 2 * p1 + 1][:, :, k_from:k_to].rearrange("n r k -> n k r")
-                    for u0 in range(2):
-                        start = ((q * 2 + p1) * 2 + u0) * UNIT + (k_from - K_SIDE) * PACK
-                        nc.vector.tensor_tensor(
-                            out=work[:, start : start + (k_to - k_from) * PACK].rearrange(
-                                "n (k r) -> n k r", r=PACK
-                            ),
-                            in0=first,
-                            in1=second,
-                            op=SIGN_OP[u0],
-                        )
+        def load_x(u):
+            x_raw = x_pool.tile([PARTS, SIDE, PACK, C], BF16, name="x_raw")
+            nc.sync.dma_start(out=x_raw[:].rearrange("n v r c -> n v (r c)"), in_=x_dram[u])
+            x_raw_of[u] = x_raw
 
-                return consume
+        def regroup_x(u, half):
+            def chore():
+                nc.scalar.copy(
+                    out=x_of[u][:, 2 * half : 2 * half + 2],
+                    in_=x_raw_of[u][:, 2 * half : 2 * half + 2].rearrange("n v r c -> n v c r"),
+                )
 
-            def pick(q, p):
-                def chore():
-                    nc.scalar.copy(
-                        out=picked[:, :, :, SIDE * p + q, :],
-                        in_=g[q, p][:, :, 0:K_TENSOR].rearrange("n r (o e) -> n r o e", e=OCTET),
-                    )
+            return chore
 
-                return chore
+        load_x(u_order[0])
+        load_x(u_order[1])
 
-            for q in range(SIDE):
-                for p1 in range(2):
-                    for source_from, k_from, k_to in ((K_SIDE, K_SIDE, K_SIDE + 256), (K - 256, K_SIDE + 256, K)):
-                        sources = [
-                            g[q, 2 * p1][:, r, source_from : source_from + 256].bitcast(F32) for r in range(PACK)
-                        ]
-                        jobs.append((sources, level1(p1, q, source_from, k_from, k_to)))
-                for p in range(SIDE):
-                    add_chore(len(jobs) - 1 + p, pick(q, p))
-            level1_jobs = len(jobs)
-
-            for q in range(SIDE):
-                for c in range(2 * UNIT // CHUNK):
-                    chunk_job(q * 4 * UNIT + c * CHUNK, (q * 4 + 2) * UNIT + c * CHUNK)
-            for c in range(8 * UNIT // CHUNK):
-                chunk_job(c * CHUNK, 8 * UNIT + c * CHUNK)
-
-            run_steps(0, level1_jobs + 3)
-
-        with tc.tile_pool(name="x_pool", bufs=2) as x_pool:
-            x_raw_of = {}
-            x_of = {}
-            x_codes_of = {}
-
-            def load_x(u):
-                x_raw = x_pool.tile([PARTS, SIDE, PACK, C], BF16, name="x_raw")
-                nc.sync.dma_start(out=x_raw[:].rearrange("n v r c -> n v (r c)"), in_=x_dram[u])
-                x_raw_of[u] = x_raw
-
-            def regroup_x(u, v):
-                def chore():
-                    if v == 0:
-                        x_of[u] = x_pool.tile([PARTS, SIDE, C, PACK], BF16, name="x", align_bytes=64)
-                    nc.scalar.copy(out=x_of[u][:, v], in_=x_raw_of[u][:, v].rearrange("n r c -> n c r"))
-
-                return chore
-
-            load_x(u_order[0])
-            load_x(u_order[1])
-
-            with tc.tile_pool(name="pool_pool", bufs=1) as pool_pool, tc.psum_pool(name="psum_pe", bufs=2) as psum_pe:
-                pool_b = pool_pool.tile([PARTS, 8 * UNIT_G], F32, name="pool_b")
-                side_by_bits = side[:, 1].rearrange("n (u1 u0 v1 v0) x -> n u1 u0 v1 v0 x", u1=2, u0=2, v1=2)
+        for q in range(SIDE):
+            for p1 in range(2):
                 for u0 in range(2):
-                    half = pool_a[:, u0 * 8 * UNIT_G : (u0 + 1) * 8 * UNIT_G]
-                    for u1 in range(2):
-                        nc.gpsimd.tensor_tensor(
-                            out=pool_b[:, u1 * 4 * UNIT_G : (u1 + 1) * 4 * UNIT_G],
-                            in0=half[:, 0 : 4 * UNIT_G],
-                            in1=half[:, 4 * UNIT_G : 8 * UNIT_G],
-                            op=SIGN_OP[u1],
-                        )
-                    b_view = pool_b[:].rearrange("n (u q1 x) -> n u q1 x", u=2, q1=2)
-                    a_view = half.rearrange("n (u v x) -> n u v x", u=2, v=2)
-                    for v1 in range(2):
-                        nc.gpsimd.tensor_tensor(
-                            out=a_view[:, :, v1, :], in0=b_view[:, :, 0, :], in1=b_view[:, :, 1, :], op=SIGN_OP[v1]
-                        )
-                    a_pairs = half.rearrange("n (u v q0 x) -> n u v q0 x", u=2, v=2, q0=2)
-                    for v0 in range(2):
-                        nc.gpsimd.tensor_tensor(
-                            out=side_by_bits[:, :, u0, :, v0, :],
-                            in0=a_pairs[:, :, :, 0, :],
-                            in1=a_pairs[:, :, :, 1, :],
-                            op=SIGN_OP[v0],
-                        )
+                    start = ((u0 * 2 + p1) * SIDE + q) * UNIT_G
+                    nc.gpsimd.tensor_tensor(
+                        out=pool_a[:, start : start + UNIT_G].rearrange("n (k r) -> n k r", r=PACK),
+                        in0=g[q, 2 * p1][:, :, K_TENSOR:K_SIDE].rearrange("n r k -> n k r"),
+                        in1=g[q, 2 * p1 + 1][:, :, K_TENSOR:K_SIDE].rearrange("n r k -> n k r"),
+                        op=SIGN_OP[u0],
+                    )
 
-                pixels_of = {}
+        def level1(p1, q, source_from, k_from, k_to):
+            def consume(pa):
+                first = pa[:].bitcast(BF16)[:, :, k_from - source_from : k_to - source_from].rearrange(
+                    "n r k -> n k r"
+                )
+                second = g[q, 2 * p1 + 1][:, :, k_from:k_to].rearrange("n r k -> n k r")
+                for u0 in range(2):
+                    start = ((q * 2 + p1) * 2 + u0) * UNIT + (k_from - K_SIDE) * PACK
+                    nc.vector.tensor_tensor(
+                        out=work[:, start : start + (k_to - k_from) * PACK].rearrange("n (k r) -> n k r", r=PACK),
+                        in0=first,
+                        in1=second,
+                        op=SIGN_OP[u0],
+                    )
 
-                def pixels_to_partitions(o):
-                    def chore():
-                        pix_ps = psum_pe.tile([PARTS, PACK, PARTS], BF16, name="pix_ps")
+            return consume
+
+        def pick(q, p):
+            def chore():
+                nc.scalar.copy(
+                    out=picked[:, :, :, SIDE * p + q, :],
+                    in_=g[q, p][:, :, 0:K_TENSOR].rearrange("n r (o e) -> n r o e", e=OCTET),
+                )
+
+            return chore
+
+        for q in range(SIDE):
+            for p1 in range(2):
+                for source_from, k_from, k_to in ((K_SIDE, K_SIDE, K_SIDE + 256), (K - 256, K_SIDE + 256, K)):
+                    sources = [g[q, 2 * p1][:, r, source_from : source_from + 256].bitcast(F32) for r in range(PACK)]
+                    jobs.append((sources, level1(p1, q, source_from, k_from, k_to)))
+            for p in range(SIDE):
+                add_chore(len(jobs) - 1 + p, pick(q, p))
+        level1_jobs = len(jobs)
+
+        for q in range(SIDE):
+            for c in range(2 * UNIT // CHUNK):
+                chunk_job(q * 4 * UNIT + c * CHUNK, (q * 4 + 2) * UNIT + c * CHUNK)
+        for c in range(8 * UNIT // CHUNK):
+            chunk_job(c * CHUNK, 8 * UNIT + c * CHUNK)
+
+        step = level1_jobs + 3
+        run_steps(0, step)
+
+        gy_all = overlay.tile([PARTS, T, K * PACK], BF16, name="gy_all", offset=0, align_bytes=64)
+        gy_by_bits = gy_all[:].rearrange("n (u1 u0 v1 v0) x -> n u1 u0 v1 v0 x", u1=2, u0=2, v1=2)
+
+        x_of[u_order[0]] = x_pool.tile([PARTS, SIDE, C, PACK], BF16, name="x", align_bytes=64)
+        nc.gpsimd.tensor_scalar(
+            out=x_of[u_order[0]][:],
+            in0=x_raw_of[u_order[0]][:].rearrange("n v r c -> n v c r"),
+            scalar1=1.0,
+            scalar2=0.0,
+            op0=mybir.AluOpType.mult,
+            op1=mybir.AluOpType.add,
+        )
+        load_x(u_order[2])
+        pool_b = overlay.tile([PARTS, 8 * UNIT_G], F32, name="pool_b", offset=102400)
+        for u0 in range(2):
+            half = pool_a[:, u0 * 8 * UNIT_G : (u0 + 1) * 8 * UNIT_G]
+            for u1 in range(2):
+                nc.gpsimd.tensor_tensor(
+                    out=pool_b[:, u1 * 4 * UNIT_G : (u1 + 1) * 4 * UNIT_G],
+                    in0=half[:, 0 : 4 * UNIT_G],
+                    in1=half[:, 4 * UNIT_G : 8 * UNIT_G],
+                    op=SIGN_OP[u1],
+                )
+            b_view = pool_b[:].rearrange("n (u q1 x) -> n u q1 x", u=2, q1=2)
+            a_view = half.rearrange("n (u v x) -> n u v x", u=2, v=2)
+            for v1 in range(2):
+                nc.gpsimd.tensor_tensor(
+                    out=a_view[:, :, v1, :], in0=b_view[:, :, 0, :], in1=b_view[:, :, 1, :], op=SIGN_OP[v1]
+                )
+
+        with tc.psum_pool(name="psum_pe", bufs=2) as psum_pe:
+            pixels_of = {}
+
+            def pixels_to_partitions(o2):
+                def chore():
+                    pix_ps = psum_pe.tile([PARTS, 2, PACK, PARTS], BF16, name="pix_ps")
+                    for i in range(2):
                         for r in range(PACK):
                             nc.tensor.transpose(
-                                out=pix_ps[:, r, :],
-                                in_=picked[:, r, o, :, :].rearrange("n a e -> n (a e)"),
+                                out=pix_ps[:, i, r, :],
+                                in_=picked[:, r, 2 * o2 + i, :, :].rearrange("n a e -> n (a e)"),
                                 identity=ident[:],
                             )
-                        pixels = pixel_pool.tile([PARTS, PACK, PARTS], BF16, name="pixels")
-                        nc.scalar.copy(out=pixels[:], in_=pix_ps[:])
-                        pixels_of[o] = pixels
+                    pixels = pixel_pool.tile([PARTS, 2, PACK, PARTS], BF16, name="pixels")
+                    nc.scalar.copy(out=pixels[:], in_=pix_ps[:])
+                    pixels_of[o2] = pixels
 
-                    return chore
+                return chore
 
-                def transform(o):
-                    def chore():
-                        coef_ps = psum_pe.tile([PARTS, PACK, PARTS], F32, name="coef_ps")
-                        for r in range(PACK):
-                            nc.tensor.matmul(
-                                out=coef_ps[:, r, :], lhsT=pixels_of[o][:, r, :], rhs=matrix[:], start=True, stop=True
-                            )
-                        nc.scalar.copy(
-                            out=side[:, 0, :, o * OCTET * PACK : (o + 1) * OCTET * PACK].rearrange(
-                                "n t (e r) -> n t e r", r=PACK
-                            ),
-                            in_=coef_ps[:].rearrange("n r (t e) -> n t e r", e=OCTET),
+            def transform(o):
+                def chore():
+                    coef_ps = psum_pe.tile([PARTS, PACK, PARTS], F32, name="coef_ps")
+                    for r in range(PACK):
+                        nc.tensor.matmul(
+                            out=coef_ps[:, r, :],
+                            lhsT=pixels_of[o // 2][:, o % 2, r, :],
+                            rhs=matrix[:],
+                            start=True,
+                            stop=True,
                         )
-
-                    return chore
-
-                step = level1_jobs + 3
-                for o in range(OCTETS + 1):
-                    if o < OCTETS:
-                        add_chore(step + 2 * o, pixels_to_partitions(o))
-                    if o >= 1:
-                        add_chore(step + 2 * o + 1, transform(o - 1))
-                for i in range(2):
-                    for v in range(SIDE):
-                        add_chore(step + 27 + 4 * i + v, regroup_x(u_order[i], v))
-
-                run_steps(level1_jobs + 3, len(jobs) + 3)
-
-            with tc.tile_pool(name="leaf", bufs=3) as leaf, tc.tile_pool(name="flow", bufs=2) as flow, tc.psum_pool(
-                name="acc_pool", bufs=4
-            ) as acc_pool:
-                pairs = [(u0, u1, v1) for u0 in range(2) for u1 in range(2) for v1 in range(2)]
-                gy_of = {}
-                banks_of = {}
-
-                def first_t(m):
-                    u0, u1, v1 = pairs[m]
-                    return SIDE * (2 * u1 + u0) + 2 * v1
-
-                def sums(m):
-                    u0, u1, v1 = pairs[m]
-                    gy = leaf.tile([PARTS, 2, K * PACK], BF16, name="gy", align_bytes=64)
                     nc.scalar.copy(
-                        out=gy[:, :, 0 : K_SIDE * PACK].rearrange("n v (s x) -> n v s x", s=2),
-                        in_=side[:, :, first_t(m) : first_t(m) + 2, :].rearrange("n s v x -> n v s x"),
+                        out=gy_all[:, :, o * OCTET * PACK : (o + 1) * OCTET * PACK].rearrange(
+                            "n t (e r) -> n t e r", r=PACK
+                        ),
+                        in_=coef_ps[:].rearrange("n r (t e) -> n t e r", e=OCTET),
                     )
-                    a0 = (((2 * v1) * 2 + u1) * 2 + u0) * UNIT
-                    b0 = (((2 * v1 + 1) * 2 + u1) * 2 + u0) * UNIT
-                    for v0 in range(2):
-                        nc.vector.tensor_tensor(
-                            out=gy[:, v0, K_SIDE * PACK : K * PACK],
-                            in0=work[:, a0 : a0 + UNIT],
-                            in1=work[:, b0 : b0 + UNIT],
-                            op=SIGN_OP[v0],
-                        )
-                    gy_of[m] = gy
 
-                def multiply(m):
-                    u = first_t(m) // SIDE
-                    if u not in x_codes_of:
-                        x_codes = flow.tile([PARTS, SIDE * C], U32, name="x_codes", align_bytes=64)
-                        x_scales = flow.tile([PARTS, SIDE * C], U8, name="x_scales", align_bytes=64)
-                        nc.vector.quantize_mx(
-                            out=x_codes[:].bitcast(E4M3_X4),
-                            scales=x_scales[:],
-                            in_=x_of[u][:].rearrange("n v c r -> n (v c r)"),
-                        )
-                        x_codes_of[u] = (x_codes, x_scales)
-                    x_codes, x_scales = x_codes_of[u]
-                    gy_codes = flow.tile([PARTS, 2 * K], U32, name="gy_codes", align_bytes=64)
-                    gy_scales = flow.tile([PARTS, 2 * K], U8, name="gy_scales", align_bytes=64)
+                return chore
+
+            at = step
+            add_chore(at, pixels_to_partitions(0))
+            for o2 in range(OCTETS // 2):
+                if o2 + 1 < OCTETS // 2:
+                    add_chore(at + 1, pixels_to_partitions(o2 + 1))
+                add_chore(at + 2, transform(2 * o2))
+                add_chore(at + 3, transform(2 * o2 + 1))
+                at += 3
+            path_end = at + 1
+
+            def open_x(u, pool_tile):
+                def chore():
+                    x_of[u] = pool_tile()
+
+                return chore
+
+            add_chore(path_end, open_x(u_order[1], lambda: x_pool.tile([PARTS, SIDE, C, PACK], BF16, name="x", align_bytes=64)))
+            add_chore(path_end, regroup_x(u_order[1], 0))
+            add_chore(path_end + 3, regroup_x(u_order[1], 1))
+            add_chore(path_end + 3, lambda: load_x(u_order[3]))
+
+            run_steps(step, path_end)
+
+        for u0 in range(2):
+            a_pairs = pool_a[:, u0 * 8 * UNIT_G : (u0 + 1) * 8 * UNIT_G].rearrange(
+                "n (u v q0 x) -> n u v q0 x", u=2, v=2, q0=2
+            )
+            for v0 in range(2):
+                nc.gpsimd.tensor_tensor(
+                    out=gy_by_bits[:, :, u0, :, v0, K_TENSOR * PACK : K_SIDE * PACK],
+                    in0=a_pairs[:, :, :, 0, :],
+                    in1=a_pairs[:, :, :, 1, :],
+                    op=SIGN_OP[v0],
+                )
+
+        add_chore(
+            path_end + 8,
+            open_x(
+                u_order[2],
+                lambda: overlay.tile([PARTS, SIDE, C, PACK], BF16, name="x_third", offset=98304, align_bytes=64),
+            ),
+        )
+        add_chore(path_end + 8, regroup_x(u_order[2], 0))
+        add_chore(path_end + 11, regroup_x(u_order[2], 1))
+        run_steps(path_end, len(jobs) + 3)
+
+        with tc.psum_pool(name="acc_pool", bufs=4) as acc_pool:
+            pairs = [(u0, u1, v1) for u0 in range(2) for u1 in range(2) for v1 in range(2)]
+            banks_of = {}
+
+            def first_t(m):
+                u0, u1, v1 = pairs[m]
+                return SIDE * (2 * u1 + u0) + 2 * v1
+
+            def sums(m):
+                u0, u1, v1 = pairs[m]
+                a0 = (((2 * v1) * 2 + u1) * 2 + u0) * UNIT
+                b0 = (((2 * v1 + 1) * 2 + u1) * 2 + u0) * UNIT
+                for v0 in range(2):
+                    nc.vector.tensor_tensor(
+                        out=gy_all[:, first_t(m) + v0, K_SIDE * PACK : K * PACK],
+                        in0=work[:, a0 : a0 + UNIT],
+                        in1=work[:, b0 : b0 + UNIT],
+                        op=SIGN_OP[v0],
+                    )
+
+            def multiply(m):
+                u = first_t(m) // SIDE
+                if u not in x_codes_of:
+                    x_codes = overlay.tile(
+                        [PARTS, SIDE * C], U32, name="x_codes", bufs=2, offset=65536, align_bytes=64
+                    )
+                    x_scales = overlay.tile(
+                        [PARTS, SIDE * C], U8, name="x_scales", bufs=2, offset=73728, align_bytes=64
+                    )
                     nc.vector.quantize_mx(
-                        out=gy_codes[:].bitcast(E5M2_X4),
-                        scales=gy_scales[:],
-                        in_=gy_of[m][:].rearrange("n v x -> n (v x)"),
+                        out=x_codes[:].bitcast(E4M3_X4),
+                        scales=x_scales[:],
+                        in_=x_of[u][:].rearrange("n v c r -> n (v c r)"),
                     )
-                    banks = []
-                    for v0 in range(2):
-                        v = (first_t(m) + v0) % SIDE
-                        for h in range(C_HALVES):
-                            column = v * C + h * PARTS
-                            acc = acc_pool.tile([PARTS, K], F32, name="acc")
-                            nc.tensor.matmul_mx(
-                                out=acc[:],
-                                lhsT=x_codes[:, column : column + PARTS].bitcast(E4M3_X4),
-                                lhsT_scale=x_scales[:, column : column + PARTS],
-                                rhs=gy_codes[:, v0 * K : (v0 + 1) * K].bitcast(E5M2_X4),
-                                rhs_scale=gy_scales[:, v0 * K : (v0 + 1) * K],
-                                start=True,
-                                stop=True,
+                    x_codes_of[u] = (x_codes, x_scales)
+                x_codes, x_scales = x_codes_of[u]
+                gy_codes = overlay.tile([PARTS, 2 * K], U32, name="gy_codes", bufs=2, offset=75776, align_bytes=64)
+                gy_scales = overlay.tile([PARTS, 2 * K], U8, name="gy_scales", bufs=2, offset=83968, align_bytes=64)
+                nc.vector.quantize_mx(
+                    out=gy_codes[:].bitcast(E5M2_X4),
+                    scales=gy_scales[:],
+                    in_=gy_all[:, first_t(m) : first_t(m) + 2, :].rearrange("n v x -> n (v x)"),
+                )
+                banks = []
+                for v0 in range(2):
+                    v = (first_t(m) + v0) % SIDE
+                    for h in range(C_HALVES):
+                        column = v * C + h * PARTS
+                        acc = acc_pool.tile([PARTS, K], F32, name="acc")
+                        nc.tensor.matmul_mx(
+                            out=acc[:],
+                            lhsT=x_codes[:, column : column + PARTS].bitcast(E4M3_X4),
+                            lhsT_scale=x_scales[:, column : column + PARTS],
+                            rhs=gy_codes[:, v0 * K : (v0 + 1) * K].bitcast(E5M2_X4),
+                            rhs_scale=gy_scales[:, v0 * K : (v0 + 1) * K],
+                            start=True,
+                            stop=True,
+                        )
+                        banks.append(acc)
+                banks_of[m] = banks
+
+            def store(m, vector_helps):
+                for v0 in range(2):
+                    result = overlay.tile([PARTS, C_HALVES, K], F32, name="result", bufs=3, offset=86016)
+                    for h in range(C_HALVES):
+                        bank = banks_of[m][v0 * C_HALVES + h]
+                        if vector_helps and h == 1:
+                            nc.vector.tensor_scalar(
+                                out=result[:, h, :],
+                                in0=bank[:],
+                                scalar1=1.0 / T,
+                                scalar2=None,
+                                op0=mybir.AluOpType.mult,
                             )
-                            banks.append(acc)
-                    banks_of[m] = banks
+                        else:
+                            nc.scalar.activation(out=result[:, h, :], in_=bank[:], func=COPY, scale=1.0 / T)
+                    nc.sync.dma_start(out=out_dram[first_t(m) + v0], in_=result[:])
 
-                def store(m, vector_helps):
-                    for v0 in range(2):
-                        result = flow.tile([PARTS, C_HALVES, K], F32, name="result")
-                        for h in range(C_HALVES):
-                            bank = banks_of[m][v0 * C_HALVES + h]
-                            if vector_helps and h == 1:
-                                nc.vector.tensor_scalar(
-                                    out=result[:, h, :], in0=bank[:], scalar1=1.0 / T, scalar2=None,
-                                    op0=mybir.AluOpType.mult,
-                                )
-                            else:
-                                nc.scalar.activation(out=result[:, h, :], in_=bank[:], func=COPY, scale=1.0 / T)
-                        nc.scalar.dma_start(out=out_dram[first_t(m) + v0], in_=result[:])
-
-                count = len(pairs)
-                for m in range(count + 2):
-                    if m < count:
-                        sums(m)
-                    if 0 <= m - 2:
-                        store(m - 2, m - 2 >= count - 1)
-                    if 0 <= m - 1 < count:
-                        multiply(m - 1)
-                    if m in (1, 3):
-                        late = u_order[(m + 3) // 2]
-                        load_x(late)
-                        for v in range(SIDE):
-                            regroup_x(late, v)()
+            count = len(pairs)
+            for m in range(count + 2):
+                if m < count:
+                    sums(m)
+                if 0 <= m - 2:
+                    store(m - 2, m - 2 >= count - 1)
+                if 0 <= m - 1 < count:
+                    multiply(m - 1)
+                if m == 1:
+                    x_of[u_order[3]] = x_pool.tile([PARTS, SIDE, C, PACK], BF16, name="x", align_bytes=64)
+                    regroup_x(u_order[3], 0)()
+                if m == 2:
+                    regroup_x(u_order[3], 1)()

@@ -162,22 +162,24 @@ def tile_iwht3layer_pa_kernel(tc, trans, weight, bias, grad_out, out):
                 for u0 in range(2):
                     start = ((u0 * 2 + p1) * SIDE + q) * UNIT_G
                     nc.gpsimd.tensor_tensor(
-                        out=pool_a[:, start : start + UNIT_G].rearrange("n (k r) -> n k r", r=PACK),
-                        in0=g[q, 2 * p1][:, :, K_TENSOR:K_SIDE].rearrange("n r k -> n k r"),
-                        in1=g[q, 2 * p1 + 1][:, :, K_TENSOR:K_SIDE].rearrange("n r k -> n k r"),
+                        out=pool_a[:, start : start + UNIT_G].rearrange("n (r1 k r0) -> n r1 k r0", r1=2, r0=2),
+                        in0=g[q, 2 * p1][:, :, K_TENSOR:K_SIDE].rearrange("n (r1 r0) k -> n r1 k r0", r0=2),
+                        in1=g[q, 2 * p1 + 1][:, :, K_TENSOR:K_SIDE].rearrange("n (r1 r0) k -> n r1 k r0", r0=2),
                         op=SIGN_OP[u0],
                     )
 
         def level1(p1, q, source_from, k_from, k_to):
             def consume(pa):
                 first = pa[:].bitcast(BF16)[:, :, k_from - source_from : k_to - source_from].rearrange(
-                    "n r k -> n k r"
+                    "n (r1 r0) k -> n r1 k r0", r0=2
                 )
-                second = g[q, 2 * p1 + 1][:, :, k_from:k_to].rearrange("n r k -> n k r")
+                second = g[q, 2 * p1 + 1][:, :, k_from:k_to].rearrange("n (r1 r0) k -> n r1 k r0", r0=2)
                 for u0 in range(2):
-                    start = ((q * 2 + p1) * 2 + u0) * UNIT + (k_from - K_SIDE) * PACK
+                    start = ((q * 2 + p1) * 2 + u0) * UNIT
                     nc.vector.tensor_tensor(
-                        out=work[:, start : start + (k_to - k_from) * PACK].rearrange("n (k r) -> n k r", r=PACK),
+                        out=work[:, start : start + UNIT].rearrange("n (r1 k r0) -> n r1 k r0", r1=2, r0=2)[
+                            :, :, k_from - K_SIDE : k_to - K_SIDE, :
+                        ],
                         in0=first,
                         in1=second,
                         op=SIGN_OP[u0],
@@ -308,13 +310,17 @@ def tile_iwht3layer_pa_kernel(tc, trans, weight, bias, grad_out, out):
             a_pairs = pool_a[:, u0 * 8 * UNIT_G : (u0 + 1) * 8 * UNIT_G].rearrange(
                 "n (u v q0 x) -> n u v q0 x", u=2, v=2, q0=2
             )
-            for v0 in range(2):
-                nc.gpsimd.tensor_tensor(
-                    out=gy_by_bits[:, :, u0, :, v0, K_TENSOR * PACK : K_SIDE * PACK],
-                    in0=a_pairs[:, :, :, 0, :],
-                    in1=a_pairs[:, :, :, 1, :],
-                    op=SIGN_OP[v0],
-                )
+            for u1 in range(2):
+                for v1 in range(2):
+                    for v0 in range(2):
+                        nc.gpsimd.tensor_tensor(
+                            out=gy_by_bits[:, u1, u0, v1, v0, K_TENSOR * PACK : K_SIDE * PACK].rearrange(
+                                "n (k r1 r0) -> n k r1 r0", r1=2, r0=2
+                            ),
+                            in0=a_pairs[:, u1, v1, 0, :].rearrange("n (r1 k r0) -> n k r1 r0", r1=2, r0=2),
+                            in1=a_pairs[:, u1, v1, 1, :].rearrange("n (r1 k r0) -> n k r1 r0", r1=2, r0=2),
+                            op=SIGN_OP[v0],
+                        )
 
         add_chore(
             path_end + 8,
@@ -341,9 +347,11 @@ def tile_iwht3layer_pa_kernel(tc, trans, weight, bias, grad_out, out):
                 b0 = (((2 * v1 + 1) * 2 + u1) * 2 + u0) * UNIT
                 for v0 in range(2):
                     nc.vector.tensor_tensor(
-                        out=gy_all[:, first_t(m) + v0, K_SIDE * PACK : K * PACK],
-                        in0=work[:, a0 : a0 + UNIT],
-                        in1=work[:, b0 : b0 + UNIT],
+                        out=gy_all[:, first_t(m) + v0, K_SIDE * PACK : K * PACK].rearrange(
+                            "n (k r1 r0) -> n k r1 r0", r1=2, r0=2
+                        ),
+                        in0=work[:, a0 : a0 + UNIT].rearrange("n (r1 k r0) -> n k r1 r0", r1=2, r0=2),
+                        in1=work[:, b0 : b0 + UNIT].rearrange("n (r1 k r0) -> n k r1 r0", r1=2, r0=2),
                         op=SIGN_OP[v0],
                     )
 

@@ -28,6 +28,7 @@ K_SIDE = K_TENSOR + K_POOL
 K_VECTOR = K - K_SIDE
 UNIT = K_VECTOR * PACK
 UNIT_G = K_POOL * PACK
+HALF = K_VECTOR * 2
 BLOCK = 128
 BLOCKS = 4
 CHUNK = BLOCK * BLOCKS
@@ -54,7 +55,7 @@ def transform_matrix(nc, pool, ident):
 def tile_iwht3layer_pa_kernel(tc, trans, weight, bias, grad_out, out):
     nc = tc.nc
 
-    g_dram = grad_out.rearrange("b (i p) (jh r q) k -> jh p q (b i) r k", p=SIDE, jh=2, r=PACK)
+    g_dram = grad_out.rearrange("b (i p) (jh r1 r0 q) k -> jh p r1 (b i) (r0 q k)", p=SIDE, jh=2, r1=2, r0=2)
     x_dram = trans.rearrange("(u v) b i (jh r) c -> u (b i jh) v (r c)", v=SIDE, r=PACK)
     out_dram = out.rearrange("t (h m) k -> t m h k", h=C_HALVES)
 
@@ -130,11 +131,15 @@ def tile_iwht3layer_pa_kernel(tc, trans, weight, bias, grad_out, out):
                     jobs[s - 3][1](pa_of[s - 3])
 
         g = {}
-        for q in range(SIDE):
+        for r1 in range(2):
             for p in range(SIDE):
-                g[q, p] = overlay.tile([PARTS, PACK, K], BF16, name="g%d%d" % (q, p), offset=(SIDE * q + p) * 4096)
+                g[p, r1] = overlay.tile(
+                    [PARTS, 2, SIDE, K], BF16, name="g%d%d" % (p, r1), offset=(SIDE * r1 + p) * 8192
+                )
                 for jh in range(2):
-                    nc.sync.dma_start(out=g[q, p][jh:PARTS:2, :, :], in_=g_dram[jh, p, q])
+                    nc.sync.dma_start(
+                        out=g[p, r1][jh:PARTS:2].rearrange("n r0 q k -> n (r0 q k)"), in_=g_dram[jh, p, r1]
+                    )
 
         x_raw_of = {}
         x_of = {}
@@ -157,29 +162,35 @@ def tile_iwht3layer_pa_kernel(tc, trans, weight, bias, grad_out, out):
         load_x(u_order[0])
         load_x(u_order[1])
 
-        for q in range(SIDE):
+        for r1 in range(2):
             for p1 in range(2):
                 for u0 in range(2):
-                    start = ((u0 * 2 + p1) * SIDE + q) * UNIT_G
+                    start = (u0 * 2 + p1) * SIDE * UNIT_G
                     nc.gpsimd.tensor_tensor(
-                        out=pool_a[:, start : start + UNIT_G].rearrange("n (r1 k r0) -> n r1 k r0", r1=2, r0=2),
-                        in0=g[q, 2 * p1][:, :, K_TENSOR:K_SIDE].rearrange("n (r1 r0) k -> n r1 k r0", r0=2),
-                        in1=g[q, 2 * p1 + 1][:, :, K_TENSOR:K_SIDE].rearrange("n (r1 r0) k -> n r1 k r0", r0=2),
+                        out=pool_a[:, start : start + SIDE * UNIT_G]
+                        .rearrange("n (q r1 x) -> n q r1 x", q=SIDE, r1=2)[:, :, r1, :]
+                        .rearrange("n q (k r0) -> n q k r0", r0=2),
+                        in0=g[2 * p1, r1][:, :, :, K_TENSOR:K_SIDE].rearrange("n r0 q k -> n q k r0"),
+                        in1=g[2 * p1 + 1, r1][:, :, :, K_TENSOR:K_SIDE].rearrange("n r0 q k -> n q k r0"),
                         op=SIGN_OP[u0],
                     )
 
-        def level1(p1, q, source_from, k_from, k_to):
+        def level1(r1, p1, pair, source_from, k_from, k_to):
             def consume(pa):
                 first = pa[:].bitcast(BF16)[:, :, k_from - source_from : k_to - source_from].rearrange(
-                    "n (r1 r0) k -> n r1 k r0", r0=2
+                    "n (q r0) k -> n q k r0", r0=2
                 )
-                second = g[q, 2 * p1 + 1][:, :, k_from:k_to].rearrange("n (r1 r0) k -> n r1 k r0", r0=2)
+                second = g[2 * p1 + 1, r1][:, :, 2 * pair : 2 * pair + 2, k_from:k_to].rearrange(
+                    "n r0 q k -> n q k r0"
+                )
+                start = (r1 * 2 + p1) * 8 * HALF
                 for u0 in range(2):
-                    start = ((q * 2 + p1) * 2 + u0) * UNIT
                     nc.vector.tensor_tensor(
-                        out=work[:, start : start + UNIT].rearrange("n (r1 k r0) -> n r1 k r0", r1=2, r0=2)[
-                            :, :, k_from - K_SIDE : k_to - K_SIDE, :
-                        ],
+                        out=work[:, start : start + 8 * HALF]
+                        .rearrange("n (q u x) -> n q u x", q=SIDE, u=2)[
+                            :, 2 * pair : 2 * pair + 2, u0, (k_from - K_SIDE) * 2 : (k_to - K_SIDE) * 2
+                        ]
+                        .rearrange("n q (k r0) -> n q k r0", r0=2),
                         in0=first,
                         in1=second,
                         op=SIGN_OP[u0],
@@ -187,29 +198,37 @@ def tile_iwht3layer_pa_kernel(tc, trans, weight, bias, grad_out, out):
 
             return consume
 
-        def pick(q, p):
+        def pick(p, r):
             def chore():
                 nc.scalar.copy(
-                    out=picked[:, :, :, SIDE * p + q, :],
-                    in_=g[q, p][:, :, 0:K_TENSOR].rearrange("n r (o e) -> n r o e", e=OCTET),
+                    out=picked[:, r, :, SIDE * p : SIDE * p + SIDE, :].rearrange("n o q e -> n q o e"),
+                    in_=g[p, r // 2][:, r % 2, :, 0:K_TENSOR].rearrange("n q (o e) -> n q o e", e=OCTET),
                 )
 
             return chore
 
-        for q in range(SIDE):
+        for r1 in range(2):
             for p1 in range(2):
-                for source_from, k_from, k_to in ((K_SIDE, K_SIDE, K_SIDE + 256), (K - 256, K_SIDE + 256, K)):
-                    sources = [g[q, 2 * p1][:, r, source_from : source_from + 256].bitcast(F32) for r in range(PACK)]
-                    jobs.append((sources, level1(p1, q, source_from, k_from, k_to)))
-            for p in range(SIDE):
-                add_chore(len(jobs) - 1 + p, pick(q, p))
+                for pair in range(2):
+                    for source_from, k_from, k_to in ((K_SIDE, K_SIDE, K_SIDE + 256), (K - 256, K_SIDE + 256, K)):
+                        sources = [
+                            g[2 * p1, r1][:, r0, 2 * pair + qi, source_from : source_from + 256].bitcast(F32)
+                            for qi in range(2)
+                            for r0 in range(2)
+                        ]
+                        jobs.append((sources, level1(r1, p1, pair, source_from, k_from, k_to)))
+                for i in range(4):
+                    add_chore(len(jobs) - 1 + i, pick(2 * p1 + i // 2, 2 * r1 + i % 2))
         level1_jobs = len(jobs)
 
-        for q in range(SIDE):
-            for c in range(2 * UNIT // CHUNK):
-                chunk_job(q * 4 * UNIT + c * CHUNK, (q * 4 + 2) * UNIT + c * CHUNK)
-        for c in range(8 * UNIT // CHUNK):
-            chunk_job(c * CHUNK, 8 * UNIT + c * CHUNK)
+        for r1 in range(2):
+            for c in range(8 * HALF // CHUNK):
+                chunk_job((r1 * 2) * 8 * HALF + c * CHUNK, (r1 * 2 + 1) * 8 * HALF + c * CHUNK)
+        for r1 in range(2):
+            for u1 in range(2):
+                for c in range(4 * HALF // CHUNK):
+                    start = (r1 * 2 + u1) * 8 * HALF
+                    chunk_job(start + c * CHUNK, start + 4 * HALF + c * CHUNK)
 
         step = level1_jobs + 3
         run_steps(0, step)
@@ -343,15 +362,16 @@ def tile_iwht3layer_pa_kernel(tc, trans, weight, bias, grad_out, out):
 
             def sums(m):
                 u0, u1, v1 = pairs[m]
-                a0 = (((2 * v1) * 2 + u1) * 2 + u0) * UNIT
-                b0 = (((2 * v1 + 1) * 2 + u1) * 2 + u0) * UNIT
+                by_unit = work[:].rearrange("n (r1 s x) -> n r1 s x", r1=2, s=T)
+                a_unit = ((u1 * 2 + v1) * 2) * 2 + u0
+                b_unit = ((u1 * 2 + v1) * 2 + 1) * 2 + u0
                 for v0 in range(2):
                     nc.vector.tensor_tensor(
                         out=gy_all[:, first_t(m) + v0, K_SIDE * PACK : K * PACK].rearrange(
                             "n (k r1 r0) -> n k r1 r0", r1=2, r0=2
                         ),
-                        in0=work[:, a0 : a0 + UNIT].rearrange("n (r1 k r0) -> n k r1 r0", r1=2, r0=2),
-                        in1=work[:, b0 : b0 + UNIT].rearrange("n (r1 k r0) -> n k r1 r0", r1=2, r0=2),
+                        in0=by_unit[:, :, a_unit, :].rearrange("n r1 (k r0) -> n k r1 r0", r0=2),
+                        in1=by_unit[:, :, b_unit, :].rearrange("n r1 (k r0) -> n k r1 r0", r0=2),
                         op=SIGN_OP[v0],
                     )
 

@@ -65,294 +65,287 @@ def tile_iwht3layer_pa_kernel(tc, trans, weight, bias, grad_out, out):
         name="pixel_pool", bufs=2
     ) as pixel_pool, tc.tile_pool(name="x_pool", bufs=2) as x_pool, tc.tile_pool(
         name="overlay", bufs=1
-    ) as overlay, tc.psum_pool(name="psum_t", bufs=2) as psum_t, tc.psum_pool(
-        name="psum_a", bufs=2
-    ) as psum_a, tc.manual_schedule():
-        ident = keep.tile([PARTS, PARTS], BF16, name="ident")
-        make_identity(nc, ident[:])
-        ident_f = keep.tile([PARTS, PARTS], F32, name="ident_f")
-        make_identity(nc, ident_f[:])
-        warm = keep.tile([PARTS, 1], BF16, name="warm")
-        nc.scalar.copy(out=warm[:], in_=ident[:, 0:1])
-        matrix = transform_matrix(nc, keep, ident)
+    ) as overlay, tc.manual_schedule():
+        with tc.psum_pool(name="psum_t", bufs=2) as psum_t, tc.psum_pool(name="psum_a", bufs=2) as psum_a:
+            ident = keep.tile([PARTS, PARTS], BF16, name="ident")
+            make_identity(nc, ident[:])
+            ident_f = keep.tile([PARTS, PARTS], F32, name="ident_f")
+            make_identity(nc, ident_f[:])
+            warm = keep.tile([PARTS, 1], BF16, name="warm")
+            nc.scalar.copy(out=warm[:], in_=ident[:, 0:1])
+            matrix = transform_matrix(nc, keep, ident)
 
-        work = keep.tile([PARTS, T * UNIT], F32, name="work")
-        pool_a = overlay.tile([PARTS, T * UNIT_G], F32, name="pool_a", offset=65536)
-        picked = overlay.tile([PARTS, PACK, OCTETS, T, OCTET], BF16, name="picked", offset=90112)
+            work = keep.tile([PARTS, T * UNIT], F32, name="work")
+            pool_a = overlay.tile([PARTS, T * UNIT_G], F32, name="pool_a", offset=65536)
+            picked = overlay.tile([PARTS, PACK, OCTETS, T, OCTET], BF16, name="picked", offset=90112)
 
-        jobs = []
-        st_of = {}
-        pa_of = {}
+            jobs = []
+            st_of = {}
+            pa_of = {}
 
-        def turn(s):
-            pt = psum_t.tile([PARTS, BLOCKS, BLOCK], F32, name="pt")
-            for j in range(BLOCKS):
-                nc.tensor.transpose(out=pt[:, j, :], in_=jobs[s][0][j], identity=ident_f[:])
-            st = turned.tile([PARTS, BLOCKS, BLOCK], F32, name="st")
-            nc.scalar.copy(out=st[:], in_=pt[:])
-            st_of[s] = st
+            def turn(s):
+                pt = psum_t.tile([PARTS, BLOCKS, BLOCK], F32, name="pt")
+                for j in range(BLOCKS):
+                    nc.tensor.transpose(out=pt[:, j, :], in_=jobs[s][0][j], identity=ident_f[:])
+                st = turned.tile([PARTS, BLOCKS, BLOCK], F32, name="st")
+                nc.scalar.copy(out=st[:], in_=pt[:])
+                st_of[s] = st
 
-        def turn_back(s):
-            pa = psum_a.tile([PARTS, BLOCKS, BLOCK], F32, name="pa")
-            for j in range(BLOCKS):
-                nc.tensor.transpose(out=pa[:, j, :], in_=st_of[s][:, j, :], identity=ident_f[:])
-            pa_of[s] = pa
+            def turn_back(s):
+                pa = psum_a.tile([PARTS, BLOCKS, BLOCK], F32, name="pa")
+                for j in range(BLOCKS):
+                    nc.tensor.transpose(out=pa[:, j, :], in_=st_of[s][:, j, :], identity=ident_f[:])
+                pa_of[s] = pa
 
-        def in_place(a0, b0):
-            def consume(pa):
-                first = pa[:].rearrange("n j w -> n (j w)")
-                nc.vector.tensor_tensor(
-                    out=work[:, a0 : a0 + CHUNK], in0=first, in1=work[:, b0 : b0 + CHUNK], op=SIGN_OP[0]
-                )
-                nc.vector.tensor_tensor(
-                    out=work[:, b0 : b0 + CHUNK], in0=first, in1=work[:, b0 : b0 + CHUNK], op=SIGN_OP[1]
-                )
-
-            return consume
-
-        def chunk_job(a0, b0):
-            sources = [work[:, a0 + j * BLOCK : a0 + (j + 1) * BLOCK] for j in range(BLOCKS)]
-            jobs.append((sources, in_place(a0, b0)))
-
-        chores = {}
-
-        def add_chore(step, chore):
-            chores.setdefault(step, []).append(chore)
-
-        def run_steps(first, last):
-            for s in range(first, last):
-                if s < len(jobs):
-                    turn(s)
-                for chore in chores.get(s, []):
-                    chore()
-                if 0 <= s - 2 < len(jobs):
-                    turn_back(s - 2)
-                if 0 <= s - 3 < len(jobs):
-                    jobs[s - 3][1](pa_of[s - 3])
-
-        g = {}
-        for r1 in range(2):
-            for p in range(SIDE):
-                g[p, r1] = overlay.tile(
-                    [PARTS, 2, SIDE, K], BF16, name="g%d%d" % (p, r1), offset=(SIDE * r1 + p) * 8192
-                )
-                for jh in range(2):
-                    nc.sync.dma_start(
-                        out=g[p, r1][jh:PARTS:2].rearrange("n r0 q k -> n (r0 q k)"), in_=g_dram[jh, p, r1]
-                    )
-
-        x_raw_of = {}
-        x_of = {}
-        x_codes_of = {}
-
-        def load_x(u):
-            x_raw = x_pool.tile([PARTS, SIDE, PACK, C], BF16, name="x_raw")
-            nc.sync.dma_start(out=x_raw[:].rearrange("n v r c -> n v (r c)"), in_=x_dram[u])
-            x_raw_of[u] = x_raw
-
-        def regroup_x(u, half):
-            def chore():
-                nc.scalar.copy(
-                    out=x_of[u][:, 2 * half : 2 * half + 2],
-                    in_=x_raw_of[u][:, 2 * half : 2 * half + 2].rearrange("n v r c -> n v c r"),
-                )
-
-            return chore
-
-        load_x(u_order[0])
-        load_x(u_order[1])
-
-        for r1 in range(2):
-            for p1 in range(2):
-                for u0 in range(2):
-                    start = (u0 * 2 + p1) * SIDE * UNIT_G
-                    nc.gpsimd.tensor_tensor(
-                        out=pool_a[:, start : start + SIDE * UNIT_G]
-                        .rearrange("n (q r1 x) -> n q r1 x", q=SIDE, r1=2)[:, :, r1, :]
-                        .rearrange("n q (k r0) -> n q k r0", r0=2),
-                        in0=g[2 * p1, r1][:, :, :, K_TENSOR:K_SIDE].rearrange("n r0 q k -> n q k r0"),
-                        in1=g[2 * p1 + 1, r1][:, :, :, K_TENSOR:K_SIDE].rearrange("n r0 q k -> n q k r0"),
-                        op=SIGN_OP[u0],
-                    )
-
-        def level1(r1, p1, pair, source_from, k_from, k_to):
-            def consume(pa):
-                first = pa[:].bitcast(BF16)[:, :, k_from - source_from : k_to - source_from].rearrange(
-                    "n (q r0) k -> n q k r0", r0=2
-                )
-                second = g[2 * p1 + 1, r1][:, :, 2 * pair : 2 * pair + 2, k_from:k_to].rearrange(
-                    "n r0 q k -> n q k r0"
-                )
-                start = (r1 * 2 + p1) * 8 * HALF
-                for u0 in range(2):
+            def in_place(a0, b0):
+                def consume(pa):
+                    first = pa[:].rearrange("n j w -> n (j w)")
                     nc.vector.tensor_tensor(
-                        out=work[:, start : start + 8 * HALF]
-                        .rearrange("n (q u x) -> n q u x", q=SIDE, u=2)[
-                            :, 2 * pair : 2 * pair + 2, u0, (k_from - K_SIDE) * 2 : (k_to - K_SIDE) * 2
-                        ]
-                        .rearrange("n q (k r0) -> n q k r0", r0=2),
-                        in0=first,
-                        in1=second,
-                        op=SIGN_OP[u0],
+                        out=work[:, a0 : a0 + CHUNK], in0=first, in1=work[:, b0 : b0 + CHUNK], op=SIGN_OP[0]
+                    )
+                    nc.vector.tensor_tensor(
+                        out=work[:, b0 : b0 + CHUNK], in0=first, in1=work[:, b0 : b0 + CHUNK], op=SIGN_OP[1]
                     )
 
-            return consume
+                return consume
 
-        def pick(p, r):
-            def chore():
-                nc.scalar.copy(
-                    out=picked[:, r, :, SIDE * p : SIDE * p + SIDE, :].rearrange("n o q e -> n q o e"),
-                    in_=g[p, r // 2][:, r % 2, :, 0:K_TENSOR].rearrange("n q (o e) -> n q o e", e=OCTET),
-                )
+            def chunk_job(a0, b0):
+                sources = [work[:, a0 + j * BLOCK : a0 + (j + 1) * BLOCK] for j in range(BLOCKS)]
+                jobs.append((sources, in_place(a0, b0)))
 
-            return chore
+            chores = {}
 
-        for r1 in range(2):
-            for p1 in range(2):
-                for pair in range(2):
-                    for source_from, k_from, k_to in ((K_SIDE, K_SIDE, K_SIDE + 256), (K - 256, K_SIDE + 256, K)):
-                        sources = [
-                            g[2 * p1, r1][:, r0, 2 * pair + qi, source_from : source_from + 256].bitcast(F32)
-                            for qi in range(2)
-                            for r0 in range(2)
-                        ]
-                        jobs.append((sources, level1(r1, p1, pair, source_from, k_from, k_to)))
-                for i in range(4):
-                    add_chore(len(jobs) - 1 + i, pick(2 * p1 + i // 2, 2 * r1 + i % 2))
-        level1_jobs = len(jobs)
+            def add_chore(step, chore):
+                chores.setdefault(step, []).append(chore)
 
-        for r1 in range(2):
-            for c in range(8 * HALF // CHUNK):
-                chunk_job((r1 * 2) * 8 * HALF + c * CHUNK, (r1 * 2 + 1) * 8 * HALF + c * CHUNK)
-        for r1 in range(2):
-            for u1 in range(2):
-                for c in range(4 * HALF // CHUNK):
-                    start = (r1 * 2 + u1) * 8 * HALF
-                    chunk_job(start + c * CHUNK, start + 4 * HALF + c * CHUNK)
+            def run_steps(first, last):
+                for s in range(first, last):
+                    if 0 <= s - 2 < len(jobs):
+                        turn_back(s - 2)
+                    if s < len(jobs):
+                        turn(s)
+                    for chore in chores.get(s, []):
+                        chore()
+                    if 0 <= s - 3 < len(jobs):
+                        jobs[s - 3][1](pa_of[s - 3])
 
-        step = level1_jobs + 3
-        run_steps(0, step)
-
-        gy_all = overlay.tile([PARTS, T, K * PACK], BF16, name="gy_all", offset=0, align_bytes=64)
-        gy_by_bits = gy_all[:].rearrange("n (u1 u0 v1 v0) x -> n u1 u0 v1 v0 x", u1=2, u0=2, v1=2)
-
-        x_of[u_order[0]] = x_pool.tile([PARTS, SIDE, C, PACK], BF16, name="x", align_bytes=64)
-        nc.gpsimd.tensor_scalar(
-            out=x_of[u_order[0]][:],
-            in0=x_raw_of[u_order[0]][:].rearrange("n v r c -> n v c r"),
-            scalar1=1.0,
-            scalar2=0.0,
-            op0=mybir.AluOpType.mult,
-            op1=mybir.AluOpType.add,
-        )
-        load_x(u_order[2])
-        pool_b = overlay.tile([PARTS, 8 * UNIT_G], F32, name="pool_b", offset=102400)
-        for u0 in range(2):
-            half = pool_a[:, u0 * 8 * UNIT_G : (u0 + 1) * 8 * UNIT_G]
-            for u1 in range(2):
-                nc.gpsimd.tensor_tensor(
-                    out=pool_b[:, u1 * 4 * UNIT_G : (u1 + 1) * 4 * UNIT_G],
-                    in0=half[:, 0 : 4 * UNIT_G],
-                    in1=half[:, 4 * UNIT_G : 8 * UNIT_G],
-                    op=SIGN_OP[u1],
-                )
-            b_view = pool_b[:].rearrange("n (u q1 x) -> n u q1 x", u=2, q1=2)
-            a_view = half.rearrange("n (u v x) -> n u v x", u=2, v=2)
-            for v1 in range(2):
-                nc.gpsimd.tensor_tensor(
-                    out=a_view[:, :, v1, :], in0=b_view[:, :, 0, :], in1=b_view[:, :, 1, :], op=SIGN_OP[v1]
-                )
-
-        with tc.psum_pool(name="psum_pe", bufs=2) as psum_pe:
-            pixels_of = {}
-
-            def pixels_to_partitions(o2):
-                def chore():
-                    pix_ps = psum_pe.tile([PARTS, 2, PACK, PARTS], BF16, name="pix_ps")
-                    for i in range(2):
-                        for r in range(PACK):
-                            nc.tensor.transpose(
-                                out=pix_ps[:, i, r, :],
-                                in_=picked[:, r, 2 * o2 + i, :, :].rearrange("n a e -> n (a e)"),
-                                identity=ident[:],
-                            )
-                    pixels = pixel_pool.tile([PARTS, 2, PACK, PARTS], BF16, name="pixels")
-                    nc.scalar.copy(out=pixels[:], in_=pix_ps[:])
-                    pixels_of[o2] = pixels
-
-                return chore
-
-            def transform(o):
-                def chore():
-                    coef_ps = psum_pe.tile([PARTS, PACK, PARTS], F32, name="coef_ps")
-                    for r in range(PACK):
-                        nc.tensor.matmul(
-                            out=coef_ps[:, r, :],
-                            lhsT=pixels_of[o // 2][:, o % 2, r, :],
-                            rhs=matrix[:],
-                            start=True,
-                            stop=True,
+            g = {}
+            for r1 in range(2):
+                for p in range(SIDE):
+                    g[p, r1] = overlay.tile(
+                        [PARTS, 2, SIDE, K], BF16, name="g%d%d" % (p, r1), offset=(SIDE * r1 + p) * 8192
+                    )
+                    for jh in range(2):
+                        nc.sync.dma_start(
+                            out=g[p, r1][jh:PARTS:2].rearrange("n r0 q k -> n (r0 q k)"), in_=g_dram[jh, p, r1]
                         )
+
+            x_raw_of = {}
+            x_of = {}
+            x_codes_of = {}
+
+            def load_x(u):
+                x_raw = x_pool.tile([PARTS, SIDE, PACK, C], BF16, name="x_raw")
+                nc.sync.dma_start(out=x_raw[:].rearrange("n v r c -> n v (r c)"), in_=x_dram[u])
+                x_raw_of[u] = x_raw
+
+            def regroup_x(u, half):
+                def chore():
                     nc.scalar.copy(
-                        out=gy_all[:, :, o * OCTET * PACK : (o + 1) * OCTET * PACK].rearrange(
-                            "n t (e r) -> n t e r", r=PACK
-                        ),
-                        in_=coef_ps[:].rearrange("n r (t e) -> n t e r", e=OCTET),
+                        out=x_of[u][:, 2 * half : 2 * half + 2],
+                        in_=x_raw_of[u][:, 2 * half : 2 * half + 2].rearrange("n v r c -> n v c r"),
                     )
 
                 return chore
 
-            at = step
-            add_chore(at, pixels_to_partitions(0))
-            for o2 in range(OCTETS // 2):
-                if o2 + 1 < OCTETS // 2:
-                    add_chore(at + 1, pixels_to_partitions(o2 + 1))
-                add_chore(at + 2, transform(2 * o2))
-                add_chore(at + 3, transform(2 * o2 + 1))
-                at += 3
-            path_end = at + 1
+            load_x(u_order[0])
+            load_x(u_order[1])
 
-            def open_x(u, pool_tile):
+            for r1 in range(2):
+                for p1 in range(2):
+                    for u0 in range(2):
+                        start = (u0 * 2 + p1) * SIDE * UNIT_G
+                        nc.gpsimd.tensor_tensor(
+                            out=pool_a[:, start : start + SIDE * UNIT_G]
+                            .rearrange("n (q r1 x) -> n q r1 x", q=SIDE, r1=2)[:, :, r1, :]
+                            .rearrange("n q (k r0) -> n q k r0", r0=2),
+                            in0=g[2 * p1, r1][:, :, :, K_TENSOR:K_SIDE].rearrange("n r0 q k -> n q k r0"),
+                            in1=g[2 * p1 + 1, r1][:, :, :, K_TENSOR:K_SIDE].rearrange("n r0 q k -> n q k r0"),
+                            op=SIGN_OP[u0],
+                        )
+                    for u0 in range(2):
+                        start = (r1 * 2 + p1) * 8 * HALF
+                        nc.gpsimd.tensor_tensor(
+                            out=work[:, start : start + 8 * HALF]
+                            .rearrange("n (q u x) -> n q u x", q=SIDE, u=2)[:, :, u0, 512:HALF]
+                            .rearrange("n q (k r0) -> n q k r0", r0=2),
+                            in0=g[2 * p1, r1][:, :, :, K_SIDE + 256 : K].rearrange("n r0 q k -> n q k r0"),
+                            in1=g[2 * p1 + 1, r1][:, :, :, K_SIDE + 256 : K].rearrange("n r0 q k -> n q k r0"),
+                            op=SIGN_OP[u0],
+                        )
+
+            def level1(r1, p1, pair, source_from, k_from, k_to):
+                def consume(pa):
+                    first = pa[:].bitcast(BF16)[:, :, k_from - source_from : k_to - source_from].rearrange(
+                        "n (q r0) k -> n q k r0", r0=2
+                    )
+                    second = g[2 * p1 + 1, r1][:, :, 2 * pair : 2 * pair + 2, k_from:k_to].rearrange(
+                        "n r0 q k -> n q k r0"
+                    )
+                    start = (r1 * 2 + p1) * 8 * HALF
+                    for u0 in range(2):
+                        nc.vector.tensor_tensor(
+                            out=work[:, start : start + 8 * HALF]
+                            .rearrange("n (q u x) -> n q u x", q=SIDE, u=2)[
+                                :, 2 * pair : 2 * pair + 2, u0, (k_from - K_SIDE) * 2 : (k_to - K_SIDE) * 2
+                            ]
+                            .rearrange("n q (k r0) -> n q k r0", r0=2),
+                            in0=first,
+                            in1=second,
+                            op=SIGN_OP[u0],
+                        )
+
+                return consume
+
+            def pick(p, r):
                 def chore():
-                    x_of[u] = pool_tile()
+                    nc.scalar.copy(
+                        out=picked[:, r, :, SIDE * p : SIDE * p + SIDE, :].rearrange("n o q e -> n q o e"),
+                        in_=g[p, r // 2][:, r % 2, :, 0:K_TENSOR].rearrange("n q (o e) -> n q o e", e=OCTET),
+                    )
 
                 return chore
 
-            add_chore(path_end, open_x(u_order[1], lambda: x_pool.tile([PARTS, SIDE, C, PACK], BF16, name="x", align_bytes=64)))
-            add_chore(path_end, regroup_x(u_order[1], 0))
-            add_chore(path_end + 3, regroup_x(u_order[1], 1))
-            add_chore(path_end + 3, lambda: load_x(u_order[3]))
+            for r1 in range(2):
+                for p1 in range(2):
+                    for pair in range(2):
+                        for source_from, k_from, k_to in ((K_SIDE, K_SIDE, K_SIDE + 256),):
+                            sources = [
+                                g[2 * p1, r1][:, r0, 2 * pair + qi, source_from : source_from + 256].bitcast(F32)
+                                for qi in range(2)
+                                for r0 in range(2)
+                            ]
+                            jobs.append((sources, level1(r1, p1, pair, source_from, k_from, k_to)))
+                    for i in range(4):
+                        add_chore(len(jobs) - 1 + i, pick(2 * p1 + i // 2, 2 * r1 + i % 2))
+            level1_jobs = len(jobs)
 
-            run_steps(step, path_end)
+            for r1 in range(2):
+                for c in range(8 * HALF // CHUNK):
+                    chunk_job((r1 * 2) * 8 * HALF + c * CHUNK, (r1 * 2 + 1) * 8 * HALF + c * CHUNK)
+            for r1 in range(2):
+                for u1 in range(2):
+                    for c in range(4 * HALF // CHUNK):
+                        start = (r1 * 2 + u1) * 8 * HALF
+                        chunk_job(start + c * CHUNK, start + 4 * HALF + c * CHUNK)
 
-        for u0 in range(2):
-            a_pairs = pool_a[:, u0 * 8 * UNIT_G : (u0 + 1) * 8 * UNIT_G].rearrange(
-                "n (u v q0 x) -> n u v q0 x", u=2, v=2, q0=2
-            )
-            for u1 in range(2):
+            step = level1_jobs + 3
+            run_steps(0, step)
+
+            gy_all = overlay.tile([PARTS, T, K * PACK], BF16, name="gy_all", offset=0, align_bytes=64)
+            gy_by_bits = gy_all[:].rearrange("n (u1 u0 v1 v0) x -> n u1 u0 v1 v0 x", u1=2, u0=2, v1=2)
+
+            for i in range(2):
+                x_of[u_order[i]] = x_pool.tile([PARTS, SIDE, C, PACK], BF16, name="x", align_bytes=64)
+                add_chore(step + 3 + 8 * i, regroup_x(u_order[i], 0))
+                add_chore(step + 7 + 8 * i, regroup_x(u_order[i], 1))
+            add_chore(step + 7, lambda: load_x(u_order[2]))
+            add_chore(step + 15, lambda: load_x(u_order[3]))
+
+            pool_b = overlay.tile([PARTS, 8 * UNIT_G], F32, name="pool_b", offset=102400)
+            for u0 in range(2):
+                half = pool_a[:, u0 * 8 * UNIT_G : (u0 + 1) * 8 * UNIT_G]
+                for u1 in range(2):
+                    nc.gpsimd.tensor_tensor(
+                        out=pool_b[:, u1 * 4 * UNIT_G : (u1 + 1) * 4 * UNIT_G],
+                        in0=half[:, 0 : 4 * UNIT_G],
+                        in1=half[:, 4 * UNIT_G : 8 * UNIT_G],
+                        op=SIGN_OP[u1],
+                    )
+                b_view = pool_b[:].rearrange("n (u q1 x) -> n u q1 x", u=2, q1=2)
+                a_view = half.rearrange("n (u v x) -> n u v x", u=2, v=2)
                 for v1 in range(2):
-                    for v0 in range(2):
-                        nc.gpsimd.tensor_tensor(
-                            out=gy_by_bits[:, u1, u0, v1, v0, K_TENSOR * PACK : K_SIDE * PACK].rearrange(
-                                "n (k r1 r0) -> n k r1 r0", r1=2, r0=2
+                    nc.gpsimd.tensor_tensor(
+                        out=a_view[:, :, v1, :], in0=b_view[:, :, 0, :], in1=b_view[:, :, 1, :], op=SIGN_OP[v1]
+                    )
+
+            with tc.psum_pool(name="psum_pe", bufs=2) as psum_pe:
+                pixels_of = {}
+
+                def pixels_to_partitions(o2):
+                    def chore():
+                        pix_ps = psum_pe.tile([PARTS, 2, PACK, PARTS], BF16, name="pix_ps")
+                        for i in range(2):
+                            for r in range(PACK):
+                                nc.tensor.transpose(
+                                    out=pix_ps[:, i, r, :],
+                                    in_=picked[:, r, 2 * o2 + i, :, :].rearrange("n a e -> n (a e)"),
+                                    identity=ident[:],
+                                )
+                        pixels = pixel_pool.tile([PARTS, 2, PACK, PARTS], BF16, name="pixels")
+                        nc.scalar.copy(out=pixels[:], in_=pix_ps[:])
+                        pixels_of[o2] = pixels
+
+                    return chore
+
+                def transform(o):
+                    def chore():
+                        coef_ps = psum_pe.tile([PARTS, PACK, PARTS], F32, name="coef_ps")
+                        for r in range(PACK):
+                            nc.tensor.matmul(
+                                out=coef_ps[:, r, :],
+                                lhsT=pixels_of[o // 2][:, o % 2, r, :],
+                                rhs=matrix[:],
+                                start=True,
+                                stop=True,
+                            )
+                        nc.scalar.copy(
+                            out=gy_all[:, :, o * OCTET * PACK : (o + 1) * OCTET * PACK].rearrange(
+                                "n t (e r) -> n t e r", r=PACK
                             ),
-                            in0=a_pairs[:, u1, v1, 0, :].rearrange("n (r1 k r0) -> n k r1 r0", r1=2, r0=2),
-                            in1=a_pairs[:, u1, v1, 1, :].rearrange("n (r1 k r0) -> n k r1 r0", r1=2, r0=2),
-                            op=SIGN_OP[v0],
+                            in_=coef_ps[:].rearrange("n r (t e) -> n t e r", e=OCTET),
                         )
 
-        add_chore(
-            path_end + 8,
-            open_x(
-                u_order[2],
-                lambda: overlay.tile([PARTS, SIDE, C, PACK], BF16, name="x_third", offset=98304, align_bytes=64),
-            ),
-        )
-        add_chore(path_end + 8, regroup_x(u_order[2], 0))
-        add_chore(path_end + 11, regroup_x(u_order[2], 1))
-        run_steps(path_end, len(jobs) + 3)
+                    return chore
 
-        with tc.psum_pool(name="acc_pool", bufs=4) as acc_pool:
+                path = [pixels_to_partitions(0)]
+                for o2 in range(OCTETS // 2):
+                    if o2 + 1 < OCTETS // 2:
+                        path.append(pixels_to_partitions(o2 + 1))
+                    path.append(transform(2 * o2))
+                    path.append(transform(2 * o2 + 1))
+                for i in range(len(path)):
+                    add_chore(step + 2 * i, path[i])
+                path_end = step + 2 * len(path)
+                run_steps(step, path_end)
+
+            for u0 in range(2):
+                a_pairs = pool_a[:, u0 * 8 * UNIT_G : (u0 + 1) * 8 * UNIT_G].rearrange(
+                    "n (u v q0 x) -> n u v q0 x", u=2, v=2, q0=2
+                )
+                for u1 in range(2):
+                    for v1 in range(2):
+                        for v0 in range(2):
+                            nc.gpsimd.tensor_tensor(
+                                out=gy_by_bits[:, u1, u0, v1, v0, K_TENSOR * PACK : K_SIDE * PACK].rearrange(
+                                    "n (k r1 r0) -> n k r1 r0", r1=2, r0=2
+                                ),
+                                in0=a_pairs[:, u1, v1, 0, :].rearrange("n (r1 k r0) -> n k r1 r0", r1=2, r0=2),
+                                in1=a_pairs[:, u1, v1, 1, :].rearrange("n (r1 k r0) -> n k r1 r0", r1=2, r0=2),
+                                op=SIGN_OP[v0],
+                            )
+
+            def open_third():
+                x_of[u_order[2]] = overlay.tile(
+                    [PARTS, SIDE, C, PACK], BF16, name="x_third", offset=98304, align_bytes=64
+                )
+
+            add_chore(path_end, open_third)
+            add_chore(path_end, regroup_x(u_order[2], 0))
+            add_chore(path_end + 3, regroup_x(u_order[2], 1))
+            run_steps(path_end, len(jobs) + 3)
+
+        with tc.psum_pool(name="acc_pool", bufs=8) as acc_pool:
             pairs = [(u0, u1, v1) for u0 in range(2) for u1 in range(2) for v1 in range(2)]
             banks_of = {}
 
@@ -441,8 +434,9 @@ def tile_iwht3layer_pa_kernel(tc, trans, weight, bias, grad_out, out):
                     store(m - 2, m - 2 >= count - 1)
                 if 0 <= m - 1 < count:
                     multiply(m - 1)
-                if m == 1:
-                    x_of[u_order[3]] = x_pool.tile([PARTS, SIDE, C, PACK], BF16, name="x", align_bytes=64)
-                    regroup_x(u_order[3], 0)()
-                if m == 2:
-                    regroup_x(u_order[3], 1)()
+                if m == 0:
+                    x_of[u_order[3]] = overlay.tile(
+                        [PARTS, SIDE, C, PACK], BF16, name="x_fourth", offset=106496, align_bytes=64
+                    )
+                if m in (0, 1):
+                    regroup_x(u_order[3], m)()

@@ -28,7 +28,9 @@ K_SIDE = K_TENSOR + K_POOL
 K_VECTOR = K - K_SIDE
 UNIT = K_VECTOR * PACK
 UNIT_G = K_POOL * PACK
-HALF = K_VECTOR * 2
+K_BLOCK = 256
+HALF_A = K_BLOCK * 2
+HALF_B = (K_VECTOR - K_BLOCK) * 2
 BLOCK = 128
 BLOCKS = 4
 CHUNK = BLOCK * BLOCKS
@@ -55,7 +57,7 @@ def transform_matrix(nc, pool, ident):
 def tile_iwht3layer_pa_kernel(tc, trans, weight, bias, grad_out, out):
     nc = tc.nc
 
-    g_dram = grad_out.rearrange("b (i p) (jh r1 r0 q) k -> jh p r1 (b i) (r0 q k)", p=SIDE, jh=2, r1=2, r0=2)
+    g_dram = grad_out.rearrange("b (i p) (jh r1 r0 q) k -> jh p r1 (b i) r0 (q k)", p=SIDE, jh=2, r1=2, r0=2)
     x_dram = trans.rearrange("(u v) b i (jh r) c -> u (b i jh) v (r c)", v=SIDE, r=PACK)
     out_dram = out.rearrange("t (h m) k -> t m h k", h=C_HALVES)
 
@@ -66,7 +68,7 @@ def tile_iwht3layer_pa_kernel(tc, trans, weight, bias, grad_out, out):
     ) as pixel_pool, tc.tile_pool(name="x_pool", bufs=2) as x_pool, tc.tile_pool(
         name="overlay", bufs=1
     ) as overlay, tc.manual_schedule():
-        with tc.psum_pool(name="psum_t", bufs=2) as psum_t, tc.psum_pool(name="psum_a", bufs=2) as psum_a:
+        with tc.psum_pool(name="psum_t", bufs=3) as psum_t, tc.psum_pool(name="psum_a", bufs=3) as psum_a:
             ident = keep.tile([PARTS, PARTS], BF16, name="ident")
             make_identity(nc, ident[:])
             ident_f = keep.tile([PARTS, PARTS], F32, name="ident_f")
@@ -75,7 +77,8 @@ def tile_iwht3layer_pa_kernel(tc, trans, weight, bias, grad_out, out):
             nc.scalar.copy(out=warm[:], in_=ident[:, 0:1])
             matrix = transform_matrix(nc, keep, ident)
 
-            work = keep.tile([PARTS, T * UNIT], F32, name="work")
+            work = keep.tile([PARTS, 2 * T * HALF_A], F32, name="work")
+            work_b = keep.tile([PARTS, 2 * T * HALF_B], F32, name="work_b")
             pool_a = overlay.tile([PARTS, T * UNIT_G], F32, name="pool_a", offset=65536)
             picked = overlay.tile([PARTS, PACK, OCTETS, T, OCTET], BF16, name="picked", offset=90112)
 
@@ -97,21 +100,22 @@ def tile_iwht3layer_pa_kernel(tc, trans, weight, bias, grad_out, out):
                     nc.tensor.transpose(out=pa[:, j, :], in_=st_of[s][:, j, :], identity=ident_f[:])
                 pa_of[s] = pa
 
-            def in_place(a0, b0):
+            def in_place(buffer, a0, b0):
                 def consume(pa):
                     first = pa[:].rearrange("n j w -> n (j w)")
                     nc.vector.tensor_tensor(
-                        out=work[:, a0 : a0 + CHUNK], in0=first, in1=work[:, b0 : b0 + CHUNK], op=SIGN_OP[0]
+                        out=buffer[:, a0 : a0 + CHUNK], in0=first, in1=buffer[:, b0 : b0 + CHUNK], op=SIGN_OP[0]
                     )
                     nc.vector.tensor_tensor(
-                        out=work[:, b0 : b0 + CHUNK], in0=first, in1=work[:, b0 : b0 + CHUNK], op=SIGN_OP[1]
+                        out=buffer[:, b0 : b0 + CHUNK], in0=first, in1=buffer[:, b0 : b0 + CHUNK], op=SIGN_OP[1]
                     )
 
                 return consume
 
-            def chunk_job(a0, b0):
-                sources = [work[:, a0 + j * BLOCK : a0 + (j + 1) * BLOCK] for j in range(BLOCKS)]
-                jobs.append((sources, in_place(a0, b0)))
+            def chunk_jobs(buffer, a0, b0, length):
+                for c0 in range(0, length, CHUNK):
+                    sources = [buffer[:, a0 + c0 + j * BLOCK : a0 + c0 + (j + 1) * BLOCK] for j in range(BLOCKS)]
+                    jobs.append((sources, in_place(buffer, a0 + c0, b0 + c0)))
 
             chores = {}
 
@@ -131,14 +135,31 @@ def tile_iwht3layer_pa_kernel(tc, trans, weight, bias, grad_out, out):
 
             g = {}
             for r1 in range(2):
-                for p in range(SIDE):
-                    g[p, r1] = overlay.tile(
-                        [PARTS, 2, SIDE, K], BF16, name="g%d%d" % (p, r1), offset=(SIDE * r1 + p) * 8192
-                    )
-                    for jh in range(2):
-                        nc.sync.dma_start(
-                            out=g[p, r1][jh:PARTS:2].rearrange("n r0 q k -> n (r0 q k)"), in_=g_dram[jh, p, r1]
-                        )
+                for p1 in range(2):
+                    split = 2 if (r1, p1) == (0, 0) else 1
+                    for part in range(split):
+                        for p in (2 * p1, 2 * p1 + 1):
+                            q_count = SIDE // split
+                            tile = overlay.tile(
+                                [PARTS, 2, q_count, K],
+                                BF16,
+                                name="g%d%d%d" % (p, r1, part),
+                                offset=(SIDE * r1 + p) * 8192 + part * 4096,
+                            )
+                            for jh in range(2):
+                                nc.sync.dma_start(
+                                    out=tile[jh:PARTS:2].rearrange("n r0 q k -> n r0 (q k)"),
+                                    in_=g_dram[jh, p, r1][:, :, part * q_count * K : (part + 1) * q_count * K],
+                                )
+                            for q in range(part * q_count, (part + 1) * q_count):
+                                g[p, r1, q] = (tile, part * q_count)
+
+            def rows(p, r1, q_from, q_count):
+                tile, first_q = g[p, r1, q_from]
+                return tile[:, :, q_from - first_q : q_from - first_q + q_count, :]
+
+            def spans(r1, p1):
+                return ((0, 2), (2, 2)) if (r1, p1) == (0, 0) else ((0, SIDE),)
 
             x_raw_of = {}
             x_of = {}
@@ -163,39 +184,42 @@ def tile_iwht3layer_pa_kernel(tc, trans, weight, bias, grad_out, out):
 
             for r1 in range(2):
                 for p1 in range(2):
-                    for u0 in range(2):
-                        start = (u0 * 2 + p1) * SIDE * UNIT_G
-                        nc.gpsimd.tensor_tensor(
-                            out=pool_a[:, start : start + SIDE * UNIT_G]
-                            .rearrange("n (q r1 x) -> n q r1 x", q=SIDE, r1=2)[:, :, r1, :]
-                            .rearrange("n q (k r0) -> n q k r0", r0=2),
-                            in0=g[2 * p1, r1][:, :, :, K_TENSOR:K_SIDE].rearrange("n r0 q k -> n q k r0"),
-                            in1=g[2 * p1 + 1, r1][:, :, :, K_TENSOR:K_SIDE].rearrange("n r0 q k -> n q k r0"),
-                            op=SIGN_OP[u0],
-                        )
-                    for u0 in range(2):
-                        start = (r1 * 2 + p1) * 8 * HALF
-                        nc.gpsimd.tensor_tensor(
-                            out=work[:, start : start + 8 * HALF]
-                            .rearrange("n (q u x) -> n q u x", q=SIDE, u=2)[:, :, u0, 512:HALF]
-                            .rearrange("n q (k r0) -> n q k r0", r0=2),
-                            in0=g[2 * p1, r1][:, :, :, K_SIDE + 256 : K].rearrange("n r0 q k -> n q k r0"),
-                            in1=g[2 * p1 + 1, r1][:, :, :, K_SIDE + 256 : K].rearrange("n r0 q k -> n q k r0"),
-                            op=SIGN_OP[u0],
-                        )
+                    for q_from, q_count in spans(r1, p1):
+                        a_rows = rows(2 * p1, r1, q_from, q_count)
+                        b_rows = rows(2 * p1 + 1, r1, q_from, q_count)
+                        for u0 in range(2):
+                            start = (u0 * 2 + p1) * SIDE * UNIT_G
+                            nc.gpsimd.tensor_tensor(
+                                out=pool_a[:, start : start + SIDE * UNIT_G]
+                                .rearrange("n (q r1 x) -> n q r1 x", q=SIDE, r1=2)[:, q_from : q_from + q_count, r1, :]
+                                .rearrange("n q (k r0) -> n q k r0", r0=2),
+                                in0=a_rows[:, :, :, K_TENSOR:K_SIDE].rearrange("n r0 q k -> n q k r0"),
+                                in1=b_rows[:, :, :, K_TENSOR:K_SIDE].rearrange("n r0 q k -> n q k r0"),
+                                op=SIGN_OP[u0],
+                            )
+                        for u0 in range(2):
+                            start = (r1 * 2 + p1) * 8 * HALF_B
+                            nc.gpsimd.tensor_tensor(
+                                out=work_b[:, start : start + 8 * HALF_B]
+                                .rearrange("n (q u x) -> n q u x", q=SIDE, u=2)[:, q_from : q_from + q_count, u0, :]
+                                .rearrange("n q (k r0) -> n q k r0", r0=2),
+                                in0=a_rows[:, :, :, K_SIDE + K_BLOCK : K].rearrange("n r0 q k -> n q k r0"),
+                                in1=b_rows[:, :, :, K_SIDE + K_BLOCK : K].rearrange("n r0 q k -> n q k r0"),
+                                op=SIGN_OP[u0],
+                            )
 
             def level1(r1, p1, pair, source_from, k_from, k_to):
                 def consume(pa):
                     first = pa[:].bitcast(BF16)[:, :, k_from - source_from : k_to - source_from].rearrange(
                         "n (q r0) k -> n q k r0", r0=2
                     )
-                    second = g[2 * p1 + 1, r1][:, :, 2 * pair : 2 * pair + 2, k_from:k_to].rearrange(
+                    second = rows(2 * p1 + 1, r1, 2 * pair, 2)[:, :, :, k_from:k_to].rearrange(
                         "n r0 q k -> n q k r0"
                     )
-                    start = (r1 * 2 + p1) * 8 * HALF
+                    start = (r1 * 2 + p1) * 8 * HALF_A
                     for u0 in range(2):
                         nc.vector.tensor_tensor(
-                            out=work[:, start : start + 8 * HALF]
+                            out=work[:, start : start + 8 * HALF_A]
                             .rearrange("n (q u x) -> n q u x", q=SIDE, u=2)[
                                 :, 2 * pair : 2 * pair + 2, u0, (k_from - K_SIDE) * 2 : (k_to - K_SIDE) * 2
                             ]
@@ -209,37 +233,49 @@ def tile_iwht3layer_pa_kernel(tc, trans, weight, bias, grad_out, out):
 
             def pick(p, r):
                 def chore():
-                    nc.scalar.copy(
-                        out=picked[:, r, :, SIDE * p : SIDE * p + SIDE, :].rearrange("n o q e -> n q o e"),
-                        in_=g[p, r // 2][:, r % 2, :, 0:K_TENSOR].rearrange("n q (o e) -> n q o e", e=OCTET),
-                    )
+                    for q_from, q_count in spans(r // 2, p // 2):
+                        nc.scalar.copy(
+                            out=picked[:, r, :, SIDE * p + q_from : SIDE * p + q_from + q_count, :].rearrange(
+                                "n o q e -> n q o e"
+                            ),
+                            in_=rows(p, r // 2, q_from, q_count)[:, r % 2, :, 0:K_TENSOR].rearrange(
+                                "n q (o e) -> n q o e", e=OCTET
+                            ),
+                        )
 
                 return chore
 
-            for r1 in range(2):
-                for p1 in range(2):
-                    for pair in range(2):
-                        for source_from, k_from, k_to in ((K_SIDE, K_SIDE, K_SIDE + 256),):
-                            sources = [
-                                g[2 * p1, r1][:, r0, 2 * pair + qi, source_from : source_from + 256].bitcast(F32)
-                                for qi in range(2)
-                                for r0 in range(2)
-                            ]
-                            jobs.append((sources, level1(r1, p1, pair, source_from, k_from, k_to)))
-                    for i in range(4):
-                        add_chore(len(jobs) - 1 + i, pick(2 * p1 + i // 2, 2 * r1 + i % 2))
-            level1_jobs = len(jobs)
+            def level1_group(r1, p1):
+                for pair in range(2):
+                    sources = [
+                        rows(2 * p1, r1, 2 * pair + qi, 1)[:, r0, 0, K_SIDE : K_SIDE + K_BLOCK].bitcast(F32)
+                        for qi in range(2)
+                        for r0 in range(2)
+                    ]
+                    jobs.append((sources, level1(r1, p1, pair, K_SIDE, K_SIDE, K_SIDE + K_BLOCK)))
+                for i in range(4):
+                    add_chore(len(jobs) - 1 + i, pick(2 * p1 + i // 2, 2 * r1 + i % 2))
 
-            for r1 in range(2):
-                for c in range(8 * HALF // CHUNK):
-                    chunk_job((r1 * 2) * 8 * HALF + c * CHUNK, (r1 * 2 + 1) * 8 * HALF + c * CHUNK)
+            def level2(buffer, half, r1, part, parts):
+                length = 8 * half // parts
+                chunk_jobs(buffer, (r1 * 2) * 8 * half + part * length, (r1 * 2 + 1) * 8 * half + part * length, length)
+
+            level1_group(0, 0)
+            level1_group(0, 1)
+            level2(work, HALF_A, 0, 0, 2)
+            level1_group(1, 0)
+            level2(work, HALF_A, 0, 1, 2)
+            level1_group(1, 1)
+            step = len(jobs) + 3
+            level2(work_b, HALF_B, 0, 0, 1)
+            level2(work, HALF_A, 1, 0, 1)
+            level2(work_b, HALF_B, 1, 0, 1)
             for r1 in range(2):
                 for u1 in range(2):
-                    for c in range(4 * HALF // CHUNK):
-                        start = (r1 * 2 + u1) * 8 * HALF
-                        chunk_job(start + c * CHUNK, start + 4 * HALF + c * CHUNK)
+                    for buffer, half in ((work, HALF_A), (work_b, HALF_B)):
+                        start = (r1 * 2 + u1) * 8 * half
+                        chunk_jobs(buffer, start, start + 4 * half, 4 * half)
 
-            step = level1_jobs + 3
             run_steps(0, step)
 
             gy_all = overlay.tile([PARTS, T, K * PACK], BF16, name="gy_all", offset=0, align_bytes=64)
@@ -247,10 +283,10 @@ def tile_iwht3layer_pa_kernel(tc, trans, weight, bias, grad_out, out):
 
             for i in range(2):
                 x_of[u_order[i]] = x_pool.tile([PARTS, SIDE, C, PACK], BF16, name="x", align_bytes=64)
-                add_chore(step + 3 + 8 * i, regroup_x(u_order[i], 0))
-                add_chore(step + 7 + 8 * i, regroup_x(u_order[i], 1))
-            add_chore(step + 7, lambda: load_x(u_order[2]))
-            add_chore(step + 15, lambda: load_x(u_order[3]))
+                add_chore(step + 5 + 12 * i, regroup_x(u_order[i], 0))
+                add_chore(step + 11 + 12 * i, regroup_x(u_order[i], 1))
+            add_chore(step + 11, lambda: load_x(u_order[2]))
+            add_chore(step + 23, lambda: load_x(u_order[3]))
 
             pool_b = overlay.tile([PARTS, 8 * UNIT_G], F32, name="pool_b", offset=102400)
             for u0 in range(2):
@@ -269,7 +305,7 @@ def tile_iwht3layer_pa_kernel(tc, trans, weight, bias, grad_out, out):
                         out=a_view[:, :, v1, :], in0=b_view[:, :, 0, :], in1=b_view[:, :, 1, :], op=SIGN_OP[v1]
                     )
 
-            with tc.psum_pool(name="psum_pe", bufs=2) as psum_pe:
+            with tc.psum_pool(name="psum_pe", bufs=1) as psum_pe:
                 pixels_of = {}
 
                 def pixels_to_partitions(o2):
@@ -315,8 +351,8 @@ def tile_iwht3layer_pa_kernel(tc, trans, weight, bias, grad_out, out):
                     path.append(transform(2 * o2))
                     path.append(transform(2 * o2 + 1))
                 for i in range(len(path)):
-                    add_chore(step + 2 * i, path[i])
-                path_end = step + 2 * len(path)
+                    add_chore(step + 3 * i // 2, path[i])
+                path_end = step + 3 * len(path) // 2
                 run_steps(step, path_end)
 
             for u0 in range(2):
@@ -355,20 +391,21 @@ def tile_iwht3layer_pa_kernel(tc, trans, weight, bias, grad_out, out):
 
             def sums(m):
                 u0, u1, v1 = pairs[m]
-                by_unit = work[:].rearrange("n (r1 s x) -> n r1 s x", r1=2, s=T)
                 a_unit = ((u1 * 2 + v1) * 2) * 2 + u0
                 b_unit = ((u1 * 2 + v1) * 2 + 1) * 2 + u0
-                for v0 in range(2):
-                    nc.vector.tensor_tensor(
-                        out=gy_all[:, first_t(m) + v0, K_SIDE * PACK : K * PACK].rearrange(
-                            "n (k r1 r0) -> n k r1 r0", r1=2, r0=2
-                        ),
-                        in0=by_unit[:, :, a_unit, :].rearrange("n r1 (k r0) -> n k r1 r0", r0=2),
-                        in1=by_unit[:, :, b_unit, :].rearrange("n r1 (k r0) -> n k r1 r0", r0=2),
-                        op=SIGN_OP[v0],
-                    )
+                for buffer, k_from, k_to in ((work, K_SIDE, K_SIDE + K_BLOCK), (work_b, K_SIDE + K_BLOCK, K)):
+                    by_unit = buffer[:].rearrange("n (r1 s x) -> n r1 s x", r1=2, s=T)
+                    for v0 in range(2):
+                        nc.vector.tensor_tensor(
+                            out=gy_all[:, first_t(m) + v0, k_from * PACK : k_to * PACK].rearrange(
+                                "n (k r1 r0) -> n k r1 r0", r1=2, r0=2
+                            ),
+                            in0=by_unit[:, :, a_unit, :].rearrange("n r1 (k r0) -> n k r1 r0", r0=2),
+                            in1=by_unit[:, :, b_unit, :].rearrange("n r1 (k r0) -> n k r1 r0", r0=2),
+                            op=SIGN_OP[v0],
+                        )
 
-            def multiply(m):
+            def multiply(m, pieces):
                 u = first_t(m) // SIDE
                 if u not in x_codes_of:
                     x_codes = overlay.tile(
@@ -386,11 +423,15 @@ def tile_iwht3layer_pa_kernel(tc, trans, weight, bias, grad_out, out):
                 x_codes, x_scales = x_codes_of[u]
                 gy_codes = overlay.tile([PARTS, 2 * K], U32, name="gy_codes", bufs=2, offset=75776, align_bytes=64)
                 gy_scales = overlay.tile([PARTS, 2 * K], U8, name="gy_scales", bufs=2, offset=83968, align_bytes=64)
-                nc.vector.quantize_mx(
-                    out=gy_codes[:].bitcast(E5M2_X4),
-                    scales=gy_scales[:],
-                    in_=gy_all[:, first_t(m) : first_t(m) + 2, :].rearrange("n v x -> n (v x)"),
-                )
+                width = 2 * K // pieces
+                for i in range(pieces):
+                    nc.vector.quantize_mx(
+                        out=gy_codes[:, i * width : (i + 1) * width].bitcast(E5M2_X4),
+                        scales=gy_scales[:, i * width : (i + 1) * width],
+                        in_=gy_all[:, first_t(m) : first_t(m) + 2, :].rearrange("n v x -> n (v x)")[
+                            :, i * width * PACK : (i + 1) * width * PACK
+                        ],
+                    )
                 banks = []
                 for v0 in range(2):
                     v = (first_t(m) + v0) % SIDE
@@ -414,7 +455,7 @@ def tile_iwht3layer_pa_kernel(tc, trans, weight, bias, grad_out, out):
                     result = overlay.tile([PARTS, C_HALVES, K], F32, name="result", bufs=3, offset=86016)
                     for h in range(C_HALVES):
                         bank = banks_of[m][v0 * C_HALVES + h]
-                        if vector_helps and h == 1:
+                        if vector_helps and v0 == 1:
                             nc.vector.tensor_scalar(
                                 out=result[:, h, :],
                                 in0=bank[:],
@@ -427,16 +468,21 @@ def tile_iwht3layer_pa_kernel(tc, trans, weight, bias, grad_out, out):
                     nc.sync.dma_start(out=out_dram[first_t(m) + v0], in_=result[:])
 
             count = len(pairs)
-            for m in range(count + 2):
-                if m < count:
-                    sums(m)
+            for m in range(count - 1):
+                sums(m)
                 if 0 <= m - 2:
-                    store(m - 2, m - 2 >= count - 1)
-                if 0 <= m - 1 < count:
-                    multiply(m - 1)
+                    store(m - 2, False)
+                if 0 <= m - 1:
+                    multiply(m - 1, 1)
                 if m == 0:
                     x_of[u_order[3]] = overlay.tile(
                         [PARTS, SIDE, C, PACK], BF16, name="x_fourth", offset=106496, align_bytes=64
                     )
                 if m in (0, 1):
                     regroup_x(u_order[3], m)()
+            store(count - 3, False)
+            multiply(count - 2, 1)
+            sums(count - 1)
+            store(count - 2, False)
+            multiply(count - 1, 2)
+            store(count - 1, True)

@@ -8,7 +8,10 @@ U8 = mybir.dt.uint8
 E4M3_X4 = mybir.dt.float8_e4m3fn_x4
 E5M2_X4 = mybir.dt.float8_e5m2_x4
 COPY = mybir.ActivationFunctionType.Copy
-SIGN_OP = (mybir.AluOpType.add, mybir.AluOpType.subtract)
+ADD = mybir.AluOpType.add
+SUBTRACT = mybir.AluOpType.subtract
+MULT = mybir.AluOpType.mult
+SIGN_OP = (ADD, SUBTRACT)
 
 PARTS = 128
 PACK = 4
@@ -22,18 +25,17 @@ C_HALVES = C // PARTS
 
 OCTET = PARTS // T
 OCTETS = 12
-K_TENSOR = OCTETS * OCTET
 K_POOL = 96
-K_SIDE = K_TENSOR + K_POOL
-K_VECTOR = K - K_SIDE
-UNIT = K_VECTOR * PACK
+K_HOP = 64
+K_TENSOR = OCTETS * OCTET
+K_POOL_END = K_TENSOR + K_POOL
+K_SUM = K_POOL_END + K_HOP
 UNIT_G = K_POOL * PACK
-K_BLOCK = 256
-HALF_A = K_BLOCK * 2
-HALF_B = (K_VECTOR - K_BLOCK) * 2
+ROW_H = K_HOP * 2
 BLOCK = 128
 BLOCKS = 4
 CHUNK = BLOCK * BLOCKS
+HALF = T // 2
 
 FLOPS = 2 * T * N * C * K
 BYTES = 2 * T * N * C + 2 * T * N * K + 4 * T * C * K
@@ -51,7 +53,16 @@ def transform_matrix(nc, pool, ident):
                 out=signed[:, :, bit, :], in0=halves[:, :, 0, :], in1=halves[:, :, 1, :], op=SIGN_OP[bit]
             )
         current = following
-    return current
+    ordered = pool.tile([PARTS, PARTS], BF16, name="matrix_ordered")
+    nc.vector.tensor_copy(
+        out=ordered[:].rearrange("n (u0 u1 x) -> n u0 u1 x", u0=2, u1=2),
+        in_=current[:].rearrange("n (u1 u0 x) -> n u0 u1 x", u0=2, u1=2),
+    )
+    return ordered
+
+
+def positive(s):
+    return [j for j in range(HALF) if sum(((j & s) >> b) & 1 for b in range(LEVELS - 1)) % 2 == 0]
 
 
 def tile_iwht3layer_pa_kernel(tc, trans, weight, bias, grad_out, out):
@@ -61,428 +72,428 @@ def tile_iwht3layer_pa_kernel(tc, trans, weight, bias, grad_out, out):
     x_dram = trans.rearrange("(u v) b i (jh r) c -> u (b i jh) v (r c)", v=SIDE, r=PACK)
     out_dram = out.rearrange("t (h m) k -> t m h k", h=C_HALVES)
 
-    u_order = [2 * u1 + u0 for u0 in range(2) for u1 in range(2)]
-
-    with tc.tile_pool(name="keep", bufs=1) as keep, tc.tile_pool(name="turned", bufs=3) as turned, tc.tile_pool(
+    with tc.tile_pool(name="keep", bufs=1) as keep, tc.tile_pool(name="turned", bufs=2) as turned, tc.tile_pool(
         name="pixel_pool", bufs=2
-    ) as pixel_pool, tc.tile_pool(name="x_pool", bufs=2) as x_pool, tc.tile_pool(
-        name="overlay", bufs=1
-    ) as overlay, tc.manual_schedule():
-        with tc.psum_pool(name="psum_t", bufs=3) as psum_t, tc.psum_pool(name="psum_a", bufs=3) as psum_a:
-            ident = keep.tile([PARTS, PARTS], BF16, name="ident")
-            make_identity(nc, ident[:])
-            ident_f = keep.tile([PARTS, PARTS], F32, name="ident_f")
-            make_identity(nc, ident_f[:])
-            warm = keep.tile([PARTS, 1], BF16, name="warm")
-            nc.scalar.copy(out=warm[:], in_=ident[:, 0:1])
-            matrix = transform_matrix(nc, keep, ident)
+    ) as pixel_pool, tc.tile_pool(name="overlay", bufs=1) as overlay, tc.psum_pool(
+        name="psum_a", bufs=3
+    ) as psum_a, tc.psum_pool(name="psum_b", bufs=2) as psum_b, tc.psum_pool(
+        name="psum_c", bufs=3
+    ) as psum_c, tc.manual_schedule():
+        ident = keep.tile([PARTS, PARTS], BF16, name="ident")
+        make_identity(nc, ident[:])
+        ident_f = keep.tile([PARTS, PARTS], F32, name="ident_f")
+        make_identity(nc, ident_f[:])
+        warm = keep.tile([PARTS, 1], BF16, name="warm")
+        nc.scalar.copy(out=warm[:], in_=ident[:, 0:1])
+        matrix = transform_matrix(nc, keep, ident)
 
-            work = keep.tile([PARTS, 2 * T * HALF_A], F32, name="work")
-            work_b = keep.tile([PARTS, 2 * T * HALF_B], F32, name="work_b")
-            pool_a = overlay.tile([PARTS, T * UNIT_G], F32, name="pool_a", offset=65536)
-            picked = overlay.tile([PARTS, PACK, OCTETS, T, OCTET], BF16, name="picked", offset=90112)
+        sums = [
+            overlay.tile([PARTS, 2, PACK, HALF, PARTS], F32, name="sums%d" % u0, offset=65536 + u0 * 32768)
+            for u0 in range(2)
+        ]
+        hop = overlay.tile([PARTS, 2 * T * ROW_H], F32, name="hop", offset=131072)
+        pool_a = overlay.tile([PARTS, T * UNIT_G], F32, name="pool_a", offset=147456)
+        picked = overlay.tile([PARTS, PACK, OCTETS, T, OCTET], BF16, name="picked", offset=192512)
 
-            jobs = []
-            st_of = {}
-            pa_of = {}
-
-            def turn(s):
-                pt = psum_t.tile([PARTS, BLOCKS, BLOCK], F32, name="pt")
-                for j in range(BLOCKS):
-                    nc.tensor.transpose(out=pt[:, j, :], in_=jobs[s][0][j], identity=ident_f[:])
-                st = turned.tile([PARTS, BLOCKS, BLOCK], F32, name="st")
-                nc.scalar.copy(out=st[:], in_=pt[:])
-                st_of[s] = st
-
-            def turn_back(s):
-                pa = psum_a.tile([PARTS, BLOCKS, BLOCK], F32, name="pa")
-                for j in range(BLOCKS):
-                    nc.tensor.transpose(out=pa[:, j, :], in_=st_of[s][:, j, :], identity=ident_f[:])
-                pa_of[s] = pa
-
-            def in_place(buffer, a0, b0):
-                def consume(pa):
-                    first = pa[:].rearrange("n j w -> n (j w)")
-                    nc.vector.tensor_tensor(
-                        out=buffer[:, a0 : a0 + CHUNK], in0=first, in1=buffer[:, b0 : b0 + CHUNK], op=SIGN_OP[0]
-                    )
-                    nc.vector.tensor_tensor(
-                        out=buffer[:, b0 : b0 + CHUNK], in0=first, in1=buffer[:, b0 : b0 + CHUNK], op=SIGN_OP[1]
-                    )
-
-                return consume
-
-            def chunk_jobs(buffer, a0, b0, length):
-                for c0 in range(0, length, CHUNK):
-                    sources = [buffer[:, a0 + c0 + j * BLOCK : a0 + c0 + (j + 1) * BLOCK] for j in range(BLOCKS)]
-                    jobs.append((sources, in_place(buffer, a0 + c0, b0 + c0)))
-
-            chores = {}
-
-            def add_chore(step, chore):
-                chores.setdefault(step, []).append(chore)
-
-            def run_steps(first, last):
-                for s in range(first, last):
-                    if 0 <= s - 2 < len(jobs):
-                        turn_back(s - 2)
-                    if s < len(jobs):
-                        turn(s)
-                    for chore in chores.get(s, []):
-                        chore()
-                    if 0 <= s - 3 < len(jobs):
-                        jobs[s - 3][1](pa_of[s - 3])
-
-            g = {}
-            for r1 in range(2):
-                for p1 in range(2):
-                    split = 2 if (r1, p1) == (0, 0) else 1
-                    for part in range(split):
-                        for p in (2 * p1, 2 * p1 + 1):
-                            q_count = SIDE // split
-                            tile = overlay.tile(
-                                [PARTS, 2, q_count, K],
-                                BF16,
-                                name="g%d%d%d" % (p, r1, part),
-                                offset=(SIDE * r1 + p) * 8192 + part * 4096,
-                            )
-                            for jh in range(2):
-                                nc.sync.dma_start(
-                                    out=tile[jh:PARTS:2].rearrange("n r0 q k -> n r0 (q k)"),
-                                    in_=g_dram[jh, p, r1][:, :, part * q_count * K : (part + 1) * q_count * K],
-                                )
-                            for q in range(part * q_count, (part + 1) * q_count):
-                                g[p, r1, q] = (tile, part * q_count)
-
-            def rows(p, r1, q_from, q_count):
-                tile, first_q = g[p, r1, q_from]
-                return tile[:, :, q_from - first_q : q_from - first_q + q_count, :]
-
-            def spans(r1, p1):
-                return ((0, 2), (2, 2)) if (r1, p1) == (0, 0) else ((0, SIDE),)
-
-            x_raw_of = {}
-            x_of = {}
-            x_codes_of = {}
-
-            def load_x(u):
-                x_raw = x_pool.tile([PARTS, SIDE, PACK, C], BF16, name="x_raw")
-                nc.sync.dma_start(out=x_raw[:].rearrange("n v r c -> n v (r c)"), in_=x_dram[u])
-                x_raw_of[u] = x_raw
-
-            def regroup_x(u, half):
-                def chore():
-                    nc.scalar.copy(
-                        out=x_of[u][:, 2 * half : 2 * half + 2],
-                        in_=x_raw_of[u][:, 2 * half : 2 * half + 2].rearrange("n v r c -> n v c r"),
-                    )
-
-                return chore
-
-            load_x(u_order[0])
-            load_x(u_order[1])
-
-            for r1 in range(2):
-                for p1 in range(2):
-                    for q_from, q_count in spans(r1, p1):
-                        a_rows = rows(2 * p1, r1, q_from, q_count)
-                        b_rows = rows(2 * p1 + 1, r1, q_from, q_count)
-                        for u0 in range(2):
-                            start = (u0 * 2 + p1) * SIDE * UNIT_G
-                            nc.gpsimd.tensor_tensor(
-                                out=pool_a[:, start : start + SIDE * UNIT_G]
-                                .rearrange("n (q r1 x) -> n q r1 x", q=SIDE, r1=2)[:, q_from : q_from + q_count, r1, :]
-                                .rearrange("n q (k r0) -> n q k r0", r0=2),
-                                in0=a_rows[:, :, :, K_TENSOR:K_SIDE].rearrange("n r0 q k -> n q k r0"),
-                                in1=b_rows[:, :, :, K_TENSOR:K_SIDE].rearrange("n r0 q k -> n q k r0"),
-                                op=SIGN_OP[u0],
-                            )
-                        for u0 in range(2):
-                            start = (r1 * 2 + p1) * 8 * HALF_B
-                            nc.gpsimd.tensor_tensor(
-                                out=work_b[:, start : start + 8 * HALF_B]
-                                .rearrange("n (q u x) -> n q u x", q=SIDE, u=2)[:, q_from : q_from + q_count, u0, :]
-                                .rearrange("n q (k r0) -> n q k r0", r0=2),
-                                in0=a_rows[:, :, :, K_SIDE + K_BLOCK : K].rearrange("n r0 q k -> n q k r0"),
-                                in1=b_rows[:, :, :, K_SIDE + K_BLOCK : K].rearrange("n r0 q k -> n q k r0"),
-                                op=SIGN_OP[u0],
-                            )
-
-            def level1(r1, p1, pair, source_from, k_from, k_to):
-                def consume(pa):
-                    first = pa[:].bitcast(BF16)[:, :, k_from - source_from : k_to - source_from].rearrange(
-                        "n (q r0) k -> n q k r0", r0=2
-                    )
-                    second = rows(2 * p1 + 1, r1, 2 * pair, 2)[:, :, :, k_from:k_to].rearrange(
-                        "n r0 q k -> n q k r0"
-                    )
-                    start = (r1 * 2 + p1) * 8 * HALF_A
-                    for u0 in range(2):
-                        nc.vector.tensor_tensor(
-                            out=work[:, start : start + 8 * HALF_A]
-                            .rearrange("n (q u x) -> n q u x", q=SIDE, u=2)[
-                                :, 2 * pair : 2 * pair + 2, u0, (k_from - K_SIDE) * 2 : (k_to - K_SIDE) * 2
-                            ]
-                            .rearrange("n q (k r0) -> n q k r0", r0=2),
-                            in0=first,
-                            in1=second,
-                            op=SIGN_OP[u0],
+        g = {}
+        for r1 in range(2):
+            for p1 in range(2):
+                split = 2 if (r1, p1) == (0, 0) else 1
+                for part in range(split):
+                    for p in (2 * p1, 2 * p1 + 1):
+                        q_count = SIDE // split
+                        tile = overlay.tile(
+                            [PARTS, 2, q_count, K],
+                            BF16,
+                            name="g%d%d%d" % (p, r1, part),
+                            offset=(SIDE * r1 + p) * 8192 + part * 4096,
                         )
+                        for jh in range(2):
+                            nc.sync.dma_start(
+                                out=tile[jh:PARTS:2].rearrange("n r0 q k -> n r0 (q k)"),
+                                in_=g_dram[jh, p, r1][:, :, part * q_count * K : (part + 1) * q_count * K],
+                            )
+                        for q in range(part * q_count, (part + 1) * q_count):
+                            g[p, r1, q] = (tile, part * q_count)
 
-                return consume
+        def rows(p, r1, q_from, q_count):
+            tile, first_q = g[p, r1, q_from]
+            return tile[:, :, q_from - first_q : q_from - first_q + q_count, :]
 
-            def pick(p, r):
-                def chore():
-                    for q_from, q_count in spans(r // 2, p // 2):
+        def spans(r1, p1):
+            return ((0, 2), (2, 2)) if (r1, p1) == (0, 0) else ((0, SIDE),)
+
+        def gpsimd_level1(r1, p1):
+            for q_from, q_count in spans(r1, p1):
+                a_rows = rows(2 * p1, r1, q_from, q_count)
+                b_rows = rows(2 * p1 + 1, r1, q_from, q_count)
+                for u0 in range(2):
+                    start = (u0 * 2 + p1) * SIDE * UNIT_G
+                    nc.gpsimd.tensor_tensor(
+                        out=pool_a[:, start : start + SIDE * UNIT_G]
+                        .rearrange("n (q r1 x) -> n q r1 x", q=SIDE, r1=2)[:, q_from : q_from + q_count, r1, :]
+                        .rearrange("n q (k r0) -> n q k r0", r0=2),
+                        in0=a_rows[:, :, :, K_TENSOR:K_POOL_END].rearrange("n r0 q k -> n q k r0"),
+                        in1=b_rows[:, :, :, K_TENSOR:K_POOL_END].rearrange("n r0 q k -> n q k r0"),
+                        op=SIGN_OP[u0],
+                    )
+                for u0 in range(2):
+                    start = (r1 * 2 + p1) * 8 * ROW_H
+                    nc.gpsimd.tensor_tensor(
+                        out=hop[:, start : start + 8 * ROW_H]
+                        .rearrange("n (q u x) -> n q u x", q=SIDE, u=2)[:, q_from : q_from + q_count, u0, :]
+                        .rearrange("n q (k r0) -> n q k r0", r0=2),
+                        in0=a_rows[:, :, :, K_POOL_END:K_SUM].rearrange("n r0 q k -> n q k r0"),
+                        in1=b_rows[:, :, :, K_POOL_END:K_SUM].rearrange("n r0 q k -> n q k r0"),
+                        op=SIGN_OP[u0],
+                    )
+
+        def pick(r1, p1):
+            for p in (2 * p1, 2 * p1 + 1):
+                for r0 in range(2):
+                    for q_from, q_count in spans(r1, p1):
                         nc.scalar.copy(
-                            out=picked[:, r, :, SIDE * p + q_from : SIDE * p + q_from + q_count, :].rearrange(
+                            out=picked[:, 2 * r1 + r0, :, SIDE * p + q_from : SIDE * p + q_from + q_count, :].rearrange(
                                 "n o q e -> n q o e"
                             ),
-                            in_=rows(p, r // 2, q_from, q_count)[:, r % 2, :, 0:K_TENSOR].rearrange(
+                            in_=rows(p, r1, q_from, q_count)[:, r0, :, 0:K_TENSOR].rearrange(
                                 "n q (o e) -> n q o e", e=OCTET
                             ),
                         )
 
-                return chore
-
-            def level1_group(r1, p1):
-                for pair in range(2):
-                    sources = [
-                        rows(2 * p1, r1, 2 * pair + qi, 1)[:, r0, 0, K_SIDE : K_SIDE + K_BLOCK].bitcast(F32)
-                        for qi in range(2)
-                        for r0 in range(2)
-                    ]
-                    jobs.append((sources, level1(r1, p1, pair, K_SIDE, K_SIDE, K_SIDE + K_BLOCK)))
-                for i in range(4):
-                    add_chore(len(jobs) - 1 + i, pick(2 * p1 + i // 2, 2 * r1 + i % 2))
-
-            def level2(buffer, half, r1, part, parts):
-                length = 8 * half // parts
-                chunk_jobs(buffer, (r1 * 2) * 8 * half + part * length, (r1 * 2 + 1) * 8 * half + part * length, length)
-
-            level1_group(0, 0)
-            level1_group(0, 1)
-            level2(work, HALF_A, 0, 0, 2)
-            level1_group(1, 0)
-            level2(work, HALF_A, 0, 1, 2)
-            level1_group(1, 1)
-            step = len(jobs) + 3
-            level2(work_b, HALF_B, 0, 0, 1)
-            level2(work, HALF_A, 1, 0, 1)
-            level2(work_b, HALF_B, 1, 0, 1)
-            for r1 in range(2):
-                for u1 in range(2):
-                    for buffer, half in ((work, HALF_A), (work_b, HALF_B)):
-                        start = (r1 * 2 + u1) * 8 * half
-                        chunk_jobs(buffer, start, start + 4 * half, 4 * half)
-
-            run_steps(0, step)
-
-            gy_all = overlay.tile([PARTS, T, K * PACK], BF16, name="gy_all", offset=0, align_bytes=64)
-            gy_by_bits = gy_all[:].rearrange("n (u1 u0 v1 v0) x -> n u1 u0 v1 v0 x", u1=2, u0=2, v1=2)
-
-            for i in range(2):
-                x_of[u_order[i]] = x_pool.tile([PARTS, SIDE, C, PACK], BF16, name="x", align_bytes=64)
-                add_chore(step + 5 + 12 * i, regroup_x(u_order[i], 0))
-                add_chore(step + 11 + 12 * i, regroup_x(u_order[i], 1))
-            add_chore(step + 11, lambda: load_x(u_order[2]))
-            add_chore(step + 23, lambda: load_x(u_order[3]))
-
-            pool_b = overlay.tile([PARTS, 8 * UNIT_G], F32, name="pool_b", offset=102400)
-            for u0 in range(2):
-                half = pool_a[:, u0 * 8 * UNIT_G : (u0 + 1) * 8 * UNIT_G]
-                for u1 in range(2):
-                    nc.gpsimd.tensor_tensor(
-                        out=pool_b[:, u1 * 4 * UNIT_G : (u1 + 1) * 4 * UNIT_G],
-                        in0=half[:, 0 : 4 * UNIT_G],
-                        in1=half[:, 4 * UNIT_G : 8 * UNIT_G],
-                        op=SIGN_OP[u1],
+        def summed_level1(r1, p1, r0):
+            banks = []
+            for p, pool, name in ((2 * p1 + 1, psum_b, "bank_b"), (2 * p1, psum_a, "bank_a")):
+                bank = pool.tile([PARTS, SIDE, PARTS], F32, name=name)
+                for q in range(SIDE):
+                    nc.tensor.transpose(
+                        out=bank[:, q, :], in_=rows(p, r1, q, 1)[:, r0, 0, K_SUM:K].bitcast(F32), identity=ident_f[:]
                     )
-                b_view = pool_b[:].rearrange("n (u q1 x) -> n u q1 x", u=2, q1=2)
-                a_view = half.rearrange("n (u v x) -> n u v x", u=2, v=2)
+                banks.append(bank)
+            second = overlay.tile([PARTS, SIDE, PARTS], F32, name="second", bufs=2, offset=204800)
+            nc.scalar.copy(out=second[:], in_=banks[0][:])
+            for u0 in range(2):
+                nc.vector.tensor_tensor(
+                    out=sums[u0][:, :, 2 * r1 + r0, SIDE * p1 : SIDE * p1 + SIDE, :],
+                    in0=banks[1][:].bitcast(BF16).rearrange("w q (n e) -> w e q n", e=2),
+                    in1=second[:].bitcast(BF16).rearrange("w q (n e) -> w e q n", e=2),
+                    op=SIGN_OP[u0],
+                )
+
+        for r1 in range(2):
+            for p1 in range(2):
+                gpsimd_level1(r1, p1)
+                for r0 in range(2):
+                    summed_level1(r1, p1, r0)
+                pick(r1, p1)
+
+        gy = [
+            overlay.tile([PARTS, HALF, K * PACK], BF16, name="gy%d" % u0, offset=u0 * 32768, align_bytes=64)
+            for u0 in range(2)
+        ]
+
+        pool_b = overlay.tile([PARTS, 8 * UNIT_G], F32, name="pool_b", offset=172032)
+        for u0 in range(2):
+            half = pool_a[:, u0 * 8 * UNIT_G : (u0 + 1) * 8 * UNIT_G]
+            for u1 in range(2):
+                nc.gpsimd.tensor_tensor(
+                    out=pool_b[:, u1 * 4 * UNIT_G : (u1 + 1) * 4 * UNIT_G],
+                    in0=half[:, 0 : 4 * UNIT_G],
+                    in1=half[:, 4 * UNIT_G : 8 * UNIT_G],
+                    op=SIGN_OP[u1],
+                )
+            for u1 in range(2):
+                q_pairs = pool_b[:, u1 * 4 * UNIT_G : (u1 + 1) * 4 * UNIT_G].rearrange("n (q1 x) -> n q1 x", q1=2)
+                by_v1 = half[:, u1 * 4 * UNIT_G : (u1 + 1) * 4 * UNIT_G].rearrange(
+                    "n (v1 q0 x) -> n v1 q0 x", v1=2, q0=2
+                )
                 for v1 in range(2):
                     nc.gpsimd.tensor_tensor(
-                        out=a_view[:, :, v1, :], in0=b_view[:, :, 0, :], in1=b_view[:, :, 1, :], op=SIGN_OP[v1]
+                        out=by_v1[:, v1].rearrange("n q0 x -> n (q0 x)"),
+                        in0=q_pairs[:, 0, :],
+                        in1=q_pairs[:, 1, :],
+                        op=SIGN_OP[v1],
                     )
-
-            with tc.psum_pool(name="psum_pe", bufs=1) as psum_pe:
-                pixels_of = {}
-
-                def pixels_to_partitions(o2):
-                    def chore():
-                        pix_ps = psum_pe.tile([PARTS, 2, PACK, PARTS], BF16, name="pix_ps")
-                        for i in range(2):
-                            for r in range(PACK):
-                                nc.tensor.transpose(
-                                    out=pix_ps[:, i, r, :],
-                                    in_=picked[:, r, 2 * o2 + i, :, :].rearrange("n a e -> n (a e)"),
-                                    identity=ident[:],
-                                )
-                        pixels = pixel_pool.tile([PARTS, 2, PACK, PARTS], BF16, name="pixels")
-                        nc.scalar.copy(out=pixels[:], in_=pix_ps[:])
-                        pixels_of[o2] = pixels
-
-                    return chore
-
-                def transform(o):
-                    def chore():
-                        coef_ps = psum_pe.tile([PARTS, PACK, PARTS], F32, name="coef_ps")
-                        for r in range(PACK):
-                            nc.tensor.matmul(
-                                out=coef_ps[:, r, :],
-                                lhsT=pixels_of[o // 2][:, o % 2, r, :],
-                                rhs=matrix[:],
-                                start=True,
-                                stop=True,
-                            )
-                        nc.scalar.copy(
-                            out=gy_all[:, :, o * OCTET * PACK : (o + 1) * OCTET * PACK].rearrange(
-                                "n t (e r) -> n t e r", r=PACK
-                            ),
-                            in_=coef_ps[:].rearrange("n r (t e) -> n t e r", e=OCTET),
-                        )
-
-                    return chore
-
-                path = [pixels_to_partitions(0)]
-                for o2 in range(OCTETS // 2):
-                    if o2 + 1 < OCTETS // 2:
-                        path.append(pixels_to_partitions(o2 + 1))
-                    path.append(transform(2 * o2))
-                    path.append(transform(2 * o2 + 1))
-                for i in range(len(path)):
-                    add_chore(step + 3 * i // 2, path[i])
-                path_end = step + 3 * len(path) // 2
-                run_steps(step, path_end)
-
-            for u0 in range(2):
-                a_pairs = pool_a[:, u0 * 8 * UNIT_G : (u0 + 1) * 8 * UNIT_G].rearrange(
-                    "n (u v q0 x) -> n u v q0 x", u=2, v=2, q0=2
-                )
-                for u1 in range(2):
-                    for v1 in range(2):
-                        for v0 in range(2):
-                            nc.gpsimd.tensor_tensor(
-                                out=gy_by_bits[:, u1, u0, v1, v0, K_TENSOR * PACK : K_SIDE * PACK].rearrange(
-                                    "n (k r1 r0) -> n k r1 r0", r1=2, r0=2
-                                ),
-                                in0=a_pairs[:, u1, v1, 0, :].rearrange("n (r1 k r0) -> n k r1 r0", r1=2, r0=2),
-                                in1=a_pairs[:, u1, v1, 1, :].rearrange("n (r1 k r0) -> n k r1 r0", r1=2, r0=2),
-                                op=SIGN_OP[v0],
-                            )
-
-            def open_third():
-                x_of[u_order[2]] = overlay.tile(
-                    [PARTS, SIDE, C, PACK], BF16, name="x_third", offset=98304, align_bytes=64
-                )
-
-            add_chore(path_end, open_third)
-            add_chore(path_end, regroup_x(u_order[2], 0))
-            add_chore(path_end + 3, regroup_x(u_order[2], 1))
-            run_steps(path_end, len(jobs) + 3)
-
-        with tc.psum_pool(name="acc_pool", bufs=8) as acc_pool:
-            pairs = [(u0, u1, v1) for u0 in range(2) for u1 in range(2) for v1 in range(2)]
-            banks_of = {}
-
-            def first_t(m):
-                u0, u1, v1 = pairs[m]
-                return SIDE * (2 * u1 + u0) + 2 * v1
-
-            def sums(m):
-                u0, u1, v1 = pairs[m]
-                a_unit = ((u1 * 2 + v1) * 2) * 2 + u0
-                b_unit = ((u1 * 2 + v1) * 2 + 1) * 2 + u0
-                for buffer, k_from, k_to in ((work, K_SIDE, K_SIDE + K_BLOCK), (work_b, K_SIDE + K_BLOCK, K)):
-                    by_unit = buffer[:].rearrange("n (r1 s x) -> n r1 s x", r1=2, s=T)
+                for v1 in range(2):
                     for v0 in range(2):
-                        nc.vector.tensor_tensor(
-                            out=gy_all[:, first_t(m) + v0, k_from * PACK : k_to * PACK].rearrange(
+                        nc.gpsimd.tensor_tensor(
+                            out=gy[u0][:, 4 * u1 + 2 * v1 + v0, K_TENSOR * PACK : K_POOL_END * PACK].rearrange(
                                 "n (k r1 r0) -> n k r1 r0", r1=2, r0=2
                             ),
-                            in0=by_unit[:, :, a_unit, :].rearrange("n r1 (k r0) -> n k r1 r0", r0=2),
-                            in1=by_unit[:, :, b_unit, :].rearrange("n r1 (k r0) -> n k r1 r0", r0=2),
+                            in0=by_v1[:, v1, 0].rearrange("n (r1 k r0) -> n k r1 r0", r1=2, r0=2),
+                            in1=by_v1[:, v1, 1].rearrange("n (r1 k r0) -> n k r1 r0", r1=2, r0=2),
                             op=SIGN_OP[v0],
                         )
 
-            def multiply(m, pieces):
-                u = first_t(m) // SIDE
-                if u not in x_codes_of:
-                    x_codes = overlay.tile(
-                        [PARTS, SIDE * C], U32, name="x_codes", bufs=2, offset=65536, align_bytes=64
-                    )
-                    x_scales = overlay.tile(
-                        [PARTS, SIDE * C], U8, name="x_scales", bufs=2, offset=73728, align_bytes=64
-                    )
-                    nc.vector.quantize_mx(
-                        out=x_codes[:].bitcast(E4M3_X4),
-                        scales=x_scales[:],
-                        in_=x_of[u][:].rearrange("n v c r -> n (v c r)"),
-                    )
-                    x_codes_of[u] = (x_codes, x_scales)
-                x_codes, x_scales = x_codes_of[u]
-                gy_codes = overlay.tile([PARTS, 2 * K], U32, name="gy_codes", bufs=2, offset=75776, align_bytes=64)
-                gy_scales = overlay.tile([PARTS, 2 * K], U8, name="gy_scales", bufs=2, offset=83968, align_bytes=64)
-                width = 2 * K // pieces
-                for i in range(pieces):
-                    nc.vector.quantize_mx(
-                        out=gy_codes[:, i * width : (i + 1) * width].bitcast(E5M2_X4),
-                        scales=gy_scales[:, i * width : (i + 1) * width],
-                        in_=gy_all[:, first_t(m) : first_t(m) + 2, :].rearrange("n v x -> n (v x)")[
-                            :, i * width * PACK : (i + 1) * width * PACK
-                        ],
-                    )
-                banks = []
-                for v0 in range(2):
-                    v = (first_t(m) + v0) % SIDE
-                    for h in range(C_HALVES):
-                        column = v * C + h * PARTS
-                        acc = acc_pool.tile([PARTS, K], F32, name="acc")
-                        nc.tensor.matmul_mx(
-                            out=acc[:],
-                            lhsT=x_codes[:, column : column + PARTS].bitcast(E4M3_X4),
-                            lhsT_scale=x_scales[:, column : column + PARTS],
-                            rhs=gy_codes[:, v0 * K : (v0 + 1) * K].bitcast(E5M2_X4),
-                            rhs_scale=gy_scales[:, v0 * K : (v0 + 1) * K],
-                            start=True,
-                            stop=True,
+        pixels_of = {}
+
+        def pixels_to_partitions(o2):
+            def chore():
+                pix_ps = psum_b.tile([PARTS, 2, PACK, PARTS], BF16, name="bank_b")
+                for i in range(2):
+                    for r in range(PACK):
+                        nc.tensor.transpose(
+                            out=pix_ps[:, i, r, :],
+                            in_=picked[:, r, 2 * o2 + i, :, :].rearrange("n a e -> n (a e)"),
+                            identity=ident[:],
                         )
-                        banks.append(acc)
-                banks_of[m] = banks
+                pixels = pixel_pool.tile([PARTS, 2, PACK, PARTS], BF16, name="pixels")
+                nc.scalar.copy(out=pixels[:], in_=pix_ps[:])
+                pixels_of[o2] = pixels
 
-            def store(m, vector_helps):
-                for v0 in range(2):
-                    result = overlay.tile([PARTS, C_HALVES, K], F32, name="result", bufs=3, offset=86016)
-                    for h in range(C_HALVES):
-                        bank = banks_of[m][v0 * C_HALVES + h]
-                        if vector_helps and v0 == 1:
-                            nc.vector.tensor_scalar(
-                                out=result[:, h, :],
-                                in0=bank[:],
-                                scalar1=1.0 / T,
-                                scalar2=None,
-                                op0=mybir.AluOpType.mult,
-                            )
-                        else:
-                            nc.scalar.activation(out=result[:, h, :], in_=bank[:], func=COPY, scale=1.0 / T)
-                    nc.sync.dma_start(out=out_dram[first_t(m) + v0], in_=result[:])
+            return chore
 
-            count = len(pairs)
-            for m in range(count - 1):
-                sums(m)
-                if 0 <= m - 2:
-                    store(m - 2, False)
-                if 0 <= m - 1:
-                    multiply(m - 1, 1)
-                if m == 0:
-                    x_of[u_order[3]] = overlay.tile(
-                        [PARTS, SIDE, C, PACK], BF16, name="x_fourth", offset=106496, align_bytes=64
+        def transform(o):
+            def chore():
+                coef_ps = psum_c.tile([PARTS, PACK, PARTS], F32, name="bank_c")
+                for r in range(PACK):
+                    nc.tensor.matmul(
+                        out=coef_ps[:, r, :],
+                        lhsT=pixels_of[o // 2][:, o % 2, r, :],
+                        rhs=matrix[:],
+                        start=True,
+                        stop=True,
                     )
-                if m in (0, 1):
-                    regroup_x(u_order[3], m)()
-            store(count - 3, False)
-            multiply(count - 2, 1)
-            sums(count - 1)
-            store(count - 2, False)
-            multiply(count - 1, 2)
-            store(count - 1, True)
+                for u0 in range(2):
+                    nc.scalar.copy(
+                        out=gy[u0][:, :, o * OCTET * PACK : (o + 1) * OCTET * PACK].rearrange(
+                            "n s (e r) -> n s e r", r=PACK
+                        ),
+                        in_=coef_ps[:, :, u0 * HALF * OCTET : (u0 + 1) * HALF * OCTET].rearrange(
+                            "n r (s e) -> n s e r", e=OCTET
+                        ),
+                    )
+
+            return chore
+
+        hop_jobs = []
+        for r1 in range(2):
+            for part in range(2):
+                hop_jobs.append(((r1 * 2) * 8 * ROW_H + part * CHUNK, (r1 * 2 + 1) * 8 * ROW_H + part * CHUNK))
+        for r1 in range(2):
+            for u1 in range(2):
+                start = (r1 * 2 + u1) * 8 * ROW_H
+                hop_jobs.append((start, start + CHUNK))
+        turned_of = {}
+
+        def hop_step(s):
+            def chore():
+                if 0 <= s - 2 < len(hop_jobs):
+                    a0, b0 = hop_jobs[s - 2]
+                    back = psum_a.tile([PARTS, BLOCKS, BLOCK], F32, name="bank_a")
+                    for j in range(BLOCKS):
+                        nc.tensor.transpose(out=back[:, j, :], in_=turned_of[s - 2][:, j, :], identity=ident_f[:])
+                    first = back[:].rearrange("n j w -> n (j w)")
+                    for target, op in ((a0, ADD), (b0, SUBTRACT)):
+                        nc.vector.tensor_tensor(
+                            out=hop[:, target : target + CHUNK], in0=first, in1=hop[:, b0 : b0 + CHUNK], op=op
+                        )
+                if s < len(hop_jobs):
+                    a0 = hop_jobs[s][0]
+                    forth = psum_b.tile([PARTS, BLOCKS, BLOCK], F32, name="bank_b")
+                    for j in range(BLOCKS):
+                        nc.tensor.transpose(
+                            out=forth[:, j, :], in_=hop[:, a0 + j * BLOCK : a0 + (j + 1) * BLOCK], identity=ident_f[:]
+                        )
+                    st = turned.tile([PARTS, BLOCKS, BLOCK], F32, name="st")
+                    nc.scalar.copy(out=st[:], in_=forth[:])
+                    turned_of[s] = st
+
+            return chore
+
+        whole_of = {}
+
+        def summed(u0, s, e):
+            def piece():
+                bank = psum_a.tile([PARTS, PACK, PARTS], F32, name="bank_a")
+                members = positive(s)
+                for r in range(PACK):
+                    for j in members:
+                        nc.tensor.matmul(
+                            out=bank[:, r, :],
+                            lhsT=sums[u0][:, e, r, j, :],
+                            rhs=ident_f[:],
+                            is_transpose=True,
+                            start=j == members[0],
+                            stop=j == members[-1],
+                        )
+                column = (K_SUM + e * PARTS) * PACK
+                target = gy[u0][:, s, column : column + PARTS * PACK].rearrange("n (w r) -> n w r", r=PACK)
+                source = bank[:].rearrange("n r w -> n w r")
+                if s == 0:
+                    whole = overlay.tile([PARTS, PARTS, PACK], F32, name="whole", bufs=4, offset=184320)
+                    nc.scalar.copy(out=whole[:], in_=source)
+                    nc.scalar.copy(out=target, in_=source)
+                    whole_of[u0, e] = whole
+                else:
+                    nc.vector.scalar_tensor_tensor(
+                        out=target, in0=source, scalar=2.0, in1=whole_of[u0, e][:], op0=MULT, op1=SUBTRACT
+                    )
+
+            return piece
+
+        x_raw_of = {}
+        x_of = {}
+        x_codes_of = {}
+
+        def load_x(u, part):
+            def chore():
+                x_raw = overlay.tile([PARTS, 2, PACK, C], BF16, name="x_raw", offset=200704)
+                nc.sync.dma_start(
+                    out=x_raw[:].rearrange("n v r c -> n v (r c)"), in_=x_dram[u][:, 2 * part : 2 * part + 2]
+                )
+                x_raw_of[u, part] = x_raw
+
+            return chore
+
+        def regroup_x(u, part):
+            def chore():
+                if part == 0:
+                    x_of[u] = overlay.tile([PARTS, SIDE, C, PACK], BF16, name="x", offset=192512, align_bytes=64)
+                nc.scalar.copy(
+                    out=x_of[u][:, 2 * part : 2 * part + 2], in_=x_raw_of[u, part][:].rearrange("n v r c -> n v c r")
+                )
+
+            return chore
+
+        def quantise_x(u):
+            def chore():
+                x_codes = overlay.tile([PARTS, SIDE * C], U32, name="x_codes", bufs=2, offset=215040, align_bytes=64)
+                x_scales = overlay.tile([PARTS, SIDE * C], U8, name="x_scales", bufs=2, offset=223232, align_bytes=64)
+                nc.vector.quantize_mx(
+                    out=x_codes[:].bitcast(E4M3_X4),
+                    scales=x_scales[:],
+                    in_=x_of[u][:].rearrange("n v c r -> n (v c r)"),
+                )
+                x_codes_of[u] = (x_codes, x_scales)
+
+            return chore
+
+        codes_of = {}
+        banks_of = {}
+
+        def place(m):
+            return m // 4, 2 * (m % 4)
+
+        def u_of(m):
+            u0, s = place(m)
+            return 2 * (s // SIDE) + u0
+
+        def hop_sums(m):
+            u0, s = place(m)
+            u1, v1 = s // SIDE, s % SIDE // 2
+            by_unit = hop[:].rearrange("n (r1 s x) -> n r1 s x", r1=2, s=T)
+            a_unit = ((u1 * 2 + v1) * 2) * 2 + u0
+            b_unit = ((u1 * 2 + v1) * 2 + 1) * 2 + u0
+            for v0 in range(2):
+                nc.vector.tensor_tensor(
+                    out=gy[u0][:, s + v0, K_POOL_END * PACK : K_SUM * PACK].rearrange(
+                        "n (k r1 r0) -> n k r1 r0", r1=2, r0=2
+                    ),
+                    in0=by_unit[:, :, a_unit, :].rearrange("n r1 (k r0) -> n k r1 r0", r0=2),
+                    in1=by_unit[:, :, b_unit, :].rearrange("n r1 (k r0) -> n k r1 r0", r0=2),
+                    op=SIGN_OP[v0],
+                )
+
+        def quantise(m, pieces):
+            u0, s = place(m)
+            gy_codes = overlay.tile([PARTS, 2 * K], U32, name="gy_codes", bufs=2, offset=204800, align_bytes=64)
+            gy_scales = overlay.tile([PARTS, 2 * K], U8, name="gy_scales", bufs=2, offset=212992, align_bytes=64)
+            width = 2 * K // pieces
+            for i in range(pieces):
+                nc.vector.quantize_mx(
+                    out=gy_codes[:, i * width : (i + 1) * width].bitcast(E5M2_X4),
+                    scales=gy_scales[:, i * width : (i + 1) * width],
+                    in_=gy[u0][:, s : s + 2, :].rearrange("n v x -> n (v x)")[
+                        :, i * width * PACK : (i + 1) * width * PACK
+                    ],
+                )
+            codes_of[m] = (gy_codes, gy_scales)
+
+        def multiply(m, v0):
+            u0, s = place(m)
+            x_codes, x_scales = x_codes_of[u_of(m)]
+            gy_codes, gy_scales = codes_of[m]
+            v = (s + v0) % SIDE
+            for h in range(C_HALVES):
+                column = v * C + h * PARTS
+                acc = psum_c.tile([PARTS, K], F32, name="bank_c")
+                nc.tensor.matmul_mx(
+                    out=acc[:],
+                    lhsT=x_codes[:, column : column + PARTS].bitcast(E4M3_X4),
+                    lhsT_scale=x_scales[:, column : column + PARTS],
+                    rhs=gy_codes[:, v0 * K : (v0 + 1) * K].bitcast(E5M2_X4),
+                    rhs_scale=gy_scales[:, v0 * K : (v0 + 1) * K],
+                    start=True,
+                    stop=True,
+                )
+                banks_of[m, v0, h] = acc
+
+        def store(m, v0, vector_halves):
+            u0, s = place(m)
+            result = overlay.tile([PARTS, C_HALVES, K], F32, name="result", bufs=2, offset=225280)
+            for h in range(C_HALVES):
+                bank = banks_of[m, v0, h]
+                for target, source in (
+                    (result[:, h, 0:K_SUM], bank[:, 0:K_SUM]),
+                    (
+                        result[:, h, K_SUM:K].rearrange("n (w e) -> n w e", e=2),
+                        bank[:, K_SUM:K].rearrange("n (e w) -> n w e", e=2),
+                    ),
+                ):
+                    if h in vector_halves:
+                        nc.vector.tensor_scalar(out=target, in0=source, scalar1=1.0 / T, scalar2=None, op0=MULT)
+                    else:
+                        nc.scalar.activation(out=target, in_=source, func=COPY, scale=1.0 / T)
+            nc.sync.dma_start(out=out_dram[SIDE * u_of(m) + (s + v0) % SIDE], in_=result[:])
+
+        def pair_quantise(m):
+            def chore():
+                hop_sums(m)
+                quantise(m, 1)
+
+            return chore
+
+        def pair_multiply(m):
+            def chore():
+                for v0 in range(2):
+                    multiply(m, v0)
+                    store(m, v0, ())
+
+            return chore
+
+        units = [(u0, s, e) for u0 in range(2) for s in range(HALF) for e in range(2)]
+        chores = {}
+
+        def add_chore(slot, chore):
+            chores.setdefault(slot, []).append(chore)
+
+        path = [pixels_to_partitions(0)]
+        for o2 in range(OCTETS // 2):
+            if o2 + 1 < OCTETS // 2:
+                path.append(pixels_to_partitions(o2 + 1))
+            path.append(transform(2 * o2))
+            path.append(transform(2 * o2 + 1))
+        for i in range(len(path)):
+            add_chore(i // 2, path[i])
+        for s in range(len(hop_jobs) + 2):
+            add_chore(4 + s, hop_step(s))
+        for u, slots in ((0, (7, 9, 11, 13)), (2, (11, 14, 16, 17)), (1, (16, 18, 20, 22)), (3, (20, 23, 25, 27))):
+            add_chore(slots[3], quantise_x(u))
+            add_chore(slots[1], regroup_x(u, 0))
+            add_chore(slots[1], load_x(u, 1))
+            add_chore(slots[2], regroup_x(u, 1))
+            add_chore(slots[0], load_x(u, 0))
+        for m, slot in ((0, 14), (1, 16), (2, 18), (3, 20), (4, 24), (5, 26), (6, 28)):
+            add_chore(slot, pair_quantise(m))
+            add_chore(slot + 1, pair_multiply(m))
+        add_chore(29, lambda: hop_sums(7))
+
+        for slot in range(len(units)):
+            summed(*units[slot])()
+            for chore in chores.get(slot, []):
+                chore()
+        quantise(7, 2)
+        for v0 in range(2):
+            multiply(7, v0)
+            store(7, v0, (1,))

@@ -180,11 +180,36 @@ def tile_iwht3layer_pa_kernel(tc, trans, weight, bias, grad_out, out):
                     op=SIGN_OP[u0],
                 )
 
+        ones = overlay.tile([PARTS, CHUNK * PACK], BF16, name="ones", offset=225280, align_bytes=64)
+        nc.gpsimd.memset(ones[:], 1.0)
+        idle_rhs = overlay.tile([PARTS, CHUNK], U32, name="idle_rhs", offset=215040, align_bytes=64)
+        idle_rhs_scales = overlay.tile([PARTS, CHUNK], U8, name="idle_rhs_scales", offset=217088, align_bytes=64)
+        idle_lhs = overlay.tile([PARTS, PARTS], U32, name="idle_lhs", offset=217600, align_bytes=64)
+        idle_lhs_scales = overlay.tile([PARTS, PARTS], U8, name="idle_lhs_scales", offset=218112, align_bytes=64)
+        nc.vector.quantize_mx(out=idle_rhs[:].bitcast(E5M2_X4), scales=idle_rhs_scales[:], in_=ones[:])
+        nc.vector.quantize_mx(
+            out=idle_lhs[:].bitcast(E4M3_X4), scales=idle_lhs_scales[:], in_=ones[:, 0 : PARTS * PACK]
+        )
+        idle_bank = psum_c.tile([PARTS, CHUNK], F32, name="bank_c")
+
+        def idle_pass():
+            nc.tensor.matmul_mx(
+                out=idle_bank[:],
+                lhsT=idle_lhs[:].bitcast(E4M3_X4),
+                lhsT_scale=idle_lhs_scales[:],
+                rhs=idle_rhs[:].bitcast(E5M2_X4),
+                rhs_scale=idle_rhs_scales[:],
+                start=True,
+                stop=True,
+            )
+
         for r1 in range(2):
             for p1 in range(2):
                 gpsimd_level1(r1, p1)
                 for r0 in range(2):
                     summed_level1(r1, p1, r0)
+                    for i in range(3):
+                        idle_pass()
                 pick(r1, p1)
 
         gy = [
@@ -226,6 +251,11 @@ def tile_iwht3layer_pa_kernel(tc, trans, weight, bias, grad_out, out):
                         )
 
         pixels_of = {}
+        waiting = overlay.tile([PARTS, HALF, K_TENSOR * PACK], BF16, name="waiting", offset=208896, align_bytes=64)
+        targets = (gy[0], waiting)
+
+        def move_waiting():
+            nc.vector.tensor_copy(out=gy[1][:, :, 0 : K_TENSOR * PACK], in_=waiting[:])
 
         def pixels_to_partitions(o2):
             def chore():
@@ -256,7 +286,7 @@ def tile_iwht3layer_pa_kernel(tc, trans, weight, bias, grad_out, out):
                     )
                 for u0 in range(2):
                     nc.scalar.copy(
-                        out=gy[u0][:, :, o * OCTET * PACK : (o + 1) * OCTET * PACK].rearrange(
+                        out=targets[u0][:, :, o * OCTET * PACK : (o + 1) * OCTET * PACK].rearrange(
                             "n s (e r) -> n s e r", r=PACK
                         ),
                         in_=coef_ps[:, :, u0 * HALF * OCTET : (u0 + 1) * HALF * OCTET].rearrange(
@@ -303,11 +333,13 @@ def tile_iwht3layer_pa_kernel(tc, trans, weight, bias, grad_out, out):
 
         whole_of = {}
 
-        def summed(u0, s, e):
+        def summed(u0, s, e, between):
             def piece():
                 bank = psum_a.tile([PARTS, PACK, PARTS], F32, name="bank_a")
                 members = positive(s)
                 for r in range(PACK):
+                    if s == 0 and r == PACK // 2:
+                        between()
                     for j in members:
                         nc.tensor.matmul(
                             out=bank[:, r, :],
@@ -371,6 +403,7 @@ def tile_iwht3layer_pa_kernel(tc, trans, weight, bias, grad_out, out):
 
         codes_of = {}
         banks_of = {}
+        result_of = {}
 
         def place(m):
             return m // 4, 2 * (m % 4)
@@ -410,57 +443,42 @@ def tile_iwht3layer_pa_kernel(tc, trans, weight, bias, grad_out, out):
                 )
             codes_of[m] = (gy_codes, gy_scales)
 
-        def multiply(m, v0):
+        def multiply(m, v0, h):
             u0, s = place(m)
             x_codes, x_scales = x_codes_of[u_of(m)]
             gy_codes, gy_scales = codes_of[m]
-            v = (s + v0) % SIDE
-            for h in range(C_HALVES):
-                column = v * C + h * PARTS
-                acc = psum_c.tile([PARTS, K], F32, name="bank_c")
-                nc.tensor.matmul_mx(
-                    out=acc[:],
-                    lhsT=x_codes[:, column : column + PARTS].bitcast(E4M3_X4),
-                    lhsT_scale=x_scales[:, column : column + PARTS],
-                    rhs=gy_codes[:, v0 * K : (v0 + 1) * K].bitcast(E5M2_X4),
-                    rhs_scale=gy_scales[:, v0 * K : (v0 + 1) * K],
-                    start=True,
-                    stop=True,
-                )
-                banks_of[m, v0, h] = acc
+            column = (s + v0) % SIDE * C + h * PARTS
+            acc = psum_c.tile([PARTS, K], F32, name="bank_c")
+            nc.tensor.matmul_mx(
+                out=acc[:],
+                lhsT=x_codes[:, column : column + PARTS].bitcast(E4M3_X4),
+                lhsT_scale=x_scales[:, column : column + PARTS],
+                rhs=gy_codes[:, v0 * K : (v0 + 1) * K].bitcast(E5M2_X4),
+                rhs_scale=gy_scales[:, v0 * K : (v0 + 1) * K],
+                start=True,
+                stop=True,
+            )
+            banks_of[m, v0, h] = acc
 
-        def store(m, v0, vector_halves):
+        def store(m, v0, h, on_vector):
             u0, s = place(m)
-            result = overlay.tile([PARTS, C_HALVES, K], F32, name="result", bufs=2, offset=225280)
-            for h in range(C_HALVES):
-                bank = banks_of[m, v0, h]
-                for target, source in (
-                    (result[:, h, 0:K_SUM], bank[:, 0:K_SUM]),
-                    (
-                        result[:, h, K_SUM:K].rearrange("n (w e) -> n w e", e=2),
-                        bank[:, K_SUM:K].rearrange("n (e w) -> n w e", e=2),
-                    ),
-                ):
-                    if h in vector_halves:
-                        nc.vector.tensor_scalar(out=target, in0=source, scalar1=1.0 / T, scalar2=None, op0=MULT)
-                    else:
-                        nc.scalar.activation(out=target, in_=source, func=COPY, scale=1.0 / T)
-            nc.sync.dma_start(out=out_dram[SIDE * u_of(m) + (s + v0) % SIDE], in_=result[:])
-
-        def pair_quantise(m):
-            def chore():
-                hop_sums(m)
-                quantise(m, 1)
-
-            return chore
-
-        def pair_multiply(m):
-            def chore():
-                for v0 in range(2):
-                    multiply(m, v0)
-                    store(m, v0, ())
-
-            return chore
+            if h == 0:
+                result_of[m, v0] = overlay.tile([PARTS, C_HALVES, K], F32, name="result", bufs=2, offset=225280)
+            result = result_of[m, v0]
+            bank = banks_of[m, v0, h]
+            for target, source in (
+                (result[:, h, 0:K_SUM], bank[:, 0:K_SUM]),
+                (
+                    result[:, h, K_SUM:K].rearrange("n (w e) -> n w e", e=2),
+                    bank[:, K_SUM:K].rearrange("n (e w) -> n w e", e=2),
+                ),
+            ):
+                if on_vector:
+                    nc.vector.tensor_scalar(out=target, in0=source, scalar1=1.0 / T, scalar2=None, op0=MULT)
+                else:
+                    nc.scalar.activation(out=target, in_=source, func=COPY, scale=1.0 / T)
+            if h == C_HALVES - 1:
+                nc.sync.dma_start(out=out_dram[SIDE * u_of(m) + (s + v0) % SIDE], in_=result[:])
 
         units = [(u0, s, e) for u0 in range(2) for s in range(HALF) for e in range(2)]
         chores = {}
@@ -468,32 +486,63 @@ def tile_iwht3layer_pa_kernel(tc, trans, weight, bias, grad_out, out):
         def add_chore(slot, chore):
             chores.setdefault(slot, []).append(chore)
 
-        path = [pixels_to_partitions(0)]
-        for o2 in range(OCTETS // 2):
-            if o2 + 1 < OCTETS // 2:
-                path.append(pixels_to_partitions(o2 + 1))
-            path.append(transform(2 * o2))
-            path.append(transform(2 * o2 + 1))
-        for i in range(len(path)):
-            add_chore(i // 2, path[i])
+        for o in range(OCTETS):
+            if o % 2 == 0 and o // 2 + 1 < OCTETS // 2:
+                add_chore(o, pixels_to_partitions(o // 2 + 1))
+            add_chore(o, transform(o))
         for s in range(len(hop_jobs) + 2):
-            add_chore(4 + s, hop_step(s))
-        for u, slots in ((0, (7, 9, 11, 13)), (2, (11, 14, 16, 17)), (1, (16, 18, 20, 22)), (3, (20, 23, 25, 27))):
+            add_chore(5 + s, hop_step(s))
+        add_chore(13, move_waiting)
+        for u, slots in ((0, (9, 11, 13, 14)), (2, (13, 15, 17, 18)), (1, (16, 18, 20, 23)), (3, (20, 23, 25, 28))):
             add_chore(slots[3], quantise_x(u))
             add_chore(slots[1], regroup_x(u, 0))
             add_chore(slots[1], load_x(u, 1))
             add_chore(slots[2], regroup_x(u, 1))
             add_chore(slots[0], load_x(u, 0))
-        for m, slot in ((0, 14), (1, 16), (2, 18), (3, 20), (4, 24), (5, 26), (6, 28)):
-            add_chore(slot, pair_quantise(m))
-            add_chore(slot + 1, pair_multiply(m))
-        add_chore(29, lambda: hop_sums(7))
 
+        def prepare(m):
+            def chore():
+                hop_sums(m)
+                quantise(m, 1)
+
+            return chore
+
+        def product(m, v0, h):
+            def chore():
+                multiply(m, v0, h)
+                store(m, v0, h, False)
+
+            return chore
+
+        for m, slot in ((0, 14), (1, 16), (2, 19), (3, 22), (4, 24), (5, 27), (6, 29)):
+            add_chore(slot, prepare(m))
+        products = [(m, v0, h) for m in range(7) for v0 in range(2) for h in range(C_HALVES)]
+        slot = 15
+        while products:
+            for i in range(1 + slot % 2):
+                if products:
+                    add_chore(slot, product(*products.pop(0)))
+            slot += 1
+
+        pixels_to_partitions(0)()
         for slot in range(len(units)):
-            summed(*units[slot])()
-            for chore in chores.get(slot, []):
+            u0, s, e = units[slot]
+            waiting_chores = chores.get(slot, [])
+
+            def between():
+                if waiting_chores:
+                    waiting_chores.pop(0)()
+
+            summed(u0, s, e, between)()
+            for chore in waiting_chores:
                 chore()
+        for slot in sorted(chores):
+            if slot >= len(units):
+                for chore in chores[slot]:
+                    chore()
+        hop_sums(7)
         quantise(7, 2)
         for v0 in range(2):
-            multiply(7, v0)
-            store(7, v0, (1,))
+            for h in range(C_HALVES):
+                multiply(7, v0, h)
+                store(7, v0, h, h == 1)

@@ -218,7 +218,7 @@ def tile_iwht3layer_pa_kernel(tc, trans, weight, bias, grad_out, out):
         ]
 
         pool_b = overlay.tile([PARTS, 8 * UNIT_G], F32, name="pool_b", offset=172032)
-        for u0 in range(2):
+        def gpsimd_rest(u0):
             half = pool_a[:, u0 * 8 * UNIT_G : (u0 + 1) * 8 * UNIT_G]
             for u1 in range(2):
                 nc.gpsimd.tensor_tensor(
@@ -492,7 +492,9 @@ def tile_iwht3layer_pa_kernel(tc, trans, weight, bias, grad_out, out):
             add_chore(o, transform(o))
         for s in range(len(hop_jobs) + 2):
             add_chore(5 + s, hop_step(s))
-        add_chore(13, move_waiting)
+        add_chore(12, lambda: gpsimd_rest(0))
+        add_chore(12, move_waiting)
+        add_chore(12, lambda: gpsimd_rest(1))
         for u, slots in ((0, (9, 11, 13, 14)), (2, (13, 15, 17, 18)), (1, (16, 18, 20, 23)), (3, (20, 23, 25, 28))):
             add_chore(slots[3], quantise_x(u))
             add_chore(slots[1], regroup_x(u, 0))

@@ -61,8 +61,8 @@ def transform_matrix(nc, pool, ident):
     return ordered
 
 
-def positive(s):
-    return [j for j in range(HALF) if sum(((j & s) >> b) & 1 for b in range(LEVELS - 1)) % 2 == 0]
+def positive(v):
+    return [q for q in range(SIDE) if sum(((q & v) >> b) & 1 for b in range(LEVELS // 2)) % 2 == 0]
 
 
 def tile_iwht3layer_pa_kernel(tc, trans, weight, bias, grad_out, out):
@@ -73,12 +73,10 @@ def tile_iwht3layer_pa_kernel(tc, trans, weight, bias, grad_out, out):
     out_dram = out.rearrange("t (h m) k -> t m h k", h=C_HALVES)
 
     with tc.tile_pool(name="keep", bufs=1) as keep, tc.tile_pool(name="turned", bufs=2) as turned, tc.tile_pool(
-        name="pixel_pool", bufs=2
-    ) as pixel_pool, tc.tile_pool(name="overlay", bufs=1) as overlay, tc.psum_pool(
-        name="psum_a", bufs=3
-    ) as psum_a, tc.psum_pool(name="psum_b", bufs=2) as psum_b, tc.psum_pool(
-        name="psum_c", bufs=3
-    ) as psum_c, tc.manual_schedule():
+        name="overlay", bufs=1
+    ) as overlay, tc.psum_pool(name="psum_a", bufs=3) as psum_a, tc.psum_pool(
+        name="psum_b", bufs=2
+    ) as psum_b, tc.psum_pool(name="psum_c", bufs=3) as psum_c, tc.manual_schedule():
         ident = keep.tile([PARTS, PARTS], BF16, name="ident")
         make_identity(nc, ident[:])
         ident_f = keep.tile([PARTS, PARTS], F32, name="ident_f")
@@ -267,7 +265,7 @@ def tile_iwht3layer_pa_kernel(tc, trans, weight, bias, grad_out, out):
                             in_=picked[:, r, 2 * o2 + i, :, :].rearrange("n a e -> n (a e)"),
                             identity=ident[:],
                         )
-                pixels = pixel_pool.tile([PARTS, 2, PACK, PARTS], BF16, name="pixels")
+                pixels = overlay.tile([PARTS, 2, PACK, PARTS], BF16, name="pixels", bufs=2, offset=233472)
                 nc.scalar.copy(out=pixels[:], in_=pix_ps[:])
                 pixels_of[o2] = pixels
 
@@ -331,38 +329,79 @@ def tile_iwht3layer_pa_kernel(tc, trans, weight, bias, grad_out, out):
 
             return chore
 
-        whole_of = {}
+        all_of = {}
+        tops_of = {}
 
-        def summed(u0, s, e, between):
-            def piece():
-                bank = psum_a.tile([PARTS, PACK, PARTS], F32, name="bank_a")
-                members = positive(s)
-                for r in range(PACK):
-                    if s == 0 and r == PACK // 2:
-                        between()
-                    for j in members:
-                        nc.tensor.matmul(
-                            out=bank[:, r, :],
-                            lhsT=sums[u0][:, e, r, j, :],
-                            rhs=ident_f[:],
-                            is_transpose=True,
-                            start=j == members[0],
-                            stop=j == members[-1],
-                        )
-                column = (K_SUM + e * PARTS) * PACK
-                target = gy[u0][:, s, column : column + PARTS * PACK].rearrange("n (w r) -> n w r", r=PACK)
-                source = bank[:].rearrange("n r w -> n w r")
-                if s == 0:
-                    whole = overlay.tile([PARTS, PARTS, PACK], F32, name="whole", bufs=4, offset=184320)
-                    nc.scalar.copy(out=whole[:], in_=source)
-                    nc.scalar.copy(out=target, in_=source)
-                    whole_of[u0, e] = whole
-                else:
-                    nc.vector.scalar_tensor_tensor(
-                        out=target, in0=source, scalar=2.0, in1=whole_of[u0, e][:], op0=MULT, op1=SUBTRACT
+        def add_up(u0, e, bank, r_from, r_to, members):
+            for r in range(r_from, r_to):
+                for j in members:
+                    nc.tensor.matmul(
+                        out=bank[:, r, :],
+                        lhsT=sums[u0][:, e, r, j, :],
+                        rhs=ident_f[:],
+                        is_transpose=True,
+                        start=j == members[0],
+                        stop=j == members[-1],
                     )
 
-            return piece
+        def new_bank():
+            return psum_a.tile([PARTS, PACK, PARTS], F32, name="bank_a")
+
+        def source_of(bank):
+            return bank[:].rearrange("n r w -> n w r")
+
+        def target_of(u0, s, e):
+            column = (K_SUM + e * PARTS) * PACK
+            return gy[u0][:, s, column : column + PARTS * PACK].rearrange("n (w r) -> n w r", r=PACK)
+
+        def double(target, bank, sign, other, op):
+            nc.vector.scalar_tensor_tensor(
+                out=target, in0=source_of(bank), scalar=2.0 * sign, in1=other, op0=MULT, op1=op
+            )
+
+        def sum_of_all(u0, e):
+            held = []
+
+            def first():
+                held.append(new_bank())
+                add_up(u0, e, held[0], 0, 2, range(HALF))
+
+            def second():
+                bank = held[0]
+                add_up(u0, e, bank, 2, PACK, range(HALF))
+                whole = overlay.tile([PARTS, PARTS, PACK], F32, name="whole", bufs=4, offset=184320)
+                nc.scalar.copy(out=whole[:], in_=source_of(bank))
+                nc.scalar.copy(out=target_of(u0, 0, e), in_=source_of(bank))
+                all_of[u0, e] = whole
+
+            return [first, second]
+
+        def top_less_bottom(u0, e):
+            def piece():
+                bank = new_bank()
+                add_up(u0, e, bank, 0, PACK, range(SIDE))
+                whole = overlay.tile([PARTS, PARTS, PACK], F32, name="whole", bufs=4, offset=184320)
+                double(whole[:], bank, 1.0, all_of[u0, e][:], SUBTRACT)
+                nc.scalar.copy(out=target_of(u0, SIDE, e), in_=whole[:])
+                tops_of[u0, e] = whole
+
+            return [piece]
+
+        def both_u1(u0, v, e):
+            def piece():
+                bank = new_bank()
+                add_up(u0, e, bank, 0, PACK, positive(v))
+                parts = []
+                for name, offset, other in (("part0", 233472, all_of[u0, e]), ("part1", 235520, tops_of[u0, e])):
+                    part = overlay.tile([PARTS, PARTS, PACK], F32, name=name, offset=offset)
+                    double(part[:], bank, 1.0, other[:], SUBTRACT)
+                    parts.append(part)
+                bank = new_bank()
+                add_up(u0, e, bank, 0, PACK, [SIDE + q for q in positive(v)])
+                double(target_of(u0, v, e), bank, 1.0, parts[0][:], ADD)
+                double(target_of(u0, SIDE + v, e), bank, -1.0, parts[1][:], ADD)
+
+            return [piece]
 
         x_raw_of = {}
         x_of = {}
@@ -405,8 +444,10 @@ def tile_iwht3layer_pa_kernel(tc, trans, weight, bias, grad_out, out):
         banks_of = {}
         result_of = {}
 
+        pairs = [(0, 0), (0, 2), (0, 4), (0, 6), (1, 0), (1, 4), (1, 2), (1, 6)]
+
         def place(m):
-            return m // 4, 2 * (m % 4)
+            return pairs[m]
 
         def u_of(m):
             u0, s = place(m)
@@ -480,22 +521,30 @@ def tile_iwht3layer_pa_kernel(tc, trans, weight, bias, grad_out, out):
             if h == C_HALVES - 1:
                 nc.sync.dma_start(out=out_dram[SIDE * u_of(m) + (s + v0) % SIDE], in_=result[:])
 
-        units = [(u0, s, e) for u0 in range(2) for s in range(HALF) for e in range(2)]
+        pieces = []
+        for u0 in range(2):
+            for e in range(2):
+                pieces += sum_of_all(u0, e)
+            for e in range(2):
+                pieces += top_less_bottom(u0, e)
+            for v in range(1, SIDE):
+                for e in range(2):
+                    pieces += both_u1(u0, v, e)
         chores = {}
 
         def add_chore(slot, chore):
             chores.setdefault(slot, []).append(chore)
 
-        for o in range(OCTETS):
+        for o in range(4, OCTETS):
             if o % 2 == 0 and o // 2 + 1 < OCTETS // 2:
-                add_chore(o, pixels_to_partitions(o // 2 + 1))
-            add_chore(o, transform(o))
+                add_chore(o // 2 - 2, pixels_to_partitions(o // 2 + 1))
+            add_chore(o // 2 - 2, transform(o))
         for s in range(len(hop_jobs) + 2):
-            add_chore(5 + s, hop_step(s))
-        add_chore(12, lambda: gpsimd_rest(0))
-        add_chore(12, move_waiting)
-        add_chore(12, lambda: gpsimd_rest(1))
-        for u, slots in ((0, (9, 11, 13, 14)), (2, (13, 15, 17, 18)), (1, (16, 18, 20, 23)), (3, (20, 23, 25, 28))):
+            add_chore(2 + 3 * s // 4, hop_step(s))
+        add_chore(4, lambda: gpsimd_rest(0))
+        add_chore(4, move_waiting)
+        add_chore(4, lambda: gpsimd_rest(1))
+        for u, slots in ((0, (4, 5, 6, 8)), (2, (6, 8, 9, 12)), (1, (9, 12, 13, 17)), (3, (13, 17, 18, 20))):
             add_chore(slots[3], quantise_x(u))
             add_chore(slots[1], regroup_x(u, 0))
             add_chore(slots[1], load_x(u, 1))
@@ -516,35 +565,35 @@ def tile_iwht3layer_pa_kernel(tc, trans, weight, bias, grad_out, out):
 
             return chore
 
-        for m, slot in ((0, 14), (1, 16), (2, 19), (3, 22), (4, 24), (5, 27), (6, 29)):
+        for m, slot in ((0, 9), (1, 11), (2, 13), (3, 15), (4, 20), (5, 21)):
             add_chore(slot, prepare(m))
-        products = [(m, v0, h) for m in range(7) for v0 in range(2) for h in range(C_HALVES)]
-        slot = 15
-        while products:
-            for i in range(1 + slot % 2):
-                if products:
-                    add_chore(slot, product(*products.pop(0)))
-            slot += 1
+            for v0 in range(2):
+                for h in range(C_HALVES):
+                    add_chore(slot + 1 + v0, product(m, v0, h))
 
+        for i in range(4):
+            idle_pass()
         pixels_to_partitions(0)()
-        for slot in range(len(units)):
-            u0, s, e = units[slot]
-            waiting_chores = chores.get(slot, [])
-
-            def between():
-                if waiting_chores:
-                    waiting_chores.pop(0)()
-
-            summed(u0, s, e, between)()
-            for chore in waiting_chores:
+        pixels_to_partitions(1)()
+        for o in range(4):
+            if o == 2:
+                pixels_to_partitions(2)()
+            transform(o)()
+        for slot in range(len(pieces)):
+            pieces[slot]()
+            for chore in chores.get(slot, []):
                 chore()
+        hop_sums(6)
+        quantise(6, 1)
         for slot in sorted(chores):
-            if slot >= len(units):
+            if slot >= len(pieces):
                 for chore in chores[slot]:
                     chore()
         hop_sums(7)
-        quantise(7, 2)
-        for v0 in range(2):
-            for h in range(C_HALVES):
-                multiply(7, v0, h)
-                store(7, v0, h, h == 1)
+        for m in (6, 7):
+            if m == 7:
+                quantise(7, 2)
+            for v0 in range(2):
+                for h in range(C_HALVES):
+                    multiply(m, v0, h)
+                    store(m, v0, h, h == 1)

@@ -37,15 +37,17 @@ BLOCKS = 4
 CHUNK = BLOCK * BLOCKS
 HALF = T // 2
 
+IDLE = 2
+
 FLOPS = 2 * T * N * C * K
 BYTES = 2 * T * N * C + 2 * T * N * K + 4 * T * C * K
 
 
-def transform_matrix(nc, pool, ident):
+def transform_matrix(nc, keep, pool, ident):
     current = ident
     for level in range(LEVELS):
         distance = PARTS // 2 ** (level + 1)
-        following = pool.tile([PARTS, PARTS], BF16, name="matrix%d" % (level + 1))
+        following = pool.tile([PARTS, PARTS], BF16, name="matrix%d" % (level + 1), offset=219136 + 256 * level)
         halves = current[:].rearrange("n (a two b) -> n a two b", two=2, b=distance)
         signed = following[:].rearrange("n (a two b) -> n a two b", two=2, b=distance)
         for bit in range(2):
@@ -53,7 +55,7 @@ def transform_matrix(nc, pool, ident):
                 out=signed[:, :, bit, :], in0=halves[:, :, 0, :], in1=halves[:, :, 1, :], op=SIGN_OP[bit]
             )
         current = following
-    ordered = pool.tile([PARTS, PARTS], BF16, name="matrix_ordered")
+    ordered = keep.tile([PARTS, PARTS], BF16, name="matrix_ordered")
     nc.vector.tensor_copy(
         out=ordered[:].rearrange("n (u0 u1 x) -> n u0 u1 x", u0=2, u1=2),
         in_=current[:].rearrange("n (u1 u0 x) -> n u0 u1 x", u0=2, u1=2),
@@ -83,7 +85,7 @@ def tile_iwht3layer_pa_kernel(tc, trans, weight, bias, grad_out, out):
         make_identity(nc, ident_f[:])
         warm = keep.tile([PARTS, 1], BF16, name="warm")
         nc.scalar.copy(out=warm[:], in_=ident[:, 0:1])
-        matrix = transform_matrix(nc, keep, ident)
+        matrix = transform_matrix(nc, keep, overlay, ident)
 
         sums = [
             overlay.tile([PARTS, 2, PACK, HALF, PARTS], F32, name="sums%d" % u0, offset=65536 + u0 * 32768)
@@ -130,9 +132,9 @@ def tile_iwht3layer_pa_kernel(tc, trans, weight, bias, grad_out, out):
                     nc.gpsimd.tensor_tensor(
                         out=pool_a[:, start : start + SIDE * UNIT_G]
                         .rearrange("n (q r1 x) -> n q r1 x", q=SIDE, r1=2)[:, q_from : q_from + q_count, r1, :]
-                        .rearrange("n q (k r0) -> n q k r0", r0=2),
-                        in0=a_rows[:, :, :, K_TENSOR:K_POOL_END].rearrange("n r0 q k -> n q k r0"),
-                        in1=b_rows[:, :, :, K_TENSOR:K_POOL_END].rearrange("n r0 q k -> n q k r0"),
+                        .rearrange("n q (r0 k) -> n q r0 k", r0=2),
+                        in0=a_rows[:, :, :, K_TENSOR:K_POOL_END].rearrange("n r0 q k -> n q r0 k"),
+                        in1=b_rows[:, :, :, K_TENSOR:K_POOL_END].rearrange("n r0 q k -> n q r0 k"),
                         op=SIGN_OP[u0],
                     )
                 for u0 in range(2):
@@ -140,9 +142,9 @@ def tile_iwht3layer_pa_kernel(tc, trans, weight, bias, grad_out, out):
                     nc.gpsimd.tensor_tensor(
                         out=hop[:, start : start + 8 * ROW_H]
                         .rearrange("n (q u x) -> n q u x", q=SIDE, u=2)[:, q_from : q_from + q_count, u0, :]
-                        .rearrange("n q (k r0) -> n q k r0", r0=2),
-                        in0=a_rows[:, :, :, K_POOL_END:K_SUM].rearrange("n r0 q k -> n q k r0"),
-                        in1=b_rows[:, :, :, K_POOL_END:K_SUM].rearrange("n r0 q k -> n q k r0"),
+                        .rearrange("n q (r0 k) -> n q r0 k", r0=2),
+                        in0=a_rows[:, :, :, K_POOL_END:K_SUM].rearrange("n r0 q k -> n q r0 k"),
+                        in1=b_rows[:, :, :, K_POOL_END:K_SUM].rearrange("n r0 q k -> n q r0 k"),
                         op=SIGN_OP[u0],
                     )
 
@@ -178,12 +180,12 @@ def tile_iwht3layer_pa_kernel(tc, trans, weight, bias, grad_out, out):
                     op=SIGN_OP[u0],
                 )
 
-        ones = overlay.tile([PARTS, CHUNK * PACK], BF16, name="ones", offset=225280, align_bytes=64)
+        ones = overlay.tile([PARTS, CHUNK * PACK], BF16, name="ones", offset=215040, align_bytes=64)
         nc.gpsimd.memset(ones[:], 1.0)
-        idle_rhs = overlay.tile([PARTS, CHUNK], U32, name="idle_rhs", offset=215040, align_bytes=64)
-        idle_rhs_scales = overlay.tile([PARTS, CHUNK], U8, name="idle_rhs_scales", offset=217088, align_bytes=64)
-        idle_lhs = overlay.tile([PARTS, PARTS], U32, name="idle_lhs", offset=217600, align_bytes=64)
-        idle_lhs_scales = overlay.tile([PARTS, PARTS], U8, name="idle_lhs_scales", offset=218112, align_bytes=64)
+        idle_rhs = overlay.tile([PARTS, CHUNK], U32, name="idle_rhs", offset=225280, align_bytes=64)
+        idle_rhs_scales = overlay.tile([PARTS, CHUNK], U8, name="idle_rhs_scales", offset=227328, align_bytes=64)
+        idle_lhs = overlay.tile([PARTS, PARTS], U32, name="idle_lhs", offset=227840, align_bytes=64)
+        idle_lhs_scales = overlay.tile([PARTS, PARTS], U8, name="idle_lhs_scales", offset=228352, align_bytes=64)
         nc.vector.quantize_mx(out=idle_rhs[:].bitcast(E5M2_X4), scales=idle_rhs_scales[:], in_=ones[:])
         nc.vector.quantize_mx(
             out=idle_lhs[:].bitcast(E4M3_X4), scales=idle_lhs_scales[:], in_=ones[:, 0 : PARTS * PACK]
@@ -216,37 +218,41 @@ def tile_iwht3layer_pa_kernel(tc, trans, weight, bias, grad_out, out):
         ]
 
         pool_b = overlay.tile([PARTS, 8 * UNIT_G], F32, name="pool_b", offset=172032)
-        def gpsimd_rest(u0):
+        plain_of = {}
+
+        def gpsimd_rest(u0, u1):
             half = pool_a[:, u0 * 8 * UNIT_G : (u0 + 1) * 8 * UNIT_G]
-            for u1 in range(2):
-                nc.gpsimd.tensor_tensor(
-                    out=pool_b[:, u1 * 4 * UNIT_G : (u1 + 1) * 4 * UNIT_G],
-                    in0=half[:, 0 : 4 * UNIT_G],
-                    in1=half[:, 4 * UNIT_G : 8 * UNIT_G],
-                    op=SIGN_OP[u1],
-                )
-            for u1 in range(2):
-                q_pairs = pool_b[:, u1 * 4 * UNIT_G : (u1 + 1) * 4 * UNIT_G].rearrange("n (q1 x) -> n q1 x", q1=2)
-                by_v1 = half[:, u1 * 4 * UNIT_G : (u1 + 1) * 4 * UNIT_G].rearrange(
-                    "n (v1 q0 x) -> n v1 q0 x", v1=2, q0=2
-                )
-                for v1 in range(2):
+            if u1 == 0:
+                for bit in range(2):
                     nc.gpsimd.tensor_tensor(
-                        out=by_v1[:, v1].rearrange("n q0 x -> n (q0 x)"),
-                        in0=q_pairs[:, 0, :],
-                        in1=q_pairs[:, 1, :],
-                        op=SIGN_OP[v1],
+                        out=pool_b[:, bit * 4 * UNIT_G : (bit + 1) * 4 * UNIT_G],
+                        in0=half[:, 0 : 4 * UNIT_G],
+                        in1=half[:, 4 * UNIT_G : 8 * UNIT_G],
+                        op=SIGN_OP[bit],
                     )
-                for v1 in range(2):
-                    for v0 in range(2):
-                        nc.gpsimd.tensor_tensor(
-                            out=gy[u0][:, 4 * u1 + 2 * v1 + v0, K_TENSOR * PACK : K_POOL_END * PACK].rearrange(
-                                "n (k r1 r0) -> n k r1 r0", r1=2, r0=2
-                            ),
-                            in0=by_v1[:, v1, 0].rearrange("n (r1 k r0) -> n k r1 r0", r1=2, r0=2),
-                            in1=by_v1[:, v1, 1].rearrange("n (r1 k r0) -> n k r1 r0", r1=2, r0=2),
-                            op=SIGN_OP[v0],
-                        )
+            q_pairs = pool_b[:, u1 * 4 * UNIT_G : (u1 + 1) * 4 * UNIT_G].rearrange("n (q1 x) -> n q1 x", q1=2)
+            by_v1 = half[:, u1 * 4 * UNIT_G : (u1 + 1) * 4 * UNIT_G].rearrange("n (v1 q0 x) -> n v1 q0 x", v1=2, q0=2)
+            for v1 in range(2):
+                nc.gpsimd.tensor_tensor(
+                    out=by_v1[:, v1].rearrange("n q0 x -> n (q0 x)"),
+                    in0=q_pairs[:, 0, :],
+                    in1=q_pairs[:, 1, :],
+                    op=SIGN_OP[v1],
+                )
+            plain = overlay.tile([PARTS, 2, 2, UNIT_G], BF16, name="plain", bufs=2, offset=228480)
+            for v0 in range(2):
+                nc.gpsimd.tensor_tensor(
+                    out=plain[:, :, v0, :], in0=by_v1[:, :, 0, :], in1=by_v1[:, :, 1, :], op=SIGN_OP[v0]
+                )
+            plain_of[u0, u1] = plain
+
+        def interleave(u0, u1):
+            nc.scalar.copy(
+                out=gy[u0][:, SIDE * u1 : SIDE * u1 + SIDE, K_TENSOR * PACK : K_POOL_END * PACK].rearrange(
+                    "n v (k r) -> n v k r", r=PACK
+                ),
+                in_=plain_of[u0, u1][:].rearrange("n v1 v0 (r k) -> n (v1 v0) k r", r=PACK),
+            )
 
         pixels_of = {}
         waiting = overlay.tile([PARTS, HALF, K_TENSOR * PACK], BF16, name="waiting", offset=208896, align_bytes=64)
@@ -265,7 +271,7 @@ def tile_iwht3layer_pa_kernel(tc, trans, weight, bias, grad_out, out):
                             in_=picked[:, r, 2 * o2 + i, :, :].rearrange("n a e -> n (a e)"),
                             identity=ident[:],
                         )
-                pixels = overlay.tile([PARTS, 2, PACK, PARTS], BF16, name="pixels", bufs=2, offset=233472)
+                pixels = overlay.tile([PARTS, 2, PACK, PARTS], BF16, name="pixels", bufs=2, offset=234624)
                 nc.scalar.copy(out=pixels[:], in_=pix_ps[:])
                 pixels_of[o2] = pixels
 
@@ -347,6 +353,11 @@ def tile_iwht3layer_pa_kernel(tc, trans, weight, bias, grad_out, out):
         def new_bank():
             return psum_a.tile([PARTS, PACK, PARTS], F32, name="bank_a")
 
+        def new_whole(u0):
+            return overlay.tile(
+                [PARTS, PARTS, PACK], F32, name="whole%d" % u0, bufs=4, offset=(184320, 204800)[u0]
+            )
+
         def source_of(bank):
             return bank[:].rearrange("n r w -> n w r")
 
@@ -360,27 +371,24 @@ def tile_iwht3layer_pa_kernel(tc, trans, weight, bias, grad_out, out):
             )
 
         def sum_of_all(u0, e):
-            held = []
-
-            def first():
-                held.append(new_bank())
-                add_up(u0, e, held[0], 0, 2, range(HALF))
-
-            def second():
-                bank = held[0]
+            def piece():
+                bank = new_bank()
+                add_up(u0, e, bank, 0, 2, range(HALF))
+                for i in range(IDLE):
+                    idle_pass()
                 add_up(u0, e, bank, 2, PACK, range(HALF))
-                whole = overlay.tile([PARTS, PARTS, PACK], F32, name="whole", bufs=4, offset=184320)
+                whole = new_whole(u0)
                 nc.scalar.copy(out=whole[:], in_=source_of(bank))
                 nc.scalar.copy(out=target_of(u0, 0, e), in_=source_of(bank))
                 all_of[u0, e] = whole
 
-            return [first, second]
+            return [piece]
 
         def top_less_bottom(u0, e):
             def piece():
                 bank = new_bank()
                 add_up(u0, e, bank, 0, PACK, range(SIDE))
-                whole = overlay.tile([PARTS, PARTS, PACK], F32, name="whole", bufs=4, offset=184320)
+                whole = new_whole(u0)
                 double(whole[:], bank, 1.0, all_of[u0, e][:], SUBTRACT)
                 nc.scalar.copy(out=target_of(u0, SIDE, e), in_=whole[:])
                 tops_of[u0, e] = whole
@@ -392,7 +400,7 @@ def tile_iwht3layer_pa_kernel(tc, trans, weight, bias, grad_out, out):
                 bank = new_bank()
                 add_up(u0, e, bank, 0, PACK, positive(v))
                 parts = []
-                for name, offset, other in (("part0", 233472, all_of[u0, e]), ("part1", 235520, tops_of[u0, e])):
+                for name, offset, other in (("part0", 234624, all_of[u0, e]), ("part1", 236672, tops_of[u0, e])):
                     part = overlay.tile([PARTS, PARTS, PACK], F32, name=name, offset=offset)
                     double(part[:], bank, 1.0, other[:], SUBTRACT)
                     parts.append(part)
@@ -429,8 +437,14 @@ def tile_iwht3layer_pa_kernel(tc, trans, weight, bias, grad_out, out):
 
         def quantise_x(u):
             def chore():
-                x_codes = overlay.tile([PARTS, SIDE * C], U32, name="x_codes", bufs=2, offset=215040, align_bytes=64)
-                x_scales = overlay.tile([PARTS, SIDE * C], U8, name="x_scales", bufs=2, offset=223232, align_bytes=64)
+                first = 215040 if u in (0, 2) else 65536
+                half = u // 2
+                x_codes = overlay.tile(
+                    [PARTS, SIDE * C], U32, name="x_codes%d" % u, offset=first + half * 4096, align_bytes=64
+                )
+                x_scales = overlay.tile(
+                    [PARTS, SIDE * C], U8, name="x_scales%d" % u, offset=first + 8192 + half * 1024, align_bytes=64
+                )
                 nc.vector.quantize_mx(
                     out=x_codes[:].bitcast(E4M3_X4),
                     scales=x_scales[:],
@@ -442,9 +456,10 @@ def tile_iwht3layer_pa_kernel(tc, trans, weight, bias, grad_out, out):
 
         codes_of = {}
         banks_of = {}
+        acc_pools = ((psum_c, "bank_c"), (psum_a, "bank_a"), (psum_b, "bank_b"))
         result_of = {}
 
-        pairs = [(0, 0), (0, 2), (0, 4), (0, 6), (1, 0), (1, 4), (1, 2), (1, 6)]
+        pairs = [(u0, s) for u0 in range(2) for s in range(0, HALF, 2)]
 
         def place(m):
             return pairs[m]
@@ -464,8 +479,8 @@ def tile_iwht3layer_pa_kernel(tc, trans, weight, bias, grad_out, out):
                     out=gy[u0][:, s + v0, K_POOL_END * PACK : K_SUM * PACK].rearrange(
                         "n (k r1 r0) -> n k r1 r0", r1=2, r0=2
                     ),
-                    in0=by_unit[:, :, a_unit, :].rearrange("n r1 (k r0) -> n k r1 r0", r0=2),
-                    in1=by_unit[:, :, b_unit, :].rearrange("n r1 (k r0) -> n k r1 r0", r0=2),
+                    in0=by_unit[:, :, a_unit, :].rearrange("n r1 (r0 k) -> n k r1 r0", r0=2),
+                    in1=by_unit[:, :, b_unit, :].rearrange("n r1 (r0 k) -> n k r1 r0", r0=2),
                     op=SIGN_OP[v0],
                 )
 
@@ -489,7 +504,8 @@ def tile_iwht3layer_pa_kernel(tc, trans, weight, bias, grad_out, out):
             x_codes, x_scales = x_codes_of[u_of(m)]
             gy_codes, gy_scales = codes_of[m]
             column = (s + v0) % SIDE * C + h * PARTS
-            acc = psum_c.tile([PARTS, K], F32, name="bank_c")
+            pool, name = acc_pools[len(banks_of) % len(acc_pools)]
+            acc = pool.tile([PARTS, K], F32, name=name)
             nc.tensor.matmul_mx(
                 out=acc[:],
                 lhsT=x_codes[:, column : column + PARTS].bitcast(E4M3_X4),
@@ -504,7 +520,7 @@ def tile_iwht3layer_pa_kernel(tc, trans, weight, bias, grad_out, out):
         def store(m, v0, h, on_vector):
             u0, s = place(m)
             if h == 0:
-                result_of[m, v0] = overlay.tile([PARTS, C_HALVES, K], F32, name="result", bufs=2, offset=225280)
+                result_of[m, v0] = overlay.tile([PARTS, C_HALVES, K], F32, name="result", bufs=4, offset=98304)
             result = result_of[m, v0]
             bank = banks_of[m, v0, h]
             for target, source in (
@@ -521,15 +537,16 @@ def tile_iwht3layer_pa_kernel(tc, trans, weight, bias, grad_out, out):
             if h == C_HALVES - 1:
                 nc.sync.dma_start(out=out_dram[SIDE * u_of(m) + (s + v0) % SIDE], in_=result[:])
 
-        pieces = []
-        for u0 in range(2):
-            for e in range(2):
-                pieces += sum_of_all(u0, e)
-            for e in range(2):
-                pieces += top_less_bottom(u0, e)
-            for v in range(1, SIDE):
-                for e in range(2):
-                    pieces += both_u1(u0, v, e)
+        heads = [
+            [piece for e in range(2) for piece in sum_of_all(u0, e)]
+            + [piece for e in range(2) for piece in top_less_bottom(u0, e)]
+            for u0 in range(2)
+        ]
+        bodies = [[piece for v in range(1, SIDE) for e in range(2) for piece in both_u1(u0, v, e)] for u0 in range(2)]
+        pieces = heads[0] + bodies[0][:1]
+        for head, body in zip(heads[1], (bodies[0][1:3], bodies[0][3:4], bodies[0][4:5], bodies[0][5:])):
+            pieces += [head] + body
+        pieces += bodies[1]
         chores = {}
 
         def add_chore(slot, chore):
@@ -540,36 +557,21 @@ def tile_iwht3layer_pa_kernel(tc, trans, weight, bias, grad_out, out):
                 add_chore(o // 2 - 2, pixels_to_partitions(o // 2 + 1))
             add_chore(o // 2 - 2, transform(o))
         for s in range(len(hop_jobs) + 2):
-            add_chore(2 + 3 * s // 4, hop_step(s))
-        add_chore(4, lambda: gpsimd_rest(0))
+            add_chore(s if s < 3 else s + 1, hop_step(s))
+        add_chore(4, lambda: gpsimd_rest(0, 0))
+        add_chore(4, lambda: gpsimd_rest(0, 1))
         add_chore(4, move_waiting)
-        add_chore(4, lambda: gpsimd_rest(1))
-        for u, slots in ((0, (4, 5, 6, 8)), (2, (6, 8, 9, 12)), (1, (9, 12, 13, 17)), (3, (13, 17, 18, 20))):
+        for (u0, u1), slot in (((0, 0), 9), ((0, 1), 12)):
+            add_chore(slot, lambda u0=u0, u1=u1: interleave(u0, u1))
+            add_chore(slot, lambda u1=u1: gpsimd_rest(1, u1))
+        add_chore(17, lambda: interleave(1, 0))
+        add_chore(19, lambda: interleave(1, 1))
+        for u, slots in ((0, (4, 5, 6, 7)), (2, (6, 7, 8, 10)), (1, (8, 10, 11, 15)), (3, (11, 15, 16, 18))):
             add_chore(slots[3], quantise_x(u))
             add_chore(slots[1], regroup_x(u, 0))
             add_chore(slots[1], load_x(u, 1))
             add_chore(slots[2], regroup_x(u, 1))
             add_chore(slots[0], load_x(u, 0))
-
-        def prepare(m):
-            def chore():
-                hop_sums(m)
-                quantise(m, 1)
-
-            return chore
-
-        def product(m, v0, h):
-            def chore():
-                multiply(m, v0, h)
-                store(m, v0, h, False)
-
-            return chore
-
-        for m, slot in ((0, 9), (1, 11), (2, 13), (3, 15), (4, 20), (5, 21)):
-            add_chore(slot, prepare(m))
-            for v0 in range(2):
-                for h in range(C_HALVES):
-                    add_chore(slot + 1 + v0, product(m, v0, h))
 
         for i in range(4):
             idle_pass()
@@ -581,19 +583,28 @@ def tile_iwht3layer_pa_kernel(tc, trans, weight, bias, grad_out, out):
             transform(o)()
         for slot in range(len(pieces)):
             pieces[slot]()
+            for i in range(IDLE):
+                idle_pass()
             for chore in chores.get(slot, []):
                 chore()
-        hop_sums(6)
-        quantise(6, 1)
-        for slot in sorted(chores):
-            if slot >= len(pieces):
-                for chore in chores[slot]:
-                    chore()
-        hop_sums(7)
-        for m in (6, 7):
-            if m == 7:
-                quantise(7, 2)
+
+        hop_sums(0)
+        held = []
+        for m in range(len(pairs)):
+            last = m == len(pairs) - 1
+            quantise(m, 2 if last else 1)
             for v0 in range(2):
                 for h in range(C_HALVES):
                     multiply(m, v0, h)
-                    store(m, v0, h, h == 1)
+            if not last:
+                hop_sums(m + 1)
+            while held:
+                store(*held.pop(0))
+            for v0 in range(2):
+                for h in range(C_HALVES):
+                    if v0 == 1 and h == 1 and (last or m % 2 == 1):
+                        held.append((m, v0, h, True))
+                    else:
+                        store(m, v0, h, False)
+        while held:
+            store(*held.pop(0))

@@ -26,18 +26,19 @@ C_HALVES = C // PARTS
 OCTET = PARTS // T
 OCTETS = 12
 K_POOL = 96
-K_HOP = 64
+K_JOINT = 64
 K_TENSOR = OCTETS * OCTET
 K_POOL_END = K_TENSOR + K_POOL
-K_SUM = K_POOL_END + K_HOP
+K_SUM = K_POOL_END + K_JOINT
 UNIT_G = K_POOL * PACK
-ROW_H = K_HOP * 2
+J_WIDTH = 32
+J_TILES = K_JOINT // J_WIDTH
 BLOCK = 128
 BLOCKS = 4
 CHUNK = BLOCK * BLOCKS
 HALF = T // 2
 
-IDLE = 2
+JOINT_ALL = (235520, 236544)
 
 FLOPS = 2 * T * N * C * K
 BYTES = 2 * T * N * C + 2 * T * N * K + 4 * T * C * K
@@ -74,7 +75,7 @@ def tile_iwht3layer_pa_kernel(tc, trans, weight, bias, grad_out, out):
     x_dram = trans.rearrange("(u v) b i (jh r) c -> u (b i jh) v (r c)", v=SIDE, r=PACK)
     out_dram = out.rearrange("t (h m) k -> t m h k", h=C_HALVES)
 
-    with tc.tile_pool(name="keep", bufs=1) as keep, tc.tile_pool(name="turned", bufs=2) as turned, tc.tile_pool(
+    with tc.tile_pool(name="keep", bufs=1) as keep, tc.tile_pool(
         name="overlay", bufs=1
     ) as overlay, tc.psum_pool(name="psum_a", bufs=3) as psum_a, tc.psum_pool(
         name="psum_b", bufs=2
@@ -91,7 +92,10 @@ def tile_iwht3layer_pa_kernel(tc, trans, weight, bias, grad_out, out):
             overlay.tile([PARTS, 2, PACK, HALF, PARTS], F32, name="sums%d" % u0, offset=65536 + u0 * 32768)
             for u0 in range(2)
         ]
-        hop = overlay.tile([PARTS, 2 * T * ROW_H], F32, name="hop", offset=131072)
+        joint_raw = overlay.tile(
+            [PARTS, 2, HALF, J_TILES, PACK, J_WIDTH], F32, name="joint_raw", offset=215040
+        )
+        joint = overlay.tile([PARTS, J_TILES, 2, HALF, PARTS], F32, name="joint", offset=131072)
         pool_a = overlay.tile([PARTS, T * UNIT_G], F32, name="pool_a", offset=147456)
         picked = overlay.tile([PARTS, PACK, OCTETS, T, OCTET], BF16, name="picked", offset=192512)
 
@@ -138,15 +142,16 @@ def tile_iwht3layer_pa_kernel(tc, trans, weight, bias, grad_out, out):
                         op=SIGN_OP[u0],
                     )
                 for u0 in range(2):
-                    start = (r1 * 2 + p1) * 8 * ROW_H
-                    nc.gpsimd.tensor_tensor(
-                        out=hop[:, start : start + 8 * ROW_H]
-                        .rearrange("n (q u x) -> n q u x", q=SIDE, u=2)[:, q_from : q_from + q_count, u0, :]
-                        .rearrange("n q (r0 k) -> n q r0 k", r0=2),
-                        in0=a_rows[:, :, :, K_POOL_END:K_SUM].rearrange("n r0 q k -> n q r0 k"),
-                        in1=b_rows[:, :, :, K_POOL_END:K_SUM].rearrange("n r0 q k -> n q r0 k"),
-                        op=SIGN_OP[u0],
-                    )
+                    for i in range(J_TILES):
+                        columns = slice(K_POOL_END + i * J_WIDTH, K_POOL_END + (i + 1) * J_WIDTH)
+                        nc.gpsimd.tensor_tensor(
+                            out=joint_raw[
+                                :, u0, SIDE * p1 + q_from : SIDE * p1 + q_from + q_count, i, 2 * r1 : 2 * r1 + 2, :
+                            ],
+                            in0=a_rows[:, :, :, columns].rearrange("n r0 q k -> n q r0 k"),
+                            in1=b_rows[:, :, :, columns].rearrange("n r0 q k -> n q r0 k"),
+                            op=SIGN_OP[u0],
+                        )
 
         def pick(r1, p1):
             for p in (2 * p1, 2 * p1 + 1):
@@ -182,10 +187,10 @@ def tile_iwht3layer_pa_kernel(tc, trans, weight, bias, grad_out, out):
 
         ones = overlay.tile([PARTS, CHUNK * PACK], BF16, name="ones", offset=215040, align_bytes=64)
         nc.gpsimd.memset(ones[:], 1.0)
-        idle_rhs = overlay.tile([PARTS, CHUNK], U32, name="idle_rhs", offset=225280, align_bytes=64)
-        idle_rhs_scales = overlay.tile([PARTS, CHUNK], U8, name="idle_rhs_scales", offset=227328, align_bytes=64)
-        idle_lhs = overlay.tile([PARTS, PARTS], U32, name="idle_lhs", offset=227840, align_bytes=64)
-        idle_lhs_scales = overlay.tile([PARTS, PARTS], U8, name="idle_lhs_scales", offset=228352, align_bytes=64)
+        idle_rhs = overlay.tile([PARTS, CHUNK], U32, name="idle_rhs", offset=231424, align_bytes=64)
+        idle_rhs_scales = overlay.tile([PARTS, CHUNK], U8, name="idle_rhs_scales", offset=233472, align_bytes=64)
+        idle_lhs = overlay.tile([PARTS, PARTS], U32, name="idle_lhs", offset=233984, align_bytes=64)
+        idle_lhs_scales = overlay.tile([PARTS, PARTS], U8, name="idle_lhs_scales", offset=234496, align_bytes=64)
         nc.vector.quantize_mx(out=idle_rhs[:].bitcast(E5M2_X4), scales=idle_rhs_scales[:], in_=ones[:])
         nc.vector.quantize_mx(
             out=idle_lhs[:].bitcast(E4M3_X4), scales=idle_lhs_scales[:], in_=ones[:, 0 : PARTS * PACK]
@@ -203,19 +208,40 @@ def tile_iwht3layer_pa_kernel(tc, trans, weight, bias, grad_out, out):
                 stop=True,
             )
 
+        def turn_joint(i, u0, p1):
+            bank = psum_b.tile([PARTS, SIDE, PARTS], F32, name="bank_b")
+            for q in range(SIDE):
+                nc.tensor.transpose(
+                    out=bank[:, q, :],
+                    in_=joint_raw[:, u0, SIDE * p1 + q, i].rearrange("n r k -> n (r k)"),
+                    identity=ident_f[:],
+                )
+            nc.scalar.copy(out=joint[:, i, u0, SIDE * p1 : SIDE * p1 + SIDE, :], in_=bank[:])
+
         for r1 in range(2):
             for p1 in range(2):
                 gpsimd_level1(r1, p1)
                 for r0 in range(2):
                     summed_level1(r1, p1, r0)
-                    for i in range(3):
-                        idle_pass()
+                    if (r1, p1) != (1, 1):
+                        for i in range(3):
+                            idle_pass()
                 pick(r1, p1)
 
-        gy = [
-            overlay.tile([PARTS, HALF, K * PACK], BF16, name="gy%d" % u0, offset=u0 * 32768, align_bytes=64)
-            for u0 in range(2)
-        ]
+        gy = {}
+        for u0 in range(2):
+            for s in range(0, HALF, 2):
+                pair = overlay.tile(
+                    [PARTS, 2, K * PACK],
+                    BF16,
+                    name="gy%d%d" % (u0, s),
+                    offset=u0 * 32768 + s * 4096,
+                    align_bytes=64,
+                )
+                gy[u0, s] = pair
+
+        def gy_rows(u0, s, count):
+            return gy[u0, s - s % 2][:, s % 2 : s % 2 + count, :]
 
         pool_b = overlay.tile([PARTS, 8 * UNIT_G], F32, name="pool_b", offset=172032)
         plain_of = {}
@@ -239,7 +265,7 @@ def tile_iwht3layer_pa_kernel(tc, trans, weight, bias, grad_out, out):
                     in1=q_pairs[:, 1, :],
                     op=SIGN_OP[v1],
                 )
-            plain = overlay.tile([PARTS, 2, 2, UNIT_G], BF16, name="plain", bufs=2, offset=228480)
+            plain = overlay.tile([PARTS, 2, 2, UNIT_G], BF16, name="plain", bufs=2, offset=225280)
             for v0 in range(2):
                 nc.gpsimd.tensor_tensor(
                     out=plain[:, :, v0, :], in0=by_v1[:, :, 0, :], in1=by_v1[:, :, 1, :], op=SIGN_OP[v0]
@@ -247,19 +273,19 @@ def tile_iwht3layer_pa_kernel(tc, trans, weight, bias, grad_out, out):
             plain_of[u0, u1] = plain
 
         def interleave(u0, u1):
-            nc.scalar.copy(
-                out=gy[u0][:, SIDE * u1 : SIDE * u1 + SIDE, K_TENSOR * PACK : K_POOL_END * PACK].rearrange(
-                    "n v (k r) -> n v k r", r=PACK
-                ),
-                in_=plain_of[u0, u1][:].rearrange("n v1 v0 (r k) -> n (v1 v0) k r", r=PACK),
-            )
+            for v1 in range(2):
+                nc.scalar.copy(
+                    out=gy_rows(u0, SIDE * u1 + 2 * v1, 2)[:, :, K_TENSOR * PACK : K_POOL_END * PACK].rearrange(
+                        "n v (k r) -> n v k r", r=PACK
+                    ),
+                    in_=plain_of[u0, u1][:, v1].rearrange("n v0 (r k) -> n v0 k r", r=PACK),
+                )
 
         pixels_of = {}
         waiting = overlay.tile([PARTS, HALF, K_TENSOR * PACK], BF16, name="waiting", offset=208896, align_bytes=64)
-        targets = (gy[0], waiting)
 
-        def move_waiting():
-            nc.vector.tensor_copy(out=gy[1][:, :, 0 : K_TENSOR * PACK], in_=waiting[:])
+        def move_waiting(s):
+            nc.vector.tensor_copy(out=gy_rows(1, s, 2)[:, :, 0 : K_TENSOR * PACK], in_=waiting[:, s : s + 2, :])
 
         def pixels_to_partitions(o2):
             def chore():
@@ -271,7 +297,7 @@ def tile_iwht3layer_pa_kernel(tc, trans, weight, bias, grad_out, out):
                             in_=picked[:, r, 2 * o2 + i, :, :].rearrange("n a e -> n (a e)"),
                             identity=ident[:],
                         )
-                pixels = overlay.tile([PARTS, 2, PACK, PARTS], BF16, name="pixels", bufs=2, offset=234624)
+                pixels = overlay.tile([PARTS, 2, PACK, PARTS], BF16, name="pixels", bufs=2, offset=204800)
                 nc.scalar.copy(out=pixels[:], in_=pix_ps[:])
                 pixels_of[o2] = pixels
 
@@ -288,50 +314,16 @@ def tile_iwht3layer_pa_kernel(tc, trans, weight, bias, grad_out, out):
                         start=True,
                         stop=True,
                     )
-                for u0 in range(2):
+                columns = slice(o * OCTET * PACK, (o + 1) * OCTET * PACK)
+                by_s = coef_ps[:].rearrange("n r (s e) -> n s e r", e=OCTET)
+                for s in range(0, HALF, 2):
                     nc.scalar.copy(
-                        out=targets[u0][:, :, o * OCTET * PACK : (o + 1) * OCTET * PACK].rearrange(
-                            "n s (e r) -> n s e r", r=PACK
-                        ),
-                        in_=coef_ps[:, :, u0 * HALF * OCTET : (u0 + 1) * HALF * OCTET].rearrange(
-                            "n r (s e) -> n s e r", e=OCTET
-                        ),
+                        out=gy_rows(0, s, 2)[:, :, columns].rearrange("n s (e r) -> n s e r", r=PACK),
+                        in_=by_s[:, s : s + 2],
                     )
-
-            return chore
-
-        hop_jobs = []
-        for r1 in range(2):
-            for part in range(2):
-                hop_jobs.append(((r1 * 2) * 8 * ROW_H + part * CHUNK, (r1 * 2 + 1) * 8 * ROW_H + part * CHUNK))
-        for r1 in range(2):
-            for u1 in range(2):
-                start = (r1 * 2 + u1) * 8 * ROW_H
-                hop_jobs.append((start, start + CHUNK))
-        turned_of = {}
-
-        def hop_step(s):
-            def chore():
-                if 0 <= s - 2 < len(hop_jobs):
-                    a0, b0 = hop_jobs[s - 2]
-                    back = psum_a.tile([PARTS, BLOCKS, BLOCK], F32, name="bank_a")
-                    for j in range(BLOCKS):
-                        nc.tensor.transpose(out=back[:, j, :], in_=turned_of[s - 2][:, j, :], identity=ident_f[:])
-                    first = back[:].rearrange("n j w -> n (j w)")
-                    for target, op in ((a0, ADD), (b0, SUBTRACT)):
-                        nc.vector.tensor_tensor(
-                            out=hop[:, target : target + CHUNK], in0=first, in1=hop[:, b0 : b0 + CHUNK], op=op
-                        )
-                if s < len(hop_jobs):
-                    a0 = hop_jobs[s][0]
-                    forth = psum_b.tile([PARTS, BLOCKS, BLOCK], F32, name="bank_b")
-                    for j in range(BLOCKS):
-                        nc.tensor.transpose(
-                            out=forth[:, j, :], in_=hop[:, a0 + j * BLOCK : a0 + (j + 1) * BLOCK], identity=ident_f[:]
-                        )
-                    st = turned.tile([PARTS, BLOCKS, BLOCK], F32, name="st")
-                    nc.scalar.copy(out=st[:], in_=forth[:])
-                    turned_of[s] = st
+                nc.scalar.copy(
+                    out=waiting[:, :, columns].rearrange("n s (e r) -> n s e r", r=PACK), in_=by_s[:, HALF:T]
+                )
 
             return chore
 
@@ -350,8 +342,8 @@ def tile_iwht3layer_pa_kernel(tc, trans, weight, bias, grad_out, out):
                         stop=j == members[-1],
                     )
 
-        def new_bank():
-            return psum_a.tile([PARTS, PACK, PARTS], F32, name="bank_a")
+        def new_bank(pool=psum_a, name="bank_a"):
+            return pool.tile([PARTS, PACK, PARTS], F32, name=name)
 
         def new_whole(u0):
             return overlay.tile(
@@ -363,7 +355,7 @@ def tile_iwht3layer_pa_kernel(tc, trans, weight, bias, grad_out, out):
 
         def target_of(u0, s, e):
             column = (K_SUM + e * PARTS) * PACK
-            return gy[u0][:, s, column : column + PARTS * PACK].rearrange("n (w r) -> n w r", r=PACK)
+            return gy_rows(u0, s, 1)[:, 0, column : column + PARTS * PACK].rearrange("n (w r) -> n w r", r=PACK)
 
         def double(target, bank, sign, other, op):
             nc.vector.scalar_tensor_tensor(
@@ -373,10 +365,7 @@ def tile_iwht3layer_pa_kernel(tc, trans, weight, bias, grad_out, out):
         def sum_of_all(u0, e):
             def piece():
                 bank = new_bank()
-                add_up(u0, e, bank, 0, 2, range(HALF))
-                for i in range(IDLE):
-                    idle_pass()
-                add_up(u0, e, bank, 2, PACK, range(HALF))
+                add_up(u0, e, bank, 0, PACK, range(HALF))
                 whole = new_whole(u0)
                 nc.scalar.copy(out=whole[:], in_=source_of(bank))
                 nc.scalar.copy(out=target_of(u0, 0, e), in_=source_of(bank))
@@ -400,38 +389,96 @@ def tile_iwht3layer_pa_kernel(tc, trans, weight, bias, grad_out, out):
                 bank = new_bank()
                 add_up(u0, e, bank, 0, PACK, positive(v))
                 parts = []
-                for name, offset, other in (("part0", 234624, all_of[u0, e]), ("part1", 236672, tops_of[u0, e])):
+                for name, offset, other in (("part0", 231424, all_of[u0, e]), ("part1", 233472, tops_of[u0, e])):
                     part = overlay.tile([PARTS, PARTS, PACK], F32, name=name, offset=offset)
                     double(part[:], bank, 1.0, other[:], SUBTRACT)
                     parts.append(part)
-                bank = new_bank()
+                bank = new_bank(psum_b, "bank_b")
                 add_up(u0, e, bank, 0, PACK, [SIDE + q for q in positive(v)])
                 double(target_of(u0, v, e), bank, 1.0, parts[0][:], ADD)
                 double(target_of(u0, SIDE + v, e), bank, -1.0, parts[1][:], ADD)
 
             return [piece]
 
+        def each_u1(u0, v, e):
+            def one(u1):
+                def piece():
+                    bank = new_bank()
+                    plus = positive(v)
+                    bottom = [q for q in range(SIDE) if (q in plus) == (u1 == 0)]
+                    add_up(u0, e, bank, 0, PACK, plus + [SIDE + q for q in bottom])
+                    double(target_of(u0, SIDE * u1 + v, e), bank, 1.0, all_of[u0, e][:], SUBTRACT)
+
+                return piece
+
+            return [one(0), one(1)]
+
+        joint_all_of = {}
+
+        def joint_plus(s):
+            u1, v = s // SIDE, s % SIDE
+            plus = positive(v)
+            bottom = [q for q in range(SIDE) if (q in plus) == (u1 == 0)]
+            return plus + [SIDE + q for q in bottom] if s else list(range(HALF))
+
+        def joint_four(i, u0, u1):
+            def piece():
+                bank = psum_a.tile([PARTS, SIDE, PACK, J_WIDTH], F32, name="bank_a")
+                for v in range(SIDE):
+                    members = joint_plus(SIDE * u1 + v)
+                    for j in members:
+                        nc.tensor.matmul(
+                            out=bank[:, v].rearrange("n r k -> n (r k)"),
+                            lhsT=joint[:, i, u0, j, :],
+                            rhs=ident_f[:],
+                            is_transpose=True,
+                            start=j == members[0],
+                            stop=j == members[-1],
+                        )
+                if u1 == 0:
+                    joint_all_of[i, u0] = overlay.tile(
+                        [PARTS, J_WIDTH, PACK], F32, name="joint_all%d%d" % (i, u0), offset=JOINT_ALL[u0] + i * 512
+                    )
+                for v in range(SIDE):
+                    source = bank[:, v].rearrange("n r k -> n k r")
+                    column = (K_POOL_END + i * J_WIDTH) * PACK
+                    target = gy_rows(u0, SIDE * u1 + v, 1)[:, 0, column : column + J_WIDTH * PACK].rearrange(
+                        "n (k r) -> n k r", r=PACK
+                    )
+                    if (u1, v) == (0, 0):
+                        nc.scalar.copy(out=joint_all_of[i, u0][:], in_=source)
+                        nc.scalar.copy(out=target, in_=source)
+                    else:
+                        nc.vector.scalar_tensor_tensor(
+                            out=target, in0=source, scalar=2.0, in1=joint_all_of[i, u0][:], op0=MULT, op1=SUBTRACT
+                        )
+
+            return piece
+
         x_raw_of = {}
         x_of = {}
         x_codes_of = {}
 
-        def load_x(u, part):
+        def load_x(u):
             def chore():
-                x_raw = overlay.tile([PARTS, 2, PACK, C], BF16, name="x_raw", offset=200704)
-                nc.sync.dma_start(
-                    out=x_raw[:].rearrange("n v r c -> n v (r c)"), in_=x_dram[u][:, 2 * part : 2 * part + 2]
+                x_raw = overlay.tile(
+                    [PARTS, SIDE, PACK, C], BF16, name="x_raw%d" % u, offset=(40960, 147456, 57344, 147456)[u]
                 )
-                x_raw_of[u, part] = x_raw
+                nc.sync.dma_start(out=x_raw[:].rearrange("n v r c -> n v (r c)"), in_=x_dram[u])
+                x_raw_of[u] = x_raw
 
             return chore
 
-        def regroup_x(u, part):
+        def regroup_x(u, v, engine):
             def chore():
-                if part == 0:
+                if v == 0:
                     x_of[u] = overlay.tile([PARTS, SIDE, C, PACK], BF16, name="x", offset=192512, align_bytes=64)
-                nc.scalar.copy(
-                    out=x_of[u][:, 2 * part : 2 * part + 2], in_=x_raw_of[u, part][:].rearrange("n v r c -> n v c r")
-                )
+                target = x_of[u][:, v].rearrange("n (c i) r -> n c r i", i=4)
+                source = x_raw_of[u][:, v].rearrange("n r (c i) -> n c r i", i=4)
+                if engine == "V":
+                    nc.vector.tensor_copy(out=target, in_=source)
+                else:
+                    nc.scalar.copy(out=target, in_=source)
 
             return chore
 
@@ -459,7 +506,7 @@ def tile_iwht3layer_pa_kernel(tc, trans, weight, bias, grad_out, out):
         acc_pools = ((psum_c, "bank_c"), (psum_a, "bank_a"), (psum_b, "bank_b"))
         result_of = {}
 
-        pairs = [(u0, s) for u0 in range(2) for s in range(0, HALF, 2)]
+        pairs = [(0, 0), (0, 2), (0, 4), (0, 6), (1, 0), (1, 4), (1, 2), (1, 6)]
 
         def place(m):
             return pairs[m]
@@ -468,32 +515,16 @@ def tile_iwht3layer_pa_kernel(tc, trans, weight, bias, grad_out, out):
             u0, s = place(m)
             return 2 * (s // SIDE) + u0
 
-        def hop_sums(m):
-            u0, s = place(m)
-            u1, v1 = s // SIDE, s % SIDE // 2
-            by_unit = hop[:].rearrange("n (r1 s x) -> n r1 s x", r1=2, s=T)
-            a_unit = ((u1 * 2 + v1) * 2) * 2 + u0
-            b_unit = ((u1 * 2 + v1) * 2 + 1) * 2 + u0
-            for v0 in range(2):
-                nc.vector.tensor_tensor(
-                    out=gy[u0][:, s + v0, K_POOL_END * PACK : K_SUM * PACK].rearrange(
-                        "n (k r1 r0) -> n k r1 r0", r1=2, r0=2
-                    ),
-                    in0=by_unit[:, :, a_unit, :].rearrange("n r1 (r0 k) -> n k r1 r0", r0=2),
-                    in1=by_unit[:, :, b_unit, :].rearrange("n r1 (r0 k) -> n k r1 r0", r0=2),
-                    op=SIGN_OP[v0],
-                )
-
         def quantise(m, pieces):
             u0, s = place(m)
-            gy_codes = overlay.tile([PARTS, 2 * K], U32, name="gy_codes", bufs=2, offset=204800, align_bytes=64)
-            gy_scales = overlay.tile([PARTS, 2 * K], U8, name="gy_scales", bufs=2, offset=212992, align_bytes=64)
+            gy_codes = overlay.tile([PARTS, 2 * K], U32, name="gy_codes", bufs=2, offset=75776, align_bytes=64)
+            gy_scales = overlay.tile([PARTS, 2 * K], U8, name="gy_scales", bufs=2, offset=83968, align_bytes=64)
             width = 2 * K // pieces
             for i in range(pieces):
                 nc.vector.quantize_mx(
                     out=gy_codes[:, i * width : (i + 1) * width].bitcast(E5M2_X4),
                     scales=gy_scales[:, i * width : (i + 1) * width],
-                    in_=gy[u0][:, s : s + 2, :].rearrange("n v x -> n (v x)")[
+                    in_=gy[u0, s][:].rearrange("n v x -> n (v x)")[
                         :, i * width * PACK : (i + 1) * width * PACK
                     ],
                 )
@@ -520,7 +551,7 @@ def tile_iwht3layer_pa_kernel(tc, trans, weight, bias, grad_out, out):
         def store(m, v0, h, on_vector):
             u0, s = place(m)
             if h == 0:
-                result_of[m, v0] = overlay.tile([PARTS, C_HALVES, K], F32, name="result", bufs=4, offset=98304)
+                result_of[m, v0] = overlay.tile([PARTS, C_HALVES, K], F32, name="result", bufs=3, offset=86016)
             result = result_of[m, v0]
             bank = banks_of[m, v0, h]
             for target, source in (
@@ -537,72 +568,101 @@ def tile_iwht3layer_pa_kernel(tc, trans, weight, bias, grad_out, out):
             if h == C_HALVES - 1:
                 nc.sync.dma_start(out=out_dram[SIDE * u_of(m) + (s + v0) % SIDE], in_=result[:])
 
-        heads = [
-            [piece for e in range(2) for piece in sum_of_all(u0, e)]
-            + [piece for e in range(2) for piece in top_less_bottom(u0, e)]
-            for u0 in range(2)
+        def head(u0, e):
+            return sum_of_all(u0, e) + top_less_bottom(u0, e)
+
+        def body(u0, v, e):
+            return each_u1(u0, v, e) if v in () else both_u1(u0, v, e)
+
+        (all00, top00), (all01, top01), (all10, top10), (all11, top11) = [
+            head(u0, e) for u0 in range(2) for e in range(2)
         ]
-        bodies = [[piece for v in range(1, SIDE) for e in range(2) for piece in both_u1(u0, v, e)] for u0 in range(2)]
-        pieces = heads[0] + bodies[0][:1]
-        for head, body in zip(heads[1], (bodies[0][1:3], bodies[0][3:4], bodies[0][4:5], bodies[0][5:])):
-            pieces += [head] + body
-        pieces += bodies[1]
+        pieces = [all00, top00, *body(0, 1, 0), all01, *body(0, 2, 0), top01, *body(0, 1, 1), all10]
+        pieces += [*body(0, 3, 0), top10, *body(0, 2, 1), *body(0, 3, 1), all11, *body(1, 1, 0), top11]
+        pieces += [*body(1, 1, 1), *body(1, 2, 0), *body(1, 2, 1), *body(1, 3, 0), *body(1, 3, 1)]
         chores = {}
 
         def add_chore(slot, chore):
             chores.setdefault(slot, []).append(chore)
 
-        for o in range(4, OCTETS):
-            if o % 2 == 0 and o // 2 + 1 < OCTETS // 2:
-                add_chore(o // 2 - 2, pixels_to_partitions(o // 2 + 1))
-            add_chore(o // 2 - 2, transform(o))
-        for s in range(len(hop_jobs) + 2):
-            add_chore(s if s < 3 else s + 1, hop_step(s))
-        add_chore(4, lambda: gpsimd_rest(0, 0))
-        add_chore(4, lambda: gpsimd_rest(0, 1))
-        add_chore(4, move_waiting)
-        for (u0, u1), slot in (((0, 0), 9), ((0, 1), 12)):
-            add_chore(slot, lambda u0=u0, u1=u1: interleave(u0, u1))
-            add_chore(slot, lambda u1=u1: gpsimd_rest(1, u1))
-        add_chore(17, lambda: interleave(1, 0))
-        add_chore(19, lambda: interleave(1, 1))
-        for u, slots in ((0, (4, 5, 6, 7)), (2, (6, 7, 8, 10)), (1, (8, 10, 11, 15)), (3, (11, 15, 16, 18))):
-            add_chore(slots[3], quantise_x(u))
-            add_chore(slots[1], regroup_x(u, 0))
-            add_chore(slots[1], load_x(u, 1))
-            add_chore(slots[2], regroup_x(u, 1))
-            add_chore(slots[0], load_x(u, 0))
+        def products(m, v0):
+            def chore():
+                for h in range(C_HALVES):
+                    multiply(m, v0, h)
+                for h in range(C_HALVES):
+                    store(m, v0, h, False and h == 1 and v0 == 1)
 
-        for i in range(4):
-            idle_pass()
+            return chore
+
+        def interleave_and_go_on(u0, u1):
+            def chore():
+                interleave(u0, u1)
+                if u0 == 0:
+                    gpsimd_rest(1, u1)
+
+            return chore
+
+        for o in range(OCTETS):
+            slot = o // 2
+            add_chore(slot, transform(o))
+            if o % 2 == 1 and o // 2 + 2 < OCTETS // 2:
+                add_chore(slot, pixels_to_partitions(o // 2 + 2))
+        add_chore(0, load_x(0))
+        add_chore(0, load_x(2))
+        for i in range(J_TILES):
+            for u0 in range(2):
+                for p1 in range(2):
+                    add_chore(1 + u0, lambda i=i, u0=u0, p1=p1: turn_joint(i, u0, p1))
+        add_chore(2, lambda: gpsimd_rest(0, 0))
+        add_chore(2, lambda: gpsimd_rest(0, 1))
+        for v in range(SIDE):
+            add_chore((2, 3, 4, 5)[v], regroup_x(0, v, "S"))
+        add_chore(6, quantise_x(0))
+        for v in range(SIDE):
+            add_chore((7, 8, 9, 10)[v], regroup_x(2, v, "S"))
+        add_chore(11, quantise_x(2))
+        for i in range(J_TILES):
+            for u0 in range(2):
+                for u1 in range(2):
+                    add_chore((4, 11)[u0] + J_TILES * u1 + i, joint_four(i, u0, u1))
+        add_chore(6, interleave_and_go_on(0, 0))
+        add_chore(9, interleave_and_go_on(0, 1))
+        for s in range(0, HALF, 2):
+            add_chore(11, lambda s=s: move_waiting(s))
+        add_chore(11, load_x(1))
+        for v in range(SIDE):
+            add_chore((12, 12, 13, 13)[v], regroup_x(1, v, "S"))
+        add_chore(14, quantise_x(1))
+        add_chore(14, load_x(3))
+        add_chore(14, interleave_and_go_on(1, 0))
+        for v in range(SIDE):
+            add_chore((16, 16, 17, 17)[v], regroup_x(3, v, "V"))
+        add_chore(17, quantise_x(3))
+        add_chore(17, interleave_and_go_on(1, 1))
+        for m, slot in ((0, 12), (1, 13), (2, 14), (3, 15), (4, 17), (5, 18)):
+            add_chore(slot, lambda m=m: quantise(m, 1))
+            for v0 in range(2):
+                add_chore(min(slot + 1 + v0, 19), products(m, v0))
+
         pixels_to_partitions(0)()
         pixels_to_partitions(1)()
-        for o in range(4):
-            if o == 2:
-                pixels_to_partitions(2)()
-            transform(o)()
         for slot in range(len(pieces)):
             pieces[slot]()
-            for i in range(IDLE):
-                idle_pass()
             for chore in chores.get(slot, []):
                 chore()
 
-        hop_sums(0)
         held = []
-        for m in range(len(pairs)):
+        for m in range(6, len(pairs)):
             last = m == len(pairs) - 1
             quantise(m, 2 if last else 1)
             for v0 in range(2):
                 for h in range(C_HALVES):
                     multiply(m, v0, h)
-            if not last:
-                hop_sums(m + 1)
             while held:
                 store(*held.pop(0))
             for v0 in range(2):
                 for h in range(C_HALVES):
-                    if v0 == 1 and h == 1 and (last or m % 2 == 1):
+                    if v0 == 1 and h == 1:
                         held.append((m, v0, h, True))
                     else:
                         store(m, v0, h, False)

@@ -38,7 +38,7 @@ BLOCKS = 4
 CHUNK = BLOCK * BLOCKS
 HALF = T // 2
 
-JOINT_ALL = (235520, 236544)
+JOINT_ALL = 235520
 
 FLOPS = 2 * T * N * C * K
 BYTES = 2 * T * N * C + 2 * T * N * K + 4 * T * C * K
@@ -95,7 +95,7 @@ def tile_iwht3layer_pa_kernel(tc, trans, weight, bias, grad_out, out):
         joint_raw = overlay.tile(
             [PARTS, 2, HALF, J_TILES, PACK, J_WIDTH], F32, name="joint_raw", offset=215040
         )
-        joint = overlay.tile([PARTS, J_TILES, 2, HALF, PARTS], F32, name="joint", offset=131072)
+        joint = overlay.tile([PARTS, J_TILES, 2, 2, SIDE, PARTS], F32, name="joint", offset=131072)
         pool_a = overlay.tile([PARTS, T * UNIT_G], F32, name="pool_a", offset=147456)
         picked = overlay.tile([PARTS, PACK, OCTETS, T, OCTET], BF16, name="picked", offset=192512)
 
@@ -208,15 +208,23 @@ def tile_iwht3layer_pa_kernel(tc, trans, weight, bias, grad_out, out):
                 stop=True,
             )
 
-        def turn_joint(i, u0, p1):
-            bank = psum_b.tile([PARTS, SIDE, PARTS], F32, name="bank_b")
-            for q in range(SIDE):
-                nc.tensor.transpose(
-                    out=bank[:, q, :],
-                    in_=joint_raw[:, u0, SIDE * p1 + q, i].rearrange("n r k -> n (r k)"),
-                    identity=ident_f[:],
+        def turn_joint(i, u0):
+            banks = []
+            for p1, pool, name in ((1, psum_b, "bank_b"), (0, psum_a, "bank_a")):
+                bank = pool.tile([PARTS, SIDE, PARTS], F32, name=name)
+                for q in range(SIDE):
+                    nc.tensor.transpose(
+                        out=bank[:, q, :],
+                        in_=joint_raw[:, u0, SIDE * p1 + q, i].rearrange("n r k -> n (r k)"),
+                        identity=ident_f[:],
+                    )
+                banks.append(bank)
+            second = overlay.tile([PARTS, SIDE, PARTS], F32, name="joint_second", bufs=2, offset=237568)
+            nc.scalar.copy(out=second[:], in_=banks[0][:])
+            for u1 in range(2):
+                nc.vector.tensor_tensor(
+                    out=joint[:, i, u0, u1], in0=banks[1][:], in1=second[:], op=SIGN_OP[u1]
                 )
-            nc.scalar.copy(out=joint[:, i, u0, SIDE * p1 : SIDE * p1 + SIDE, :], in_=bank[:])
 
         for r1 in range(2):
             for p1 in range(2):
@@ -367,7 +375,10 @@ def tile_iwht3layer_pa_kernel(tc, trans, weight, bias, grad_out, out):
                 bank = new_bank()
                 add_up(u0, e, bank, 0, PACK, range(HALF))
                 whole = new_whole(u0)
-                nc.scalar.copy(out=whole[:], in_=source_of(bank))
+                if (u0, e) == (0, 0):
+                    nc.vector.tensor_copy(out=whole[:], in_=source_of(bank))
+                else:
+                    nc.scalar.copy(out=whole[:], in_=source_of(bank))
                 nc.scalar.copy(out=target_of(u0, 0, e), in_=source_of(bank))
                 all_of[u0, e] = whole
 
@@ -413,44 +424,33 @@ def tile_iwht3layer_pa_kernel(tc, trans, weight, bias, grad_out, out):
 
             return [one(0), one(1)]
 
-        joint_all_of = {}
-
-        def joint_plus(s):
-            u1, v = s // SIDE, s % SIDE
-            plus = positive(v)
-            bottom = [q for q in range(SIDE) if (q in plus) == (u1 == 0)]
-            return plus + [SIDE + q for q in bottom] if s else list(range(HALF))
-
         def joint_four(i, u0, u1):
             def piece():
                 bank = psum_a.tile([PARTS, SIDE, PACK, J_WIDTH], F32, name="bank_a")
                 for v in range(SIDE):
-                    members = joint_plus(SIDE * u1 + v)
+                    members = positive(v)
                     for j in members:
                         nc.tensor.matmul(
                             out=bank[:, v].rearrange("n r k -> n (r k)"),
-                            lhsT=joint[:, i, u0, j, :],
+                            lhsT=joint[:, i, u0, u1, j, :],
                             rhs=ident_f[:],
                             is_transpose=True,
                             start=j == members[0],
                             stop=j == members[-1],
                         )
-                if u1 == 0:
-                    joint_all_of[i, u0] = overlay.tile(
-                        [PARTS, J_WIDTH, PACK], F32, name="joint_all%d%d" % (i, u0), offset=JOINT_ALL[u0] + i * 512
-                    )
+                whole = overlay.tile([PARTS, J_WIDTH, PACK], F32, name="joint_all", bufs=4, offset=JOINT_ALL)
                 for v in range(SIDE):
                     source = bank[:, v].rearrange("n r k -> n k r")
                     column = (K_POOL_END + i * J_WIDTH) * PACK
                     target = gy_rows(u0, SIDE * u1 + v, 1)[:, 0, column : column + J_WIDTH * PACK].rearrange(
                         "n (k r) -> n k r", r=PACK
                     )
-                    if (u1, v) == (0, 0):
-                        nc.scalar.copy(out=joint_all_of[i, u0][:], in_=source)
+                    if v == 0:
+                        nc.vector.tensor_copy(out=whole[:], in_=source)
                         nc.scalar.copy(out=target, in_=source)
                     else:
                         nc.vector.scalar_tensor_tensor(
-                            out=target, in0=source, scalar=2.0, in1=joint_all_of[i, u0][:], op0=MULT, op1=SUBTRACT
+                            out=target, in0=source, scalar=2.0, in1=whole[:], op0=MULT, op1=SUBTRACT
                         )
 
             return piece
@@ -551,7 +551,10 @@ def tile_iwht3layer_pa_kernel(tc, trans, weight, bias, grad_out, out):
         def store(m, v0, h, on_vector):
             u0, s = place(m)
             if h == 0:
-                result_of[m, v0] = overlay.tile([PARTS, C_HALVES, K], F32, name="result", bufs=3, offset=86016)
+                name, bufs, offset = (
+                    ("result", 3, 86016) if m < 2 else ("result_on_joint", 4, 131072) if m < 6 else ("result_late", 8, 98304)
+                )
+                result_of[m, v0] = overlay.tile([PARTS, C_HALVES, K], F32, name=name, bufs=bufs, offset=offset)
             result = result_of[m, v0]
             bank = banks_of[m, v0, h]
             for target, source in (
@@ -603,7 +606,7 @@ def tile_iwht3layer_pa_kernel(tc, trans, weight, bias, grad_out, out):
             return chore
 
         for o in range(OCTETS):
-            slot = o // 2
+            slot = o // 2 * 3 // 2
             add_chore(slot, transform(o))
             if o % 2 == 1 and o // 2 + 2 < OCTETS // 2:
                 add_chore(slot, pixels_to_partitions(o // 2 + 2))
@@ -611,16 +614,15 @@ def tile_iwht3layer_pa_kernel(tc, trans, weight, bias, grad_out, out):
         add_chore(0, load_x(2))
         for i in range(J_TILES):
             for u0 in range(2):
-                for p1 in range(2):
-                    add_chore(1 + u0, lambda i=i, u0=u0, p1=p1: turn_joint(i, u0, p1))
+                add_chore(0, lambda i=i, u0=u0: turn_joint(i, u0))
         add_chore(2, lambda: gpsimd_rest(0, 0))
         add_chore(2, lambda: gpsimd_rest(0, 1))
         for v in range(SIDE):
-            add_chore((2, 3, 4, 5)[v], regroup_x(0, v, "S"))
-        add_chore(6, quantise_x(0))
+            add_chore((8, 8, 9, 9)[v], regroup_x(0, v, "S"))
+        add_chore(10, quantise_x(0))
         for v in range(SIDE):
-            add_chore((7, 8, 9, 10)[v], regroup_x(2, v, "S"))
-        add_chore(11, quantise_x(2))
+            add_chore((10, 10, 11, 11)[v], regroup_x(2, v, "S"))
+        add_chore(12, quantise_x(2))
         for i in range(J_TILES):
             for u0 in range(2):
                 for u1 in range(2):
@@ -646,6 +648,8 @@ def tile_iwht3layer_pa_kernel(tc, trans, weight, bias, grad_out, out):
 
         pixels_to_partitions(0)()
         pixels_to_partitions(1)()
+        for i in range(2):
+            idle_pass()
         for slot in range(len(pieces)):
             pieces[slot]()
             for chore in chores.get(slot, []):

@@ -96,7 +96,10 @@ def tile_iwht3layer_pa_kernel(tc, trans, weight, bias, grad_out, out):
             [PARTS, 2, HALF, J_TILES, PACK, J_WIDTH], F32, name="joint_raw", offset=215040
         )
         joint = overlay.tile([PARTS, J_TILES, 2, 2, SIDE, PARTS], F32, name="joint", offset=131072)
-        pool_a = overlay.tile([PARTS, T * UNIT_G], F32, name="pool_a", offset=147456)
+        pool_a = [
+            overlay.tile([PARTS, HALF * UNIT_G], F32, name="pool_a%d" % u0, offset=147456 + u0 * HALF * UNIT_G * 4)
+            for u0 in range(2)
+        ]
         picked = overlay.tile([PARTS, PACK, OCTETS, T, OCTET], BF16, name="picked", offset=192512)
 
         g = {}
@@ -132,9 +135,9 @@ def tile_iwht3layer_pa_kernel(tc, trans, weight, bias, grad_out, out):
                 a_rows = rows(2 * p1, r1, q_from, q_count)
                 b_rows = rows(2 * p1 + 1, r1, q_from, q_count)
                 for u0 in range(2):
-                    start = (u0 * 2 + p1) * SIDE * UNIT_G
+                    start = p1 * SIDE * UNIT_G
                     nc.gpsimd.tensor_tensor(
-                        out=pool_a[:, start : start + SIDE * UNIT_G]
+                        out=pool_a[u0][:, start : start + SIDE * UNIT_G]
                         .rearrange("n (q r1 x) -> n q r1 x", q=SIDE, r1=2)[:, q_from : q_from + q_count, r1, :]
                         .rearrange("n q (r0 k) -> n q r0 k", r0=2),
                         in0=a_rows[:, :, :, K_TENSOR:K_POOL_END].rearrange("n r0 q k -> n q r0 k"),
@@ -219,7 +222,7 @@ def tile_iwht3layer_pa_kernel(tc, trans, weight, bias, grad_out, out):
                         identity=ident_f[:],
                     )
                 banks.append(bank)
-            second = overlay.tile([PARTS, SIDE, PARTS], F32, name="joint_second", bufs=2, offset=237568)
+            second = overlay.tile([PARTS, SIDE, PARTS], F32, name="spare", bufs=2, offset=237568)
             nc.scalar.copy(out=second[:], in_=banks[0][:])
             for u1 in range(2):
                 nc.vector.tensor_tensor(
@@ -255,7 +258,7 @@ def tile_iwht3layer_pa_kernel(tc, trans, weight, bias, grad_out, out):
         plain_of = {}
 
         def gpsimd_rest(u0, u1):
-            half = pool_a[:, u0 * 8 * UNIT_G : (u0 + 1) * 8 * UNIT_G]
+            half = pool_a[u0][:]
             if u1 == 0:
                 for bit in range(2):
                     nc.gpsimd.tensor_tensor(
@@ -370,30 +373,21 @@ def tile_iwht3layer_pa_kernel(tc, trans, weight, bias, grad_out, out):
                 out=target, in0=source_of(bank), scalar=2.0 * sign, in1=other, op0=MULT, op1=op
             )
 
-        def sum_of_all(u0, e):
+        def head(u0, e):
             def piece():
-                bank = new_bank()
-                add_up(u0, e, bank, 0, PACK, range(HALF))
-                whole = new_whole(u0)
-                if (u0, e) == (0, 0):
-                    nc.vector.tensor_copy(out=whole[:], in_=source_of(bank))
-                else:
-                    nc.scalar.copy(out=whole[:], in_=source_of(bank))
-                nc.scalar.copy(out=target_of(u0, 0, e), in_=source_of(bank))
-                all_of[u0, e] = whole
+                bank_b = new_bank(psum_b, "bank_b")
+                add_up(u0, e, bank_b, 0, PACK, [SIDE + q for q in range(SIDE)])
+                bank_a = new_bank()
+                add_up(u0, e, bank_a, 0, PACK, range(SIDE))
+                bottom = overlay.tile([PARTS, PARTS, PACK], F32, name="spare", bufs=2, offset=237568)
+                nc.scalar.copy(out=bottom[:], in_=source_of(bank_b))
+                for u1, op, wholes in ((0, ADD, all_of), (1, SUBTRACT, tops_of)):
+                    whole = new_whole(u0)
+                    nc.vector.tensor_tensor(out=whole[:], in0=source_of(bank_a), in1=bottom[:], op=op)
+                    nc.scalar.copy(out=target_of(u0, SIDE * u1, e), in_=whole[:])
+                    wholes[u0, e] = whole
 
-            return [piece]
-
-        def top_less_bottom(u0, e):
-            def piece():
-                bank = new_bank()
-                add_up(u0, e, bank, 0, PACK, range(SIDE))
-                whole = new_whole(u0)
-                double(whole[:], bank, 1.0, all_of[u0, e][:], SUBTRACT)
-                nc.scalar.copy(out=target_of(u0, SIDE, e), in_=whole[:])
-                tops_of[u0, e] = whole
-
-            return [piece]
+            return piece
 
         def both_u1(u0, v, e):
             def piece():
@@ -462,7 +456,7 @@ def tile_iwht3layer_pa_kernel(tc, trans, weight, bias, grad_out, out):
         def load_x(u):
             def chore():
                 x_raw = overlay.tile(
-                    [PARTS, SIDE, PACK, C], BF16, name="x_raw%d" % u, offset=(40960, 147456, 57344, 147456)[u]
+                    [PARTS, SIDE, PACK, C], BF16, name="x_raw%d" % u, offset=(40960, 147456, 57344, 0)[u]
                 )
                 nc.sync.dma_start(out=x_raw[:].rearrange("n v r c -> n v (r c)"), in_=x_dram[u])
                 x_raw_of[u] = x_raw
@@ -571,18 +565,12 @@ def tile_iwht3layer_pa_kernel(tc, trans, weight, bias, grad_out, out):
             if h == C_HALVES - 1:
                 nc.sync.dma_start(out=out_dram[SIDE * u_of(m) + (s + v0) % SIDE], in_=result[:])
 
-        def head(u0, e):
-            return sum_of_all(u0, e) + top_less_bottom(u0, e)
-
         def body(u0, v, e):
             return each_u1(u0, v, e) if v in () else both_u1(u0, v, e)
 
-        (all00, top00), (all01, top01), (all10, top10), (all11, top11) = [
-            head(u0, e) for u0 in range(2) for e in range(2)
-        ]
-        pieces = [all00, top00, *body(0, 1, 0), all01, *body(0, 2, 0), top01, *body(0, 1, 1), all10]
-        pieces += [*body(0, 3, 0), top10, *body(0, 2, 1), *body(0, 3, 1), all11, *body(1, 1, 0), top11]
-        pieces += [*body(1, 1, 1), *body(1, 2, 0), *body(1, 2, 1), *body(1, 3, 0), *body(1, 3, 1)]
+        pieces = [head(0, 0), *body(0, 1, 0), head(0, 1), *body(0, 2, 0), *body(0, 1, 1), *body(0, 3, 0), head(1, 0)]
+        pieces += [*body(0, 2, 1), *body(0, 3, 1), *body(1, 1, 0), head(1, 1), *body(1, 1, 1), *body(1, 2, 0)]
+        pieces += [*body(1, 2, 1), *body(1, 3, 0), *body(1, 3, 1)]
         chores = {}
 
         def add_chore(slot, chore):
@@ -606,7 +594,7 @@ def tile_iwht3layer_pa_kernel(tc, trans, weight, bias, grad_out, out):
             return chore
 
         for o in range(OCTETS):
-            slot = o // 2 * 3 // 2
+            slot = o // 2
             add_chore(slot, transform(o))
             if o % 2 == 1 and o // 2 + 2 < OCTETS // 2:
                 add_chore(slot, pixels_to_partitions(o // 2 + 2))
@@ -614,37 +602,37 @@ def tile_iwht3layer_pa_kernel(tc, trans, weight, bias, grad_out, out):
         add_chore(0, load_x(2))
         for i in range(J_TILES):
             for u0 in range(2):
-                add_chore(0, lambda i=i, u0=u0: turn_joint(i, u0))
-        add_chore(2, lambda: gpsimd_rest(0, 0))
-        add_chore(2, lambda: gpsimd_rest(0, 1))
+                add_chore(1, lambda i=i, u0=u0: turn_joint(i, u0))
+        add_chore(1, lambda: gpsimd_rest(0, 0))
+        add_chore(1, lambda: gpsimd_rest(0, 1))
         for v in range(SIDE):
-            add_chore((8, 8, 9, 9)[v], regroup_x(0, v, "S"))
-        add_chore(10, quantise_x(0))
+            add_chore((4, 4, 5, 5)[v], regroup_x(0, v, "S"))
+        add_chore(6, quantise_x(0))
         for v in range(SIDE):
-            add_chore((10, 10, 11, 11)[v], regroup_x(2, v, "S"))
-        add_chore(12, quantise_x(2))
+            add_chore((6, 6, 7, 7)[v], regroup_x(2, v, "S"))
+        add_chore(8, quantise_x(2))
         for i in range(J_TILES):
             for u0 in range(2):
                 for u1 in range(2):
-                    add_chore((4, 11)[u0] + J_TILES * u1 + i, joint_four(i, u0, u1))
-        add_chore(6, interleave_and_go_on(0, 0))
-        add_chore(9, interleave_and_go_on(0, 1))
+                    add_chore((3, 9)[u0] + J_TILES * u1 + i, joint_four(i, u0, u1))
+        add_chore(4, interleave_and_go_on(0, 0))
+        add_chore(7, interleave_and_go_on(0, 1))
         for s in range(0, HALF, 2):
-            add_chore(11, lambda s=s: move_waiting(s))
-        add_chore(11, load_x(1))
+            add_chore(8, lambda s=s: move_waiting(s))
+        add_chore(8, load_x(1))
         for v in range(SIDE):
-            add_chore((12, 12, 13, 13)[v], regroup_x(1, v, "S"))
-        add_chore(14, quantise_x(1))
-        add_chore(14, load_x(3))
-        add_chore(14, interleave_and_go_on(1, 0))
+            add_chore((9, 9, 10, 10)[v], regroup_x(1, v, "S"))
+        add_chore(11, quantise_x(1))
+        add_chore(10, load_x(3))
+        add_chore(11, interleave_and_go_on(1, 0))
         for v in range(SIDE):
-            add_chore((16, 16, 17, 17)[v], regroup_x(3, v, "V"))
-        add_chore(17, quantise_x(3))
-        add_chore(17, interleave_and_go_on(1, 1))
-        for m, slot in ((0, 12), (1, 13), (2, 14), (3, 15), (4, 17), (5, 18)):
+            add_chore((11, 11, 12, 12)[v], regroup_x(3, v, "V"))
+        add_chore(13, quantise_x(3))
+        add_chore(13, interleave_and_go_on(1, 1))
+        for m, slot in ((0, 9), (1, 10), (2, 11), (3, 12), (4, 13), (5, 14)):
             add_chore(slot, lambda m=m: quantise(m, 1))
             for v0 in range(2):
-                add_chore(min(slot + 1 + v0, 19), products(m, v0))
+                add_chore(min(slot + 1 + v0, 15), products(m, v0))
 
         pixels_to_partitions(0)()
         pixels_to_partitions(1)()

import concourse.mybir as mybir
from concourse.masks import make_identity

F32 = mybir.dt.float32
BF16 = mybir.dt.bfloat16
U32 = mybir.dt.uint32
U8 = mybir.dt.uint8
E4M3_X4 = mybir.dt.float8_e4m3fn_x4
E5M2_X4 = mybir.dt.float8_e5m2_x4
COPY = mybir.ActivationFunctionType.Copy
ADD = mybir.AluOpType.add
SUBTRACT = mybir.AluOpType.subtract
MULT = mybir.AluOpType.mult
SIGN_OP = (ADD, SUBTRACT)

PARTS = 128
PACK = 4
SIDE = 4
T = SIDE * SIDE
LEVELS = 4
N = 512
C = 256
K = 512
C_HALVES = C // PARTS

OCTET = PARTS // T
OCTETS = 12
K_POOL = 96
K_JOINT = 64
K_TENSOR = OCTETS * OCTET
K_POOL_END = K_TENSOR + K_POOL
K_SUM = K_POOL_END + K_JOINT
UNIT_G = K_POOL * PACK
J_WIDTH = 32
J_TILES = K_JOINT // J_WIDTH
BLOCK = 128
BLOCKS = 4
CHUNK = BLOCK * BLOCKS
HALF = T // 2

JOINT_ALL = 235520

FLOPS = 2 * T * N * C * K
BYTES = 2 * T * N * C + 2 * T * N * K + 4 * T * C * K


def transform_matrix(nc, keep, pool, ident):
    current = ident
    for level in range(LEVELS):
        distance = PARTS // 2 ** (level + 1)
        following = pool.tile([PARTS, PARTS], BF16, name="matrix%d" % (level + 1), offset=219136 + 256 * level)
        halves = current[:].rearrange("n (a two b) -> n a two b", two=2, b=distance)
        signed = following[:].rearrange("n (a two b) -> n a two b", two=2, b=distance)
        for bit in range(2):
            nc.vector.tensor_tensor(
                out=signed[:, :, bit, :], in0=halves[:, :, 0, :], in1=halves[:, :, 1, :], op=SIGN_OP[bit]
            )
        current = following
    ordered = keep.tile([PARTS, PARTS], BF16, name="matrix_ordered")
    nc.vector.tensor_copy(
        out=ordered[:].rearrange("n (u0 u1 x) -> n u0 u1 x", u0=2, u1=2),
        in_=current[:].rearrange("n (u1 u0 x) -> n u0 u1 x", u0=2, u1=2),
    )
    return ordered


def positive(v):
    return [q for q in range(SIDE) if sum(((q & v) >> b) & 1 for b in range(LEVELS // 2)) % 2 == 0]


def tile_iwht3layer_pa_kernel(tc, trans, weight, bias, grad_out, out):
    nc = tc.nc

    g_dram = grad_out.rearrange("b (i p) (jh r1 r0 q) k -> jh p r1 (b i) r0 (q k)", p=SIDE, jh=2, r1=2, r0=2)
    x_dram = trans.rearrange("(u v) b i (jh r) c -> u (b i jh) v (r c)", v=SIDE, r=PACK)
    out_dram = out.rearrange("t (h m) k -> t m h k", h=C_HALVES)

    with tc.tile_pool(name="keep", bufs=1) as keep, tc.tile_pool(
        name="overlay", bufs=1
    ) as overlay, tc.psum_pool(name="psum_a", bufs=3) as psum_a, tc.psum_pool(
        name="psum_b", bufs=2
    ) as psum_b, tc.psum_pool(name="psum_c", bufs=3) as psum_c, tc.manual_schedule():
        ident = keep.tile([PARTS, PARTS], BF16, name="ident")
        make_identity(nc, ident[:])
        ident_f = keep.tile([PARTS, PARTS], F32, name="ident_f")
        make_identity(nc, ident_f[:])
        warm = keep.tile([PARTS, 1], BF16, name="warm")
        nc.scalar.copy(out=warm[:], in_=ident[:, 0:1])
        matrix = transform_matrix(nc, keep, overlay, ident)

        sums = [
            overlay.tile([PARTS, 2, PACK, HALF, PARTS], F32, name="sums%d" % u0, offset=65536 + u0 * 32768)
            for u0 in range(2)
        ]
        joint_raw = overlay.tile(
            [PARTS, 2, HALF, J_TILES, PACK, J_WIDTH], F32, name="joint_raw", offset=215040
        )
        joint = overlay.tile([PARTS, J_TILES, 2, 2, SIDE, PARTS], F32, name="joint", offset=131072)
        pool_a = [
            overlay.tile([PARTS, HALF * UNIT_G], F32, name="pool_a%d" % u0, offset=147456 + u0 * HALF * UNIT_G * 4)
            for u0 in range(2)
        ]
        picked = overlay.tile([PARTS, PACK, OCTETS, T, OCTET], BF16, name="picked", offset=192512)

        g = {}
        for r1 in range(2):
            for p1 in range(2):
                split = 2 if (r1, p1) == (0, 0) else 1
                for part in range(split):
                    for p in (2 * p1, 2 * p1 + 1):
                        q_count = SIDE // split
                        tile = overlay.tile(
                            [PARTS, 2, q_count, K],
                            BF16,
                            name="g%d%d%d" % (p, r1, part),
                            offset=(SIDE * r1 + p) * 8192 + part * 4096,
                        )
                        for jh in range(2):
                            nc.sync.dma_start(
                                out=tile[jh:PARTS:2].rearrange("n r0 q k -> n r0 (q k)"),
                                in_=g_dram[jh, p, r1][:, :, part * q_count * K : (part + 1) * q_count * K],
                            )
                        for q in range(part * q_count, (part + 1) * q_count):
                            g[p, r1, q] = (tile, part * q_count)

        def rows(p, r1, q_from, q_count):
            tile, first_q = g[p, r1, q_from]
            return tile[:, :, q_from - first_q : q_from - first_q + q_count, :]

        def spans(r1, p1):
            return ((0, 2), (2, 2)) if (r1, p1) == (0, 0) else ((0, SIDE),)

        def gpsimd_level1(r1, p1):
            for q_from, q_count in spans(r1, p1):
                a_rows = rows(2 * p1, r1, q_from, q_count)
                b_rows = rows(2 * p1 + 1, r1, q_from, q_count)
                for u0 in range(2):
                    start = p1 * SIDE * UNIT_G
                    nc.gpsimd.tensor_tensor(
                        out=pool_a[u0][:, start : start + SIDE * UNIT_G]
                        .rearrange("n (q r1 x) -> n q r1 x", q=SIDE, r1=2)[:, q_from : q_from + q_count, r1, :]
                        .rearrange("n q (r0 k) -> n q r0 k", r0=2),
                        in0=a_rows[:, :, :, K_TENSOR:K_POOL_END].rearrange("n r0 q k -> n q r0 k"),
                        in1=b_rows[:, :, :, K_TENSOR:K_POOL_END].rearrange("n r0 q k -> n q r0 k"),
                        op=SIGN_OP[u0],
                    )
                for u0 in range(2):
                    for i in range(J_TILES):
                        columns = slice(K_POOL_END + i * J_WIDTH, K_POOL_END + (i + 1) * J_WIDTH)
                        nc.gpsimd.tensor_tensor(
                            out=joint_raw[
                                :, u0, SIDE * p1 + q_from : SIDE * p1 + q_from + q_count, i, 2 * r1 : 2 * r1 + 2, :
                            ],
                            in0=a_rows[:, :, :, columns].rearrange("n r0 q k -> n q r0 k"),
                            in1=b_rows[:, :, :, columns].rearrange("n r0 q k -> n q r0 k"),
                            op=SIGN_OP[u0],
                        )

        def pick(r1, p1):
            for p in (2 * p1, 2 * p1 + 1):
                for r0 in range(2):
                    for q_from, q_count in spans(r1, p1):
                        nc.scalar.copy(
                            out=picked[:, 2 * r1 + r0, :, SIDE * p + q_from : SIDE * p + q_from + q_count, :].rearrange(
                                "n o q e -> n q o e"
                            ),
                            in_=rows(p, r1, q_from, q_count)[:, r0, :, 0:K_TENSOR].rearrange(
                                "n q (o e) -> n q o e", e=OCTET
                            ),
                        )

        def summed_level1(r1, p1, r0):
            banks = []
            for p, pool, name in ((2 * p1 + 1, psum_b, "bank_b"), (2 * p1, psum_a, "bank_a")):
                bank = pool.tile([PARTS, SIDE, PARTS], F32, name=name)
                for q in range(SIDE):
                    nc.tensor.transpose(
                        out=bank[:, q, :], in_=rows(p, r1, q, 1)[:, r0, 0, K_SUM:K].bitcast(F32), identity=ident_f[:]
                    )
                banks.append(bank)
            second = overlay.tile([PARTS, SIDE, PARTS], F32, name="second", bufs=2, offset=204800)
            nc.scalar.copy(out=second[:], in_=banks[0][:])
            for u0 in range(2):
                nc.vector.tensor_tensor(
                    out=sums[u0][:, :, 2 * r1 + r0, SIDE * p1 : SIDE * p1 + SIDE, :],
                    in0=banks[1][:].bitcast(BF16).rearrange("w q (n e) -> w e q n", e=2),
                    in1=second[:].bitcast(BF16).rearrange("w q (n e) -> w e q n", e=2),
                    op=SIGN_OP[u0],
                )

        ones = overlay.tile([PARTS, CHUNK * PACK], BF16, name="ones", offset=215040, align_bytes=64)
        nc.gpsimd.memset(ones[:], 1.0)
        idle_rhs = overlay.tile([PARTS, CHUNK], U32, name="idle_rhs", offset=231424, align_bytes=64)
        idle_rhs_scales = overlay.tile([PARTS, CHUNK], U8, name="idle_rhs_scales", offset=233472, align_bytes=64)
        idle_lhs = overlay.tile([PARTS, PARTS], U32, name="idle_lhs", offset=233984, align_bytes=64)
        idle_lhs_scales = overlay.tile([PARTS, PARTS], U8, name="idle_lhs_scales", offset=234496, align_bytes=64)
        nc.vector.quantize_mx(out=idle_rhs[:].bitcast(E5M2_X4), scales=idle_rhs_scales[:], in_=ones[:])
        nc.vector.quantize_mx(
            out=idle_lhs[:].bitcast(E4M3_X4), scales=idle_lhs_scales[:], in_=ones[:, 0 : PARTS * PACK]
        )
        idle_bank = psum_c.tile([PARTS, CHUNK], F32, name="bank_c")

        def idle_pass():
            nc.tensor.matmul_mx(
                out=idle_bank[:],
                lhsT=idle_lhs[:].bitcast(E4M3_X4),
                lhsT_scale=idle_lhs_scales[:],
                rhs=idle_rhs[:].bitcast(E5M2_X4),
                rhs_scale=idle_rhs_scales[:],
                start=True,
                stop=True,
            )

        def turn_joint(i, u0):
            banks = []
            for p1, pool, name in ((1, psum_b, "bank_b"), (0, psum_a, "bank_a")):
                bank = pool.tile([PARTS, SIDE, PARTS], F32, name=name)
                for q in range(SIDE):
                    nc.tensor.transpose(
                        out=bank[:, q, :],
                        in_=joint_raw[:, u0, SIDE * p1 + q, i].rearrange("n r k -> n (r k)"),
                        identity=ident_f[:],
                    )
                banks.append(bank)
            second = overlay.tile([PARTS, SIDE, PARTS], F32, name="spare", bufs=2, offset=237568)
            nc.scalar.copy(out=second[:], in_=banks[0][:])
            for u1 in range(2):
                nc.vector.tensor_tensor(
                    out=joint[:, i, u0, u1], in0=banks[1][:], in1=second[:], op=SIGN_OP[u1]
                )

        for r1 in range(2):
            for p1 in range(2):
                gpsimd_level1(r1, p1)
                for r0 in range(2):
                    summed_level1(r1, p1, r0)
                    if (r1, p1) != (1, 1):
                        for i in range(3):
                            idle_pass()
                pick(r1, p1)

        gy = {}
        for u0 in range(2):
            for s in range(0, HALF, 2):
                pair = overlay.tile(
                    [PARTS, 2, K * PACK],
                    BF16,
                    name="gy%d%d" % (u0, s),
                    offset=u0 * 32768 + s * 4096,
                    align_bytes=64,
                )
                gy[u0, s] = pair

        def gy_rows(u0, s, count):
            return gy[u0, s - s % 2][:, s % 2 : s % 2 + count, :]

        pool_b = overlay.tile([PARTS, 8 * UNIT_G], F32, name="pool_b", offset=172032)
        plain_of = {}

        def gpsimd_rest(u0, u1):
            half = pool_a[u0][:]
            if u1 == 0:
                for bit in range(2):
                    nc.gpsimd.tensor_tensor(
                        out=pool_b[:, bit * 4 * UNIT_G : (bit + 1) * 4 * UNIT_G],
                        in0=half[:, 0 : 4 * UNIT_G],
                        in1=half[:, 4 * UNIT_G : 8 * UNIT_G],
                        op=SIGN_OP[bit],
                    )
            q_pairs = pool_b[:, u1 * 4 * UNIT_G : (u1 + 1) * 4 * UNIT_G].rearrange("n (q1 x) -> n q1 x", q1=2)
            by_v1 = half[:, u1 * 4 * UNIT_G : (u1 + 1) * 4 * UNIT_G].rearrange("n (v1 q0 x) -> n v1 q0 x", v1=2, q0=2)
            for v1 in range(2):
                nc.gpsimd.tensor_tensor(
                    out=by_v1[:, v1].rearrange("n q0 x -> n (q0 x)"),
                    in0=q_pairs[:, 0, :],
                    in1=q_pairs[:, 1, :],
                    op=SIGN_OP[v1],
                )
            plain = overlay.tile([PARTS, 2, 2, UNIT_G], BF16, name="plain", bufs=2, offset=225280)
            for v0 in range(2):
                nc.gpsimd.tensor_tensor(
                    out=plain[:, :, v0, :], in0=by_v1[:, :, 0, :], in1=by_v1[:, :, 1, :], op=SIGN_OP[v0]
                )
            plain_of[u0, u1] = plain

        def interleave(u0, u1):
            for v1 in range(2):
                nc.scalar.copy(
                    out=gy_rows(u0, SIDE * u1 + 2 * v1, 2)[:, :, K_TENSOR * PACK : K_POOL_END * PACK].rearrange(
                        "n v (k r) -> n v k r", r=PACK
                    ),
                    in_=plain_of[u0, u1][:, v1].rearrange("n v0 (r k) -> n v0 k r", r=PACK),
                )

        pixels_of = {}
        waiting = overlay.tile([PARTS, HALF, K_TENSOR * PACK], BF16, name="waiting", offset=208896, align_bytes=64)

        def move_waiting(s):
            nc.vector.tensor_copy(out=gy_rows(1, s, 2)[:, :, 0 : K_TENSOR * PACK], in_=waiting[:, s : s + 2, :])

        def pixels_to_partitions(o2):
            def chore():
                pix_ps = psum_b.tile([PARTS, 2, PACK, PARTS], BF16, name="bank_b")
                for i in range(2):
                    for r in range(PACK):
                        nc.tensor.transpose(
                            out=pix_ps[:, i, r, :],
                            in_=picked[:, r, 2 * o2 + i, :, :].rearrange("n a e -> n (a e)"),
                            identity=ident[:],
                        )
                pixels = overlay.tile([PARTS, 2, PACK, PARTS], BF16, name="pixels", bufs=2, offset=204800)
                nc.scalar.copy(out=pixels[:], in_=pix_ps[:])
                pixels_of[o2] = pixels

            return chore

        def transform(o):
            def chore():
                coef_ps = psum_c.tile([PARTS, PACK, PARTS], F32, name="bank_c")
                for r in range(PACK):
                    nc.tensor.matmul(
                        out=coef_ps[:, r, :],
                        lhsT=pixels_of[o // 2][:, o % 2, r, :],
                        rhs=matrix[:],
                        start=True,
                        stop=True,
                    )
                columns = slice(o * OCTET * PACK, (o + 1) * OCTET * PACK)
                by_s = coef_ps[:].rearrange("n r (s e) -> n s e r", e=OCTET)
                for s in range(0, HALF, 2):
                    nc.scalar.copy(
                        out=gy_rows(0, s, 2)[:, :, columns].rearrange("n s (e r) -> n s e r", r=PACK),
                        in_=by_s[:, s : s + 2],
                    )
                nc.scalar.copy(
                    out=waiting[:, :, columns].rearrange("n s (e r) -> n s e r", r=PACK), in_=by_s[:, HALF:T]
                )

            return chore

        all_of = {}
        tops_of = {}

        def add_up(u0, e, bank, r_from, r_to, members):
            for r in range(r_from, r_to):
                for j in members:
                    nc.tensor.matmul(
                        out=bank[:, r, :],
                        lhsT=sums[u0][:, e, r, j, :],
                        rhs=ident_f[:],
                        is_transpose=True,
                        start=j == members[0],
                        stop=j == members[-1],
                    )

        def new_bank(pool=psum_a, name="bank_a"):
            return pool.tile([PARTS, PACK, PARTS], F32, name=name)

        def new_whole(u0):
            return overlay.tile(
                [PARTS, PARTS, PACK], F32, name="whole%d" % u0, bufs=4, offset=(184320, 204800)[u0]
            )

        def source_of(bank):
            return bank[:].rearrange("n r w -> n w r")

        def target_of(u0, s, e):
            column = (K_SUM + e * PARTS) * PACK
            return gy_rows(u0, s, 1)[:, 0, column : column + PARTS * PACK].rearrange("n (w r) -> n w r", r=PACK)

        def double(target, bank, sign, other, op):
            nc.vector.scalar_tensor_tensor(
                out=target, in0=source_of(bank), scalar=2.0 * sign, in1=other, op0=MULT, op1=op
            )

        def head(u0, e):
            def piece():
                bank_b = new_bank(psum_b, "bank_b")
                add_up(u0, e, bank_b, 0, PACK, [SIDE + q for q in range(SIDE)])
                bank_a = new_bank()
                add_up(u0, e, bank_a, 0, PACK, range(SIDE))
                bottom = overlay.tile([PARTS, PARTS, PACK], F32, name="spare", bufs=2, offset=237568)
                nc.scalar.copy(out=bottom[:], in_=source_of(bank_b))
                for u1, op, wholes in ((0, ADD, all_of), (1, SUBTRACT, tops_of)):
                    whole = new_whole(u0)
                    nc.vector.tensor_tensor(out=whole[:], in0=source_of(bank_a), in1=bottom[:], op=op)
                    nc.scalar.copy(out=target_of(u0, SIDE * u1, e), in_=whole[:])
                    wholes[u0, e] = whole

            return piece

        def both_u1(u0, v, e):
            def piece():
                bank = new_bank()
                add_up(u0, e, bank, 0, PACK, positive(v))
                parts = []
                for name, offset, other in (("part0", 231424, all_of[u0, e]), ("part1", 233472, tops_of[u0, e])):
                    part = overlay.tile([PARTS, PARTS, PACK], F32, name=name, offset=offset)
                    double(part[:], bank, 1.0, other[:], SUBTRACT)
                    parts.append(part)
                bank = new_bank(psum_b, "bank_b")
                add_up(u0, e, bank, 0, PACK, [SIDE + q for q in positive(v)])
                double(target_of(u0, v, e), bank, 1.0, parts[0][:], ADD)
                double(target_of(u0, SIDE + v, e), bank, -1.0, parts[1][:], ADD)

            return [piece]

        def each_u1(u0, v, e):
            def one(u1):
                def piece():
                    bank = new_bank()
                    plus = positive(v)
                    bottom = [q for q in range(SIDE) if (q in plus) == (u1 == 0)]
                    add_up(u0, e, bank, 0, PACK, plus + [SIDE + q for q in bottom])
                    double(target_of(u0, SIDE * u1 + v, e), bank, 1.0, all_of[u0, e][:], SUBTRACT)

                return piece

            return [one(0), one(1)]

        def joint_four(i, u0, u1):
            def piece():
                bank = psum_a.tile([PARTS, SIDE, PACK, J_WIDTH], F32, name="bank_a")
                for v in range(SIDE):
                    members = positive(v)
                    for j in members:
                        nc.tensor.matmul(
                            out=bank[:, v].rearrange("n r k -> n (r k)"),
                            lhsT=joint[:, i, u0, u1, j, :],
                            rhs=ident_f[:],
                            is_transpose=True,
                            start=j == members[0],
                            stop=j == members[-1],
                        )
                whole = overlay.tile([PARTS, J_WIDTH, PACK], F32, name="joint_all", bufs=4, offset=JOINT_ALL)
                for v in range(SIDE):
                    source = bank[:, v].rearrange("n r k -> n k r")
                    column = (K_POOL_END + i * J_WIDTH) * PACK
                    target = gy_rows(u0, SIDE * u1 + v, 1)[:, 0, column : column + J_WIDTH * PACK].rearrange(
                        "n (k r) -> n k r", r=PACK
                    )
                    if v == 0:
                        nc.vector.tensor_copy(out=whole[:], in_=source)
                        nc.scalar.copy(out=target, in_=source)
                    else:
                        nc.vector.scalar_tensor_tensor(
                            out=target, in0=source, scalar=2.0, in1=whole[:], op0=MULT, op1=SUBTRACT
                        )

            return piece

        x_raw_of = {}
        x_of = {}
        x_codes_of = {}

        def load_x(u):
            def chore():
                x_raw = overlay.tile(
                    [PARTS, SIDE, PACK, C], BF16, name="x_raw%d" % u, offset=(40960, 147456, 57344, 0)[u]
                )
                nc.sync.dma_start(out=x_raw[:].rearrange("n v r c -> n v (r c)"), in_=x_dram[u])
                x_raw_of[u] = x_raw

            return chore

        def regroup_x(u, v, engine):
            def chore():
                if v == 0:
                    x_of[u] = overlay.tile([PARTS, SIDE, C, PACK], BF16, name="x", offset=192512, align_bytes=64)
                target = x_of[u][:, v].rearrange("n (c i) r -> n c r i", i=4)
                source = x_raw_of[u][:, v].rearrange("n r (c i) -> n c r i", i=4)
                if engine == "V":
                    nc.vector.tensor_copy(out=target, in_=source)
                else:
                    nc.scalar.copy(out=target, in_=source)

            return chore

        def quantise_x(u):
            def chore():
                first = 215040 if u in (0, 2) else 65536
                half = u // 2
                x_codes = overlay.tile(
                    [PARTS, SIDE * C], U32, name="x_codes%d" % u, offset=first + half * 4096, align_bytes=64
                )
                x_scales = overlay.tile(
                    [PARTS, SIDE * C], U8, name="x_scales%d" % u, offset=first + 8192 + half * 1024, align_bytes=64
                )
                nc.vector.quantize_mx(
                    out=x_codes[:].bitcast(E4M3_X4),
                    scales=x_scales[:],
                    in_=x_of[u][:].rearrange("n v c r -> n (v c r)"),
                )
                x_codes_of[u] = (x_codes, x_scales)

            return chore

        codes_of = {}
        banks_of = {}
        acc_pools = ((psum_c, "bank_c"), (psum_a, "bank_a"), (psum_b, "bank_b"))
        result_of = {}

        pairs = [(0, 0), (0, 2), (0, 4), (0, 6), (1, 0), (1, 4), (1, 2), (1, 6)]

        def place(m):
            return pairs[m]

        def u_of(m):
            u0, s = place(m)
            return 2 * (s // SIDE) + u0

        def quantise(m, pieces):
            u0, s = place(m)
            gy_codes = overlay.tile([PARTS, 2 * K], U32, name="gy_codes", bufs=2, offset=75776, align_bytes=64)
            gy_scales = overlay.tile([PARTS, 2 * K], U8, name="gy_scales", bufs=2, offset=83968, align_bytes=64)
            width = 2 * K // pieces
            for i in range(pieces):
                nc.vector.quantize_mx(
                    out=gy_codes[:, i * width : (i + 1) * width].bitcast(E5M2_X4),
                    scales=gy_scales[:, i * width : (i + 1) * width],
                    in_=gy[u0, s][:].rearrange("n v x -> n (v x)")[
                        :, i * width * PACK : (i + 1) * width * PACK
                    ],
                )
            codes_of[m] = (gy_codes, gy_scales)

        def multiply(m, v0, h):
            u0, s = place(m)
            x_codes, x_scales = x_codes_of[u_of(m)]
            gy_codes, gy_scales = codes_of[m]
            column = (s + v0) % SIDE * C + h * PARTS
            pool, name = acc_pools[len(banks_of) % len(acc_pools)]
            acc = pool.tile([PARTS, K], F32, name=name)
            nc.tensor.matmul_mx(
                out=acc[:],
                lhsT=x_codes[:, column : column + PARTS].bitcast(E4M3_X4),
                lhsT_scale=x_scales[:, column : column + PARTS],
                rhs=gy_codes[:, v0 * K : (v0 + 1) * K].bitcast(E5M2_X4),
                rhs_scale=gy_scales[:, v0 * K : (v0 + 1) * K],
                start=True,
                stop=True,
            )
            banks_of[m, v0, h] = acc

        def store(m, v0, h, on_vector):
            u0, s = place(m)
            if h == 0:
                name, bufs, offset = (
                    ("result", 3, 86016) if m < 2 else ("result_on_joint", 4, 131072) if m < 6 else ("result_late", 8, 98304)
                )
                result_of[m, v0] = overlay.tile([PARTS, C_HALVES, K], F32, name=name, bufs=bufs, offset=offset)
            result = result_of[m, v0]
            bank = banks_of[m, v0, h]
            for target, source in (
                (result[:, h, 0:K_SUM], bank[:, 0:K_SUM]),
                (
                    result[:, h, K_SUM:K].rearrange("n (w e) -> n w e", e=2),
                    bank[:, K_SUM:K].rearrange("n (e w) -> n w e", e=2),
                ),
            ):
                if on_vector:
                    nc.vector.tensor_scalar(out=target, in0=source, scalar1=1.0 / T, scalar2=None, op0=MULT)
                else:
                    nc.scalar.activation(out=target, in_=source, func=COPY, scale=1.0 / T)
            if h == C_HALVES - 1:
                nc.sync.dma_start(out=out_dram[SIDE * u_of(m) + (s + v0) % SIDE], in_=result[:])

        def body(u0, v, e):
            return each_u1(u0, v, e) if v in () else both_u1(u0, v, e)

        pieces = [head(0, 0), *body(0, 1, 0), head(0, 1), *body(0, 2, 0), *body(0, 1, 1), *body(0, 3, 0), head(1, 0)]
        pieces += [*body(0, 2, 1), *body(0, 3, 1), *body(1, 1, 0), head(1, 1), *body(1, 1, 1), *body(1, 2, 0)]
        pieces += [*body(1, 2, 1), *body(1, 3, 0), *body(1, 3, 1)]
        chores = {}

        def add_chore(slot, chore):
            chores.setdefault(slot, []).append(chore)

        def products(m, v0):
            def chore():
                for h in range(C_HALVES):
                    multiply(m, v0, h)
                for h in range(C_HALVES):
                    store(m, v0, h, False and h == 1 and v0 == 1)

            return chore

        def interleave_and_go_on(u0, u1):
            def chore():
                interleave(u0, u1)
                if u0 == 0:
                    gpsimd_rest(1, u1)

            return chore

        for o in range(OCTETS):
            slot = o // 2
            add_chore(slot, transform(o))
            if o % 2 == 1 and o // 2 + 2 < OCTETS // 2:
                add_chore(slot, pixels_to_partitions(o // 2 + 2))
        add_chore(0, load_x(0))
        add_chore(0, load_x(2))
        for i in range(J_TILES):
            for u0 in range(2):
                add_chore(1, lambda i=i, u0=u0: turn_joint(i, u0))
        add_chore(1, lambda: gpsimd_rest(0, 0))
        add_chore(1, lambda: gpsimd_rest(0, 1))
        for v in range(SIDE):
            add_chore((4, 4, 5, 5)[v], regroup_x(0, v, "S"))
        add_chore(6, quantise_x(0))
        for v in range(SIDE):
            add_chore((6, 6, 7, 7)[v], regroup_x(2, v, "S"))
        add_chore(8, quantise_x(2))
        for i in range(J_TILES):
            for u0 in range(2):
                for u1 in range(2):
                    add_chore((3, 9)[u0] + J_TILES * u1 + i, joint_four(i, u0, u1))
        add_chore(4, interleave_and_go_on(0, 0))
        add_chore(7, interleave_and_go_on(0, 1))
        for s in range(0, HALF, 2):
            add_chore(8, lambda s=s: move_waiting(s))
        add_chore(8, load_x(1))
        for v in range(SIDE):
            add_chore((9, 9, 10, 10)[v], regroup_x(1, v, "S"))
        add_chore(11, quantise_x(1))
        add_chore(10, load_x(3))
        add_chore(11, interleave_and_go_on(1, 0))
        for v in range(SIDE):
            add_chore((11, 11, 12, 12)[v], regroup_x(3, v, "V"))
        add_chore(13, quantise_x(3))
        add_chore(13, interleave_and_go_on(1, 1))
        for m, slot in ((0, 9), (1, 10), (2, 11), (3, 12), (4, 13), (5, 14)):
            add_chore(slot, lambda m=m: quantise(m, 1))
            for v0 in range(2):
                add_chore(min(slot + 1 + v0, 15), products(m, v0))

        pixels_to_partitions(0)()
        pixels_to_partitions(1)()
        for i in range(2):
            idle_pass()
        for slot in range(len(pieces)):
            pieces[slot]()
            for chore in chores.get(slot, []):
                chore()

        held = []
        for m in range(6, len(pairs)):
            last = m == len(pairs) - 1
            quantise(m, 2 if last else 1)
            for v0 in range(2):
                for h in range(C_HALVES):
                    multiply(m, v0, h)
            while held:
                store(*held.pop(0))
            for v0 in range(2):
                for h in range(C_HALVES):
                    if v0 == 1 and h == 1:
                        held.append((m, v0, h, True))
                    else:
                        store(m, v0, h, False)
        while held:
            store(*held.pop(0))
